import numpy as np
import ml_dtypes


def mxq(x, axis, fmt="e4m3"):
    dtype, down = {"e4m3": (ml_dtypes.float8_e4m3fn, 7), "e5m2": (ml_dtypes.float8_e5m2, 14)}[fmt]
    v = np.moveaxis(np.asarray(x, np.float32).astype(ml_dtypes.bfloat16).astype(np.float64), axis, -1)
    blocks = v.reshape(v.shape[:-1] + (-1, 32))
    amax = np.abs(blocks).max(-1, keepdims=True)
    byte = np.maximum(np.where(amax > 0, np.frexp(amax)[1] - 1 + 127, 0) - down, 1)
    scale = np.exp2(byte - 127.0)
    codes = (blocks / scale).astype(np.float32).astype(dtype).astype(np.float64)
    return np.moveaxis((codes * scale).reshape(v.shape), -1, axis)


WIDE = False


def mx_kscale(k):
    if not WIDE:
        return np.ones(k)
    levels = np.array([10, -10, 5, -5, 0])
    a = np.random.permutation(np.resize(levels, k // 512 * 4)).reshape(k // 512, 4)
    idx = np.arange(k)
    return np.exp2(a[idx // 512, idx % 128 // 32])


BF16 = ml_dtypes.bfloat16


def bf(x):
    return np.asarray(x, np.float32).astype(BF16)


def f64(x):
    return np.asarray(x).astype(np.float64)


E2M1 = np.array([0.0, 0.5, 1.0, 1.5, 2.0, 3.0, 4.0, 6.0, -0.0, -0.5, -1.0, -1.5, -2.0, -3.0, -4.0, -6.0])


def pack_weight(w, fmt):
    k, n = w.shape
    w = f64(bf(w)).reshape(k // 32, 32, n)
    amax = np.abs(w).max(1)
    if fmt == "e4m3":
        byte = np.frexp(amax)[1] - 1 + 127 - 7
    else:
        mant, ex = np.frexp(amax / 6.0)
        byte = np.where(mant > 0.5, ex, ex - 1) + 127
    byte = np.clip(np.where(amax > 0, byte, 1), 1, 254)
    scaled = (w * np.exp2(127.0 - byte)[:, None, :]).reshape(k, n).astype(np.float32)
    by_word = np.ascontiguousarray(scaled.reshape(k // 512, 128, 4, n).transpose(0, 1, 3, 2))
    if fmt == "e4m3":
        words = by_word.astype(ml_dtypes.float8_e4m3fn).view(np.uint8)
    else:
        c = by_word.astype(ml_dtypes.float4_e2m1fn).view(np.uint8) & 0xF
        words = c[..., 0::2] | (c[..., 1::2] << 4)
    return np.ascontiguousarray(words), np.ascontiguousarray(byte.astype(np.uint8).reshape(k // 512, 16, n))


def unpack_weight(words, scales, fmt):
    g, p, n, _ = words.shape
    if fmt == "e4m3":
        vals = np.ascontiguousarray(words).view(ml_dtypes.float8_e4m3fn).astype(np.float64)
    else:
        nib = np.empty((g, p, n, 4), np.uint8)
        nib[..., 0::2] = words & 0xF
        nib[..., 1::2] = words >> 4
        vals = E2M1[nib]
    vals = vals * np.repeat(np.exp2(scales.astype(np.float64) - 127.0), 8, axis=1)[..., None]
    return vals.transpose(0, 1, 3, 2).reshape(g * 512, n)


B, C, H, W, R, G, K = 1, 2048, 16, 16, 2048, 128, 7
PAD = K // 2
KK = K * K
FMT = "e4m3"


def setup_inputs():
    t = mx_kscale(R)
    x = bf(np.random.standard_normal((B, C, H, W)))
    w_reduce = np.random.standard_normal((R, C)) * 1.0 / np.sqrt(C) * t[:, None]
    b_reduce = bf(np.random.standard_normal(R) * 0.5 * t)
    w_span = np.random.standard_normal((KK * G, R)) * 1.5 / np.sqrt(R) / t[None, :]
    b_span = bf(np.random.standard_normal(KK * G) * 0.5)
    w_reduce_words, w_reduce_scales = pack_weight(np.ascontiguousarray(w_reduce.T), FMT)
    w_span_words, w_span_scales = pack_weight(np.ascontiguousarray(w_span.T), FMT)
    return {"x": x,
            "w_reduce_words": w_reduce_words,
            "w_reduce_scales": w_reduce_scales,
            "b_reduce": b_reduce,
            "w_span_words": w_span_words,
            "w_span_scales": w_span_scales,
            "b_span": b_span}


def reference(x, w_reduce_words, w_reduce_scales, b_reduce, w_span_words, w_span_scales, b_span):
    x = f64(x)
    red = np.maximum((unpack_weight(w_reduce_words, w_reduce_scales, FMT).T @ mxq(x.reshape(B, C, H * W), 1, "e4m3")) + f64(b_reduce)[None, :, None], 0.0)
    kern = (unpack_weight(w_span_words, w_span_scales, FMT).T @ mxq(red, 1, "e4m3")) + f64(b_span)[None, :, None]
    kern = kern.reshape(B, G, KK, H, W)
    e = np.exp(kern - kern.max(axis=2, keepdims=True))
    kern = e / e.sum(axis=2, keepdims=True)
    xp = np.pad(x, ((0, 0), (0, 0), (PAD, PAD), (PAD, PAD)))
    xg = xp.reshape(B, G, C // G, H + 2 * PAD, W + 2 * PAD)
    out = np.zeros((B, G, C // G, H, W))
    for i in range(K):
        for j in range(K):
            out = out + kern[:, :, None, i * K + j] * xg[:, :, :, i:i + H, j:j + W]
    return out.reshape(B, C, H, W)

@@ -1,0 +1,229 @@
+from contextlib import ExitStack
+
+import concourse.mybir as mybir
+from concourse.masks import make_identity
+
+F32 = mybir.dt.float32
+BF16 = mybir.dt.bfloat16
+U8 = mybir.dt.uint8
+U32 = mybir.dt.uint32
+I32 = mybir.dt.int32
+FP8X4 = mybir.dt.float8_e4m3fn_x4
+ALU = mybir.AluOpType
+ACT = mybir.ActivationFunctionType
+AXIS = mybir.AxisListType
+
+P = 128
+PACK = 4
+K_PASS = P * PACK
+C = 2048
+R = 2048
+KG = C // K_PASS
+H = 16
+W = 16
+PIX = H * W
+PB = PIX // P
+G = 128
+CG = C // G
+KER = 7
+PAD = KER // 2
+TAPS = KER * KER
+O = G * TAPS
+N_TILE = 512
+
+FLOPS = 2 * C * R * PIX + 2 * R * O * PIX + 2 * TAPS * C * PIX
+
+
+def load_scale_planes(nc, planes, scales):
+    nc.vector.memset(planes[:].bitcast(I32), 0)
+    for q in range(4):
+        nc.sync.dma_start(
+            out=planes[32 * q : 32 * q + 16, :].bitcast(I32),
+            in_=scales[:, 4 * q : 4 * q + 4, :].bitcast(I32),
+        )
+
+
+def load_weight_tile(nc, ring, words, col0, ncols):
+    wt = ring.tile([P, KG, PACK * N_TILE], U8, name="wt", align_bytes=64)
+    nc.sync.dma_start(
+        out=wt[:, :, : PACK * ncols].bitcast(I32),
+        in_=words.rearrange("g p n t -> p g (n t)")[:, :, PACK * col0 : PACK * (col0 + ncols)].bitcast(I32),
+    )
+    return wt
+
+
+def mx_product(nc, acc, codes, planes, pb, wt, w_planes, col0, ncols):
+    for g in range(KG):
+        cols = slice(g * PIX + pb * P, g * PIX + (pb + 1) * P)
+        nc.tensor.matmul_mx(
+            out=acc,
+            lhsT=codes[:, cols].bitcast(FP8X4),
+            lhsT_scale=planes[:, cols],
+            rhs=wt[:, g, : PACK * ncols].bitcast(FP8X4),
+            rhs_scale=w_planes[4 * g : P, col0 : col0 + ncols],
+            start=(g == 0),
+            stop=(g == KG - 1),
+        )
+
+
+def tile_involution_w_kernel(
+    tc, x, w_reduce_words, w_reduce_scales, b_reduce, w_span_words, w_span_scales, b_span, out
+):
+    nc = tc.nc
+    with ExitStack() as whole:
+        keep = whole.enter_context(tc.tile_pool(name="keep", bufs=1))
+        ident_bf = keep.tile([P, P], BF16)
+        make_identity(nc, ident_bf[:])
+        ident_f32 = keep.tile([P, P], F32)
+        make_identity(nc, ident_f32[:])
+        e_pix = [keep.tile([P, TAPS, G], F32, name="e_pix%d" % pb) for pb in range(PB)]
+        e_sum = [keep.tile([P, G], F32, name="e_sum%d" % pb) for pb in range(PB)]
+        e_rcp = [keep.tile([P, G], F32, name="e_rcp%d" % pb) for pb in range(PB)]
+
+        with ExitStack() as branch:
+            front = branch.enter_context(tc.tile_pool(name="front", bufs=1))
+            ring = branch.enter_context(tc.tile_pool(name="ring", bufs=4))
+            work = branch.enter_context(tc.tile_pool(name="work", bufs=3))
+            psum_mx = branch.enter_context(tc.psum_pool(name="psum_mx", bufs=4))
+            psum_tr = branch.enter_context(tc.psum_pool(name="psum_tr", bufs=2))
+
+            x_raw = front.tile([P, KG, PACK * PIX], BF16)
+            nc.sync.dma_start(out=x_raw[:], in_=x[0].rearrange("(g p t) h w -> p g (t h w)", g=KG, p=P, t=PACK))
+            w1_planes = front.tile([P, R], U8, align_bytes=64)
+            load_scale_planes(nc, w1_planes, w_reduce_scales)
+            b1_bc = front.tile([P, R], BF16)
+            nc.scalar.dma_start(out=b1_bc[:], in_=b_reduce.partition_broadcast(P))
+            b2_bc = front.tile([P, O], BF16)
+            nc.scalar.dma_start(out=b2_bc[:], in_=b_span.partition_broadcast(P))
+
+            x_grouped = front.tile([P, KG, PIX, PACK], BF16, align_bytes=64)
+            nc.vector.tensor_copy(out=x_grouped[:], in_=x_raw[:].rearrange("p g (t x) -> p g x t", t=PACK))
+            x_codes = front.tile([P, KG * PIX], U32, align_bytes=64)
+            x_planes = front.tile([P, KG * PIX], U8, align_bytes=64)
+            nc.vector.quantize_mx(
+                out=x_codes[:].bitcast(FP8X4),
+                scales=x_planes[:],
+                in_=x_grouped[:].rearrange("p g x t -> p (g x t)"),
+            )
+
+            red_pix = [front.tile([P, KG, PACK, P], BF16, name="red_pix%d" % pb) for pb in range(PB)]
+            red_grouped = front.tile([P, KG, PIX, PACK], BF16, align_bytes=64)
+            red_codes = front.tile([P, KG * PIX], U32, align_bytes=64)
+            red_planes = front.tile([P, KG * PIX], U8, align_bytes=64)
+            for rt in range(R // N_TILE):
+                wt = load_weight_tile(nc, ring, w_reduce_words, rt * N_TILE, N_TILE)
+                for pb in range(PB):
+                    acc = psum_mx.tile([P, N_TILE], F32, name="acc")
+                    mx_product(nc, acc[:], x_codes, x_planes, pb, wt, w1_planes, rt * N_TILE, N_TILE)
+                    pre = work.tile([P, N_TILE], F32, name="pre")
+                    nc.vector.tensor_tensor(
+                        out=pre[:], in0=acc[:], in1=b1_bc[:, rt * N_TILE : (rt + 1) * N_TILE], op=ALU.add
+                    )
+                    nc.scalar.activation(
+                        out=red_pix[pb][:, rt, :, :],
+                        in_=pre[:].rearrange("x (p t) -> x t p", t=PACK),
+                        func=ACT.Relu,
+                    )
+            w2_planes = front.tile([P, O], U8, align_bytes=64)
+            load_scale_planes(nc, w2_planes, w_span_scales)
+            for g in range(KG):
+                for pb in range(PB):
+                    flipped = psum_tr.tile([P, PACK, P], BF16, name="flipped")
+                    for t in range(PACK):
+                        nc.tensor.transpose(flipped[:, t, :], red_pix[pb][:, g, t, :], ident_bf[:])
+                    nc.vector.tensor_copy(
+                        out=red_grouped[:, g, pb * P : (pb + 1) * P, :],
+                        in_=flipped[:].rearrange("p t x -> p x t"),
+                    )
+                nc.vector.quantize_mx(
+                    out=red_codes[:, g * PIX : (g + 1) * PIX].bitcast(FP8X4),
+                    scales=red_planes[:, g * PIX : (g + 1) * PIX],
+                    in_=red_grouped[:, g, :, :].rearrange("p x t -> p (x t)"),
+                )
+
+            z = [front.tile([P, O], F32, name="z%d" % pb) for pb in range(PB)]
+            z_max = [front.tile([P, G], F32, name="z_max%d" % pb) for pb in range(PB)]
+            g_lo = 0
+            for col0 in range(0, O, N_TILE):
+                ncols = min(N_TILE, O - col0)
+                wt = load_weight_tile(nc, ring, w_span_words, col0, ncols)
+                g_hi = (col0 + ncols) // TAPS
+                for pb in range(PB):
+                    acc = psum_mx.tile([P, N_TILE], F32, name="acc")
+                    mx_product(nc, acc[:, :ncols], red_codes, red_planes, pb, wt, w2_planes, col0, ncols)
+                    nc.vector.tensor_tensor(
+                        out=z[pb][:, col0 : col0 + ncols],
+                        in0=acc[:, :ncols],
+                        in1=b2_bc[:, col0 : col0 + ncols],
+                        op=ALU.add,
+                    )
+                    ready = z[pb][:, g_lo * TAPS : g_hi * TAPS]
+                    nc.vector.tensor_reduce(
+                        out=z_max[pb][:, g_lo:g_hi],
+                        in_=ready.rearrange("x (g t) -> x g t", t=TAPS),
+                        axis=AXIS.X,
+                        op=ALU.max,
+                    )
+                    nc.gpsimd.tensor_tensor(
+                        out=ready.rearrange("x (g t) -> x g t", t=TAPS),
+                        in0=ready.rearrange("x (g t) -> x g t", t=TAPS),
+                        in1=z_max[pb][:, g_lo:g_hi].unsqueeze(2).to_broadcast([P, g_hi - g_lo, TAPS]),
+                        op=ALU.subtract,
+                    )
+                    nc.scalar.activation(
+                        out=e_pix[pb][:, :, g_lo:g_hi],
+                        in_=ready.rearrange("x (g t) -> x t g", t=TAPS),
+                        func=ACT.Exp,
+                    )
+                    nc.vector.tensor_reduce(
+                        out=e_sum[pb][:, g_lo:g_hi],
+                        in_=e_pix[pb][:, :, g_lo:g_hi].rearrange("x t g -> x g t"),
+                        axis=AXIS.X,
+                        op=ALU.add,
+                    )
+                g_lo = g_hi
+            for pb in range(PB):
+                nc.vector.reciprocal(out=e_rcp[pb][:], in_=e_sum[pb][:])
+
+        with ExitStack() as taps:
+            hold = taps.enter_context(tc.tile_pool(name="hold", bufs=1))
+            prods = taps.enter_context(tc.tile_pool(name="prods", bufs=2))
+            psum_g = taps.enter_context(tc.psum_pool(name="psum_g", bufs=4))
+
+            x_g = hold.tile([P, CG, H, W], BF16)
+            nc.sync.dma_start(out=x_g[:], in_=x[0].rearrange("(g c) h w -> g c h w", c=CG))
+            x_pad = hold.tile([P, CG, H + 2 * PAD, W + 2 * PAD], BF16)
+            nc.vector.memset(x_pad[:], 0.0)
+            nc.vector.tensor_copy(out=x_pad[:, :, PAD : PAD + H, PAD : PAD + W], in_=x_g[:])
+
+            rcp_g = hold.tile([P, PIX], F32)
+            turned = psum_g.tile([P, PIX], F32, name="turned")
+            for pb in range(PB):
+                nc.tensor.transpose(turned[:, pb * P : (pb + 1) * P], e_rcp[pb][:], ident_f32[:])
+            nc.scalar.copy(out=rcp_g[:], in_=turned[:])
+            e_g = hold.tile([P, TAPS, PIX], F32)
+            for tap in range(TAPS):
+                turned = psum_g.tile([P, PIX], F32, name="turned")
+                for pb in range(PB):
+                    nc.tensor.transpose(turned[:, pb * P : (pb + 1) * P], e_pix[pb][:, tap, :], ident_f32[:])
+                nc.scalar.copy(out=e_g[:, tap, :], in_=turned[:])
+
+            total = hold.tile([P, CG, H, W], F32)
+            for tap in range(TAPS):
+                i, j = divmod(tap, KER)
+                window = x_pad[:, :, i : i + H, j : j + W]
+                weight = e_g[:, tap, :].rearrange("g (h w) -> g h w", h=H).unsqueeze(1).to_broadcast([P, CG, H, W])
+                if tap == 0:
+                    nc.vector.tensor_tensor(out=total[:], in0=window, in1=weight, op=ALU.mult)
+                else:
+                    prod = prods.tile([P, CG, H, W], F32, name="prod")
+                    nc.vector.tensor_tensor(out=prod[:], in0=window, in1=weight, op=ALU.mult)
+                    nc.vector.tensor_tensor(out=total[:], in0=total[:], in1=prod[:], op=ALU.add)
+            result = hold.tile([P, CG, PIX], F32)
+            nc.vector.tensor_tensor(
+                out=result[:],
+                in0=total[:].rearrange("g c h w -> g c (h w)"),
+                in1=rcp_g[:].unsqueeze(1).to_broadcast([P, CG, PIX]),
+                op=ALU.mult,
+            )
+            nc.sync.dma_start(out=out[0].rearrange("(g c) h w -> g c (h w)", c=CG), in_=result[:])

@@ -30,6 +30,16 @@ PAD = KER // 2
 TAPS = KER * KER
 O = G * TAPS
 N_TILE = 512
+ROWS2 = 2
+PAIR = ROWS2 * W
+N_PAIRS = H // ROWS2
+WIN_ROWS = P // W
+QUADS = 32
+GQ = G // QUADS
+CHUNK = 64
+BAND_PITCH = 132
+BAND_START = 28
+BAND_WORDS = BAND_START + CHUNK * BAND_PITCH + 4
 
 FLOPS = 2 * C * R * PIX + 2 * R * O * PIX + 2 * TAPS * C * PIX
 
@@ -79,70 +89,106 @@ def tile_involution_w_kernel(
         e_pix = [keep.tile([P, TAPS, G], F32, name="e_pix%d" % pb) for pb in range(PB)]
         e_sum = [keep.tile([P, G], F32, name="e_sum%d" % pb) for pb in range(PB)]
         e_rcp = [keep.tile([P, G], F32, name="e_rcp%d" % pb) for pb in range(PB)]
+        x8_bf = keep.tile([P, N_PAIRS, QUADS, GQ, CG], BF16)
+        band_first = keep.tile([P, BAND_WORDS], F32)
+        nc.gpsimd.memset(band_first[:], 0.0)
+        edge = keep.tile([P, W, KER], F32)
+        nc.vector.memset(edge[:], 1.0)
+        for w in range(PAD):
+            nc.vector.memset(edge[:, w, 0 : PAD - w], 0.0)
+            nc.vector.memset(edge[:, W - 1 - w, KER - PAD + w : KER], 0.0)
 
         with ExitStack() as branch:
             front = branch.enter_context(tc.tile_pool(name="front", bufs=1))
             ring = branch.enter_context(tc.tile_pool(name="ring", bufs=4))
-            work = branch.enter_context(tc.tile_pool(name="work", bufs=3))
+            work = branch.enter_context(tc.tile_pool(name="work", bufs=2))
             psum_mx = branch.enter_context(tc.psum_pool(name="psum_mx", bufs=4))
-            psum_tr = branch.enter_context(tc.psum_pool(name="psum_tr", bufs=2))
 
-            x_raw = front.tile([P, KG, PACK * PIX], BF16)
-            nc.sync.dma_start(out=x_raw[:], in_=x[0].rearrange("(g p t) h w -> p g (t h w)", g=KG, p=P, t=PACK))
-            w1_planes = front.tile([P, R], U8, align_bytes=64)
-            load_scale_planes(nc, w1_planes, w_reduce_scales)
-            b1_bc = front.tile([P, R], BF16)
-            nc.scalar.dma_start(out=b1_bc[:], in_=b_reduce.partition_broadcast(P))
-            b2_bc = front.tile([P, O], BF16)
-            nc.scalar.dma_start(out=b2_bc[:], in_=b_span.partition_broadcast(P))
-
-            x_grouped = front.tile([P, KG, PIX, PACK], BF16, align_bytes=64)
-            nc.vector.tensor_copy(out=x_grouped[:], in_=x_raw[:].rearrange("p g (t x) -> p g x t", t=PACK))
             x_codes = front.tile([P, KG * PIX], U32, align_bytes=64)
             x_planes = front.tile([P, KG * PIX], U8, align_bytes=64)
-            nc.vector.quantize_mx(
-                out=x_codes[:].bitcast(FP8X4),
-                scales=x_planes[:],
-                in_=x_grouped[:].rearrange("p g x t -> p (g x t)"),
-            )
-
-            red_pix = [front.tile([P, KG, PACK, P], BF16, name="red_pix%d" % pb) for pb in range(PB)]
-            red_grouped = front.tile([P, KG, PIX, PACK], BF16, align_bytes=64)
             red_codes = front.tile([P, KG * PIX], U32, align_bytes=64)
             red_planes = front.tile([P, KG * PIX], U8, align_bytes=64)
-            for rt in range(R // N_TILE):
-                wt = load_weight_tile(nc, ring, w_reduce_words, rt * N_TILE, N_TILE)
-                for pb in range(PB):
-                    acc = psum_mx.tile([P, N_TILE], F32, name="acc")
-                    mx_product(nc, acc[:], x_codes, x_planes, pb, wt, w1_planes, rt * N_TILE, N_TILE)
-                    pre = work.tile([P, N_TILE], F32, name="pre")
-                    nc.vector.tensor_tensor(
-                        out=pre[:], in0=acc[:], in1=b1_bc[:, rt * N_TILE : (rt + 1) * N_TILE], op=ALU.add
-                    )
-                    nc.scalar.activation(
-                        out=red_pix[pb][:, rt, :, :],
-                        in_=pre[:].rearrange("x (p t) -> x t p", t=PACK),
-                        func=ACT.Relu,
-                    )
             w2_planes = front.tile([P, O], U8, align_bytes=64)
-            load_scale_planes(nc, w2_planes, w_span_scales)
-            for g in range(KG):
-                for pb in range(PB):
-                    flipped = psum_tr.tile([P, PACK, P], BF16, name="flipped")
-                    for t in range(PACK):
-                        nc.tensor.transpose(flipped[:, t, :], red_pix[pb][:, g, t, :], ident_bf[:])
-                    nc.vector.tensor_copy(
-                        out=red_grouped[:, g, pb * P : (pb + 1) * P, :],
-                        in_=flipped[:].rearrange("p t x -> p x t"),
-                    )
-                nc.vector.quantize_mx(
-                    out=red_codes[:, g * PIX : (g + 1) * PIX].bitcast(FP8X4),
-                    scales=red_planes[:, g * PIX : (g + 1) * PIX],
-                    in_=red_grouped[:, g, :, :].rearrange("p x t -> p (x t)"),
-                )
+            b2_bc = front.tile([P, O], BF16)
 
-            z = [front.tile([P, O], F32, name="z%d" % pb) for pb in range(PB)]
-            z_max = [front.tile([P, G], F32, name="z_max%d" % pb) for pb in range(PB)]
+            with ExitStack() as reduce_scope:
+                early = reduce_scope.enter_context(tc.tile_pool(name="early", bufs=1))
+                psum_tr = reduce_scope.enter_context(tc.psum_pool(name="psum_tr", bufs=2))
+                w1_planes = early.tile([P, R], U8, align_bytes=64)
+                x_ch = early.tile([P, C // P, (PAD + H + PAD + 1) * W], BF16)
+                b1_bc = early.tile([P, R], BF16)
+
+                with tc.tile_pool(name="xq", bufs=1) as xq:
+                    x_raw = xq.tile([P, KG, PACK * PIX], BF16)
+                    nc.sync.dma_start(
+                        out=x_raw[:], in_=x[0].rearrange("(g p t) h w -> p g (t h w)", g=KG, p=P, t=PACK)
+                    )
+                    x_grouped = xq.tile([P, KG, PIX, PACK], BF16, align_bytes=64)
+                    nc.vector.tensor_copy(out=x_grouped[:], in_=x_raw[:].rearrange("p g (t x) -> p g x t", t=PACK))
+                    nc.vector.quantize_mx(
+                        out=x_codes[:].bitcast(FP8X4),
+                        scales=x_planes[:],
+                        in_=x_grouped[:].rearrange("p g x t -> p (g x t)"),
+                    )
+                load_scale_planes(nc, w1_planes, w_reduce_scales)
+
+                nc.vector.memset(x_ch[:, :, : PAD * W], 0.0)
+                nc.vector.memset(x_ch[:, :, (PAD + H) * W :], 0.0)
+                nc.scalar.dma_start(
+                    out=x_ch[:, :, PAD * W : (PAD + H) * W], in_=x[0].rearrange("(b c) h w -> c b (h w)", c=P)
+                )
+                nc.scalar.dma_start(out=b1_bc[:], in_=b_reduce.partition_broadcast(P))
+                nc.scalar.dma_start(out=b2_bc[:], in_=b_span.partition_broadcast(P))
+                for a in range(N_PAIRS):
+                    for hb in range(2):
+                        x_turned = psum_tr.tile([P, 8, P], BF16, name="x_turned")
+                        for u in range(8):
+                            nc.tensor.transpose(
+                                x_turned[:, u, :], x_ch[:, 8 * hb + u, PAIR * a : PAIR * a + P], ident_bf[:]
+                            )
+                        nc.scalar.copy(
+                            out=x8_bf[:, a, :, 2 * hb : 2 * hb + 2, :],
+                            in_=x_turned[:].rearrange("k u m -> k (u m)").rearrange(
+                                "k (f q c) -> k q f c", f=2, q=QUADS
+                            ),
+                        )
+
+                with tc.tile_pool(name="redq", bufs=1) as redq:
+                    red_pix = [redq.tile([P, KG, PACK, P], BF16, name="red_pix%d" % pb) for pb in range(PB)]
+                    red_grouped = redq.tile([P, KG, PIX, PACK], BF16, align_bytes=64)
+                    for rt in range(R // N_TILE):
+                        wt = load_weight_tile(nc, ring, w_reduce_words, rt * N_TILE, N_TILE)
+                        for pb in range(PB):
+                            acc = psum_mx.tile([P, N_TILE], F32, name="acc")
+                            mx_product(nc, acc[:], x_codes, x_planes, pb, wt, w1_planes, rt * N_TILE, N_TILE)
+                            pre = work.tile([P, N_TILE], F32, name="pre")
+                            nc.vector.tensor_tensor(
+                                out=pre[:], in0=acc[:], in1=b1_bc[:, rt * N_TILE : (rt + 1) * N_TILE], op=ALU.add
+                            )
+                            nc.scalar.activation(
+                                out=red_pix[pb][:, rt, :, :],
+                                in_=pre[:].rearrange("x (p t) -> x t p", t=PACK),
+                                func=ACT.Relu,
+                            )
+                    load_scale_planes(nc, w2_planes, w_span_scales)
+                    for g in range(KG):
+                        for pb in range(PB):
+                            flipped = psum_tr.tile([P, PACK, P], BF16, name="flipped")
+                            for t in range(PACK):
+                                nc.tensor.transpose(flipped[:, t, :], red_pix[pb][:, g, t, :], ident_bf[:])
+                            nc.vector.tensor_copy(
+                                out=red_grouped[:, g, pb * P : (pb + 1) * P, :],
+                                in_=flipped[:].rearrange("p t x -> p x t"),
+                            )
+                        nc.vector.quantize_mx(
+                            out=red_codes[:, g * PIX : (g + 1) * PIX].bitcast(FP8X4),
+                            scales=red_planes[:, g * PIX : (g + 1) * PIX],
+                            in_=red_grouped[:, g, :, :].rearrange("p x t -> p (x t)"),
+                        )
+
+            late = branch.enter_context(tc.tile_pool(name="late", bufs=1))
+            z = [late.tile([P, O], F32, name="z%d" % pb) for pb in range(PB)]
+            z_max = [late.tile([P, G], F32, name="z_max%d" % pb) for pb in range(PB)]
             g_lo = 0
             for col0 in range(0, O, N_TILE):
                 ncols = min(N_TILE, O - col0)
@@ -187,43 +233,124 @@ def tile_involution_w_kernel(
 
         with ExitStack() as taps:
             hold = taps.enter_context(tc.tile_pool(name="hold", bufs=1))
-            prods = taps.enter_context(tc.tile_pool(name="prods", bufs=2))
-            psum_g = taps.enter_context(tc.psum_pool(name="psum_g", bufs=4))
+            turn = taps.enter_context(tc.tile_pool(name="turn", bufs=2))
+            psum_t1 = taps.enter_context(tc.psum_pool(name="psum_t1", bufs=2))
+            psum_t2 = taps.enter_context(tc.psum_pool(name="psum_t2", bufs=3))
+            psum_mm = taps.enter_context(tc.psum_pool(name="psum_mm", bufs=2))
+            psum_t3 = taps.enter_context(tc.psum_pool(name="psum_t3", bufs=1))
 
-            x_g = hold.tile([P, CG, H, W], BF16)
-            nc.sync.dma_start(out=x_g[:], in_=x[0].rearrange("(g c) h w -> g c h w", c=CG))
-            x_pad = hold.tile([P, CG, H + 2 * PAD, W + 2 * PAD], BF16)
-            nc.vector.memset(x_pad[:], 0.0)
-            nc.vector.tensor_copy(out=x_pad[:, :, PAD : PAD + H, PAD : PAD + W], in_=x_g[:])
+            band_second = hold.tile([P, BAND_WORDS], F32)
+            nc.gpsimd.memset(band_second[:], 0.0)
+            band_tiles = [band_first, band_second]
 
-            rcp_g = hold.tile([P, PIX], F32)
-            turned = psum_g.tile([P, PIX], F32, name="turned")
+            scale = hold.tile([P, PIX, KER], F32)
+            rcp_turned = psum_t3.tile([P, 4, P], F32, name="out_turned")
             for pb in range(PB):
-                nc.tensor.transpose(turned[:, pb * P : (pb + 1) * P], e_rcp[pb][:], ident_f32[:])
-            nc.scalar.copy(out=rcp_g[:], in_=turned[:])
-            e_g = hold.tile([P, TAPS, PIX], F32)
-            for tap in range(TAPS):
-                turned = psum_g.tile([P, PIX], F32, name="turned")
-                for pb in range(PB):
-                    nc.tensor.transpose(turned[:, pb * P : (pb + 1) * P], e_pix[pb][:, tap, :], ident_f32[:])
-                nc.scalar.copy(out=e_g[:, tap, :], in_=turned[:])
+                nc.tensor.transpose(rcp_turned[:, pb, :], e_rcp[pb][:], ident_f32[:])
+                nc.vector.tensor_tensor(
+                    out=scale[:, pb * P : (pb + 1) * P, :].rearrange("g (h w) j -> g h w j", w=W),
+                    in0=rcp_turned[:, pb, :].rearrange("g (h w) -> g h w", w=W).unsqueeze(3).to_broadcast([P, P // W, W, KER]),
+                    in1=edge[:].unsqueeze(1).to_broadcast([P, P // W, W, KER]),
+                    op=ALU.mult,
+                )
 
-            total = hold.tile([P, CG, H, W], F32)
-            for tap in range(TAPS):
-                i, j = divmod(tap, KER)
-                window = x_pad[:, :, i : i + H, j : j + W]
-                weight = e_g[:, tap, :].rearrange("g (h w) -> g h w", h=H).unsqueeze(1).to_broadcast([P, CG, H, W])
-                if tap == 0:
-                    nc.vector.tensor_tensor(out=total[:], in0=window, in1=weight, op=ALU.mult)
-                else:
-                    prod = prods.tile([P, CG, H, W], F32, name="prod")
-                    nc.vector.tensor_tensor(out=prod[:], in0=window, in1=weight, op=ALU.mult)
-                    nc.vector.tensor_tensor(out=total[:], in0=total[:], in1=prod[:], op=ALU.add)
-            result = hold.tile([P, CG, PIX], F32)
-            nc.vector.tensor_tensor(
-                out=result[:],
-                in0=total[:].rearrange("g c h w -> g c (h w)"),
-                in1=rcp_g[:].unsqueeze(1).to_broadcast([P, CG, PIX]),
-                op=ALU.mult,
-            )
-            nc.sync.dma_start(out=out[0].rearrange("(g c) h w -> g c (h w)", c=CG), in_=result[:])
+            x8_of = {}
+            banded_of = {}
+            sums_of = {}
+
+            def lay_weights(step):
+                chunk, part = divmod(step, 2)
+                pb, half = divmod(chunk, P // CHUNK)
+                weights = band_tiles[chunk % 2][:, BAND_START : BAND_START + CHUNK * BAND_PITCH].rearrange(
+                    "g (n l) -> g n l", l=BAND_PITCH
+                )
+                for i in range(4 * part, min(4 * part + 4, KER)):
+                    for j0 in range(0, KER, 4):
+                        nj = min(4, KER - j0)
+                        e_turned = psum_t1.tile([P, 4, P], F32, name="e_turned")
+                        for j in range(j0, j0 + nj):
+                            nc.tensor.transpose(e_turned[:, j - j0, :], e_pix[pb][:, KER * i + j, :], ident_f32[:])
+                        nc.vector.tensor_tensor(
+                            out=weights[:, :, W * i + j0 : W * i + j0 + nj],
+                            in0=e_turned[:, :nj, CHUNK * half : CHUNK * (half + 1)].rearrange("g j n -> g n j"),
+                            in1=scale[:, CHUNK * chunk : CHUNK * (chunk + 1), j0 : j0 + nj],
+                            op=ALU.mult,
+                        )
+
+            def turn_weights(a):
+                chunk, a2 = divmod(a, CHUNK // PAIR)
+                band = band_tiles[chunk % 2]
+                x8 = turn.tile([P, QUADS, GQ * CG], F32, name="x8")
+                nc.gpsimd.tensor_scalar(
+                    out=x8[:].rearrange("k q m -> k (q m)"),
+                    in0=x8_bf[:, a].rearrange("k q f c -> k (q f c)"),
+                    scalar1=1.0,
+                    scalar2=0.0,
+                    op0=ALU.mult,
+                    op1=ALU.add,
+                )
+                banded = turn.tile([P, QUADS, GQ, PAIR], F32, name="banded")
+                for u in range(PAIR // 4):
+                    w_turned = psum_t2.tile([P, 4, P], F32, name="w_turned")
+                    for v in range(4):
+                        n = 4 * u + v
+                        first = BAND_START + BAND_PITCH * (PAIR * a2 + n) - (n - PAD)
+                        nc.tensor.transpose(w_turned[:, v, :], band[:, first : first + P], ident_f32[:])
+                    sorted_view = w_turned[:].rearrange("k v (f q) -> k q f v", f=GQ)
+                    if (u // 2) % 2 == 0:
+                        nc.vector.tensor_copy(out=banded[:, :, :, 4 * u : 4 * u + 4], in_=sorted_view)
+                    else:
+                        nc.scalar.copy(out=banded[:, :, :, 4 * u : 4 * u + 4], in_=sorted_view)
+                x8_of[a] = x8
+                banded_of[a] = banded
+
+            def multiply(a):
+                sums = turn.tile([P, QUADS, CG], F32, name="sums")
+                for qb in range(QUADS // 8):
+                    crossed = psum_mm.tile([P, 8, GQ * CG], F32, name="crossed")
+                    for q8 in range(8):
+                        q = 8 * qb + q8
+                        nc.tensor.matmul(
+                            out=crossed[:, q8, :],
+                            lhsT=banded_of[a][:, q].rearrange("k f n -> k (f n)"),
+                            rhs=x8_of[a][:, q, :],
+                            start=True,
+                            stop=True,
+                        )
+                    for f in range(GQ):
+                        rows = slice(PAIR * f, PAIR * (f + 1))
+                        if f % 2 == 0:
+                            nc.vector.tensor_copy(
+                                out=sums[rows, 8 * qb : 8 * qb + 8, :], in_=crossed[rows, :, CG * f : CG * (f + 1)]
+                            )
+                        else:
+                            nc.scalar.copy(
+                                out=sums[rows, 8 * qb : 8 * qb + 8, :], in_=crossed[rows, :, CG * f : CG * (f + 1)]
+                            )
+                sums_of[a] = sums
+
+            def store(a):
+                out_turned = psum_t3.tile([P, 4, P], F32, name="out_turned")
+                for t in range(4):
+                    nc.tensor.transpose(
+                        out_turned[:, t, :],
+                        sums_of[a][:, 8 * t : 8 * t + 8, :].rearrange("k q c -> k (q c)"),
+                        ident_f32[:],
+                    )
+                result = turn.tile([P, GQ, 4, PAIR], F32, name="result")
+                nc.scalar.copy(out=result[:], in_=out_turned[:].rearrange("m t (f n) -> m f t n", f=GQ))
+                nc.sync.dma_start(
+                    out=out[0].rearrange("(b m) h w -> m b (h w)", m=P)[:, :, PAIR * a : PAIR * (a + 1)],
+                    in_=result[:].rearrange("m f t n -> m (f t) n"),
+                )
+
+            with tc.manual_schedule():
+                for step in range(N_PAIRS + 4):
+                    if 0 <= step - 2 < N_PAIRS:
+                        turn_weights(step - 2)
+                    if step < N_PAIRS:
+                        lay_weights(step)
+                    if 0 <= step - 3 < N_PAIRS:
+                        multiply(step - 3)
+                    if 0 <= step - 4 < N_PAIRS:
+                        store(step - 4)

@@ -30,16 +30,15 @@ PAD = KER // 2
 TAPS = KER * KER
 O = G * TAPS
 N_TILE = 512
-ROWS2 = 2
-PAIR = ROWS2 * W
-N_PAIRS = H // ROWS2
-WIN_ROWS = P // W
-QUADS = 32
-GQ = G // QUADS
-CHUNK = 64
+
+PAIR = 2 * W
+N_PAIRS = PIX // PAIR
+PAIRS_PB = P // PAIR
+GH = 2
+QS = G // GH
 BAND_PITCH = 132
 BAND_START = 28
-BAND_WORDS = BAND_START + CHUNK * BAND_PITCH + 4
+BAND_LEN = BAND_START + PAIR * BAND_PITCH + 4
 
 FLOPS = 2 * C * R * PIX + 2 * R * O * PIX + 2 * TAPS * C * PIX
 
@@ -86,21 +85,30 @@ def tile_involution_w_kernel(
         make_identity(nc, ident_bf[:])
         ident_f32 = keep.tile([P, P], F32)
         make_identity(nc, ident_f32[:])
+        edge = keep.tile([P, KER, W], F32)
+        nc.vector.memset(edge[:], 1.0)
+        for w in range(PAD):
+            nc.vector.memset(edge[:, 0 : PAD - w, w : w + 1], 0.0)
+            nc.vector.memset(edge[:, KER - PAD + w : KER, W - 1 - w : W - w], 0.0)
+        ident_edge = keep.tile([P, KER, P], F32)
+        nc.vector.tensor_tensor(
+            out=ident_edge[:].rearrange("k j (h w) -> k j h w", w=W),
+            in0=ident_f32[:].rearrange("k (h w) -> k h w", w=W).unsqueeze(1).to_broadcast([P, KER, P // W, W]),
+            in1=edge[:].unsqueeze(2).to_broadcast([P, KER, P // W, W]),
+            op=ALU.mult,
+        )
         e_pix = [keep.tile([P, TAPS, G], F32, name="e_pix%d" % pb) for pb in range(PB)]
         e_sum = [keep.tile([P, G], F32, name="e_sum%d" % pb) for pb in range(PB)]
         e_rcp = [keep.tile([P, G], F32, name="e_rcp%d" % pb) for pb in range(PB)]
-        x8_bf = keep.tile([P, N_PAIRS, QUADS, GQ, CG], BF16)
-        band_first = keep.tile([P, BAND_WORDS], F32)
-        nc.gpsimd.memset(band_first[:], 0.0)
-        edge = keep.tile([P, W, KER], F32)
-        nc.vector.memset(edge[:], 1.0)
-        for w in range(PAD):
-            nc.vector.memset(edge[:, w, 0 : PAD - w], 0.0)
-            nc.vector.memset(edge[:, W - 1 - w, KER - PAD + w : KER], 0.0)
+        x8 = keep.tile([P, N_PAIRS, QS, GH, CG], BF16)
+        bands = [[keep.tile([P, BAND_LEN], BF16, name="band%d_%d" % (part, b)) for b in range(2)] for part in range(2)]
+        for part in range(2):
+            for b in range(2):
+                nc.gpsimd.memset(bands[part][b][:], 0.0)
 
         with ExitStack() as branch:
             front = branch.enter_context(tc.tile_pool(name="front", bufs=1))
-            ring = branch.enter_context(tc.tile_pool(name="ring", bufs=4))
+            ring = branch.enter_context(tc.tile_pool(name="ring", bufs=3))
             work = branch.enter_context(tc.tile_pool(name="work", bufs=2))
             psum_mx = branch.enter_context(tc.psum_pool(name="psum_mx", bufs=4))
 
@@ -140,17 +148,15 @@ def tile_involution_w_kernel(
                 nc.scalar.dma_start(out=b1_bc[:], in_=b_reduce.partition_broadcast(P))
                 nc.scalar.dma_start(out=b2_bc[:], in_=b_span.partition_broadcast(P))
                 for a in range(N_PAIRS):
-                    for hb in range(2):
+                    for f in range(GH):
                         x_turned = psum_tr.tile([P, 8, P], BF16, name="x_turned")
                         for u in range(8):
                             nc.tensor.transpose(
-                                x_turned[:, u, :], x_ch[:, 8 * hb + u, PAIR * a : PAIR * a + P], ident_bf[:]
+                                x_turned[:, u, :], x_ch[:, 8 * f + u, PAIR * a : PAIR * a + P], ident_bf[:]
                             )
                         nc.scalar.copy(
-                            out=x8_bf[:, a, :, 2 * hb : 2 * hb + 2, :],
-                            in_=x_turned[:].rearrange("k u m -> k (u m)").rearrange(
-                                "k (f q c) -> k q f c", f=2, q=QUADS
-                            ),
+                            out=x8[:, a, :, f, :],
+                            in_=x_turned[:].rearrange("k u m -> k (u m)").rearrange("k (q c) -> k q c", c=CG),
                         )
 
                 with tc.tile_pool(name="redq", bufs=1) as redq:
@@ -234,123 +240,116 @@ def tile_involution_w_kernel(
         with ExitStack() as taps:
             hold = taps.enter_context(tc.tile_pool(name="hold", bufs=1))
             turn = taps.enter_context(tc.tile_pool(name="turn", bufs=2))
-            psum_t1 = taps.enter_context(tc.psum_pool(name="psum_t1", bufs=2))
-            psum_t2 = taps.enter_context(tc.psum_pool(name="psum_t2", bufs=3))
+            psum_w = taps.enter_context(tc.psum_pool(name="psum_w", bufs=3))
             psum_mm = taps.enter_context(tc.psum_pool(name="psum_mm", bufs=2))
-            psum_t3 = taps.enter_context(tc.psum_pool(name="psum_t3", bufs=1))
+            psum_f = taps.enter_context(tc.psum_pool(name="psum_f", bufs=3))
 
-            band_second = hold.tile([P, BAND_WORDS], F32)
-            nc.gpsimd.memset(band_second[:], 0.0)
-            band_tiles = [band_first, band_second]
-
-            scale = hold.tile([P, PIX, KER], F32)
-            rcp_turned = psum_t3.tile([P, 4, P], F32, name="out_turned")
-            for pb in range(PB):
-                nc.tensor.transpose(rcp_turned[:, pb, :], e_rcp[pb][:], ident_f32[:])
-                nc.vector.tensor_tensor(
-                    out=scale[:, pb * P : (pb + 1) * P, :].rearrange("g (h w) j -> g h w j", w=W),
-                    in0=rcp_turned[:, pb, :].rearrange("g (h w) -> g h w", w=W).unsqueeze(3).to_broadcast([P, P // W, W, KER]),
-                    in1=edge[:].unsqueeze(1).to_broadcast([P, P // W, W, KER]),
-                    op=ALU.mult,
-                )
-
-            x8_of = {}
+            rcp_g = hold.tile([P, PB, P], F32)
+            p_g = [hold.tile([P, TAPS, P], F32, name="p_g%d" % pb) for pb in range(PB)]
             banded_of = {}
             sums_of = {}
+            result_of = {}
 
-            def lay_weights(step):
-                chunk, part = divmod(step, 2)
-                pb, half = divmod(chunk, P // CHUNK)
-                weights = band_tiles[chunk % 2][:, BAND_START : BAND_START + CHUNK * BAND_PITCH].rearrange(
-                    "g (n l) -> g n l", l=BAND_PITCH
-                )
-                for i in range(4 * part, min(4 * part + 4, KER)):
-                    for j0 in range(0, KER, 4):
-                        nj = min(4, KER - j0)
-                        e_turned = psum_t1.tile([P, 4, P], F32, name="e_turned")
-                        for j in range(j0, j0 + nj):
-                            nc.tensor.transpose(e_turned[:, j - j0, :], e_pix[pb][:, KER * i + j, :], ident_f32[:])
-                        nc.vector.tensor_tensor(
-                            out=weights[:, :, W * i + j0 : W * i + j0 + nj],
-                            in0=e_turned[:, :nj, CHUNK * half : CHUNK * (half + 1)].rearrange("g j n -> g n j"),
-                            in1=scale[:, CHUNK * chunk : CHUNK * (chunk + 1), j0 : j0 + nj],
-                            op=ALU.mult,
-                        )
+            def normalise(step):
+                pb, quarter = divmod(step, 4)
+                first = 12 * quarter
+                last = TAPS if quarter == 3 else first + 12
+                for tap0 in range(first, last, 4):
+                    nt = min(4, last - tap0)
+                    e_turned = psum_f.tile([P, 4, P], F32, name="turned")
+                    for tap in range(tap0, tap0 + nt):
+                        nc.tensor.transpose(e_turned[:, tap - tap0, :], e_pix[pb][:, tap, :], ident_edge[:, tap % KER, :])
+                    nc.vector.tensor_tensor(
+                        out=p_g[pb][:, tap0 : tap0 + nt, :],
+                        in0=e_turned[:, :nt, :],
+                        in1=rcp_g[:, pb, :].unsqueeze(1).to_broadcast([P, nt, P]),
+                        op=ALU.mult,
+                    )
 
-            def turn_weights(a):
-                chunk, a2 = divmod(a, CHUNK // PAIR)
-                band = band_tiles[chunk % 2]
-                x8 = turn.tile([P, QUADS, GQ * CG], F32, name="x8")
-                nc.gpsimd.tensor_scalar(
-                    out=x8[:].rearrange("k q m -> k (q m)"),
-                    in0=x8_bf[:, a].rearrange("k q f c -> k (q f c)"),
-                    scalar1=1.0,
-                    scalar2=0.0,
-                    op0=ALU.mult,
-                    op1=ALU.add,
-                )
-                banded = turn.tile([P, QUADS, GQ, PAIR], F32, name="banded")
-                for u in range(PAIR // 4):
-                    w_turned = psum_t2.tile([P, 4, P], F32, name="w_turned")
-                    for v in range(4):
-                        n = 4 * u + v
-                        first = BAND_START + BAND_PITCH * (PAIR * a2 + n) - (n - PAD)
-                        nc.tensor.transpose(w_turned[:, v, :], band[:, first : first + P], ident_f32[:])
-                    sorted_view = w_turned[:].rearrange("k v (f q) -> k q f v", f=GQ)
-                    if (u // 2) % 2 == 0:
-                        nc.vector.tensor_copy(out=banded[:, :, :, 4 * u : 4 * u + 4], in_=sorted_view)
-                    else:
-                        nc.scalar.copy(out=banded[:, :, :, 4 * u : 4 * u + 4], in_=sorted_view)
-                x8_of[a] = x8
-                banded_of[a] = banded
+            def split(a):
+                pb, a4 = divmod(a, PAIRS_PB)
+                p_view = p_g[pb][:, :, PAIR * a4 : PAIR * (a4 + 1)].rearrange("g (i j) n -> g n i j", j=KER)
+                places = [
+                    bands[part][a % 2][:, BAND_START : BAND_START + PAIR * BAND_PITCH]
+                    .rearrange("g (n l) -> g n l", l=BAND_PITCH)[:, :, : KER * W]
+                    .rearrange("g n (i w) -> g n i w", w=W)[:, :, :, :KER]
+                    for part in range(2)
+                ]
+                nc.scalar.copy(out=places[0], in_=p_view)
+                nc.gpsimd.tensor_tensor(out=places[1], in0=p_view, in1=places[0], op=ALU.subtract)
 
-            def multiply(a):
-                sums = turn.tile([P, QUADS, CG], F32, name="sums")
-                for qb in range(QUADS // 8):
-                    crossed = psum_mm.tile([P, 8, GQ * CG], F32, name="crossed")
-                    for q8 in range(8):
-                        q = 8 * qb + q8
-                        nc.tensor.matmul(
-                            out=crossed[:, q8, :],
-                            lhsT=banded_of[a][:, q].rearrange("k f n -> k (f n)"),
-                            rhs=x8_of[a][:, q, :],
-                            start=True,
-                            stop=True,
-                        )
-                    for f in range(GQ):
-                        rows = slice(PAIR * f, PAIR * (f + 1))
-                        if f % 2 == 0:
-                            nc.vector.tensor_copy(
-                                out=sums[rows, 8 * qb : 8 * qb + 8, :], in_=crossed[rows, :, CG * f : CG * (f + 1)]
-                            )
-                        else:
-                            nc.scalar.copy(
-                                out=sums[rows, 8 * qb : 8 * qb + 8, :], in_=crossed[rows, :, CG * f : CG * (f + 1)]
-                            )
-                sums_of[a] = sums
+            def turn_bank(a, k):
+                part, u = divmod(k, 4)
+                if k == 0:
+                    banded_of[a] = turn.tile([P, QS, 2, GH, PAIR], BF16, name="banded")
+                w_turned = psum_w.tile([P, 8, P], BF16, name="w_turned")
+                for v in range(8):
+                    n = 8 * u + v
+                    first = BAND_START + BAND_PITCH * n - (n - PAD)
+                    nc.tensor.transpose(w_turned[:, v, :], bands[part][a % 2][:, first : first + P], ident_bf[:])
+                sorted_view = w_turned[:].rearrange("k v (f q) -> k q f v", f=GH)
+                if u < 2:
+                    nc.vector.tensor_copy(out=banded_of[a][:, :, part, :, 8 * u : 8 * u + 8], in_=sorted_view)
+                else:
+                    nc.scalar.copy(out=banded_of[a][:, :, part, :, 8 * u : 8 * u + 8], in_=sorted_view)
 
-            def store(a):
-                out_turned = psum_t3.tile([P, 4, P], F32, name="out_turned")
-                for t in range(4):
+            def multiply_bank(a, qb):
+                if qb == 0:
+                    sums_of[a] = turn.tile([P, GH, QS, CG], F32, name="sums")
+                crossed = psum_mm.tile([P, 16, GH * CG], F32, name="crossed")
+                for q16 in range(16):
+                    q = 16 * qb + q16
+                    nc.tensor.matmul(
+                        out=crossed[:, q16, :],
+                        lhsT=banded_of[a][:, q].rearrange("k s f n -> k (s f n)"),
+                        rhs=x8[:, a, q].rearrange("k f c -> k (f c)"),
+                        start=True,
+                        stop=True,
+                    )
+                crossed_view = crossed[:].rearrange("k q (f c) -> k f q c", f=GH)
+                if qb % 2 == 0:
+                    nc.vector.tensor_copy(out=sums_of[a][:, :, 16 * qb : 16 * qb + 16, :], in_=crossed_view)
+                else:
+                    nc.scalar.copy(out=sums_of[a][:, :, 16 * qb : 16 * qb + 16, :], in_=crossed_view)
+
+            def store_bank(a, k):
+                f, th = divmod(k, 2)
+                if k == 0:
+                    result_of[a] = turn.tile([P, GH, 8, PAIR], F32, name="result")
+                out_turned = psum_f.tile([P, 4, P], F32, name="turned")
+                for t4 in range(4):
+                    t = 4 * th + t4
                     nc.tensor.transpose(
-                        out_turned[:, t, :],
-                        sums_of[a][:, 8 * t : 8 * t + 8, :].rearrange("k q c -> k (q c)"),
+                        out_turned[:, t4, :],
+                        sums_of[a][:, f, 8 * t : 8 * t + 8, :].rearrange("k q c -> k (q c)"),
                         ident_f32[:],
                     )
-                result = turn.tile([P, GQ, 4, PAIR], F32, name="result")
-                nc.scalar.copy(out=result[:], in_=out_turned[:].rearrange("m t (f n) -> m f t n", f=GQ))
-                nc.sync.dma_start(
-                    out=out[0].rearrange("(b m) h w -> m b (h w)", m=P)[:, :, PAIR * a : PAIR * (a + 1)],
-                    in_=result[:].rearrange("m f t n -> m (f t) n"),
+                parts = out_turned[:].rearrange("m t (s f n) -> m t s f n", s=2, f=GH)
+                lo_part = turn.tile([P, 4, PAIR], F32, name="lo_part")
+                nc.scalar.copy(out=lo_part[:], in_=parts[:, :, 1, f, :])
+                nc.vector.tensor_tensor(
+                    out=result_of[a][:, f, 4 * th : 4 * th + 4, :], in0=parts[:, :, 0, f, :], in1=lo_part[:], op=ALU.add
                 )
+                if k == 3:
+                    nc.sync.dma_start(
+                        out=out[0].rearrange("(b m) h w -> m b (h w)", m=P)[:, :, PAIR * a : PAIR * (a + 1)],
+                        in_=result_of[a][:].rearrange("m f t n -> m (f t) n"),
+                    )
 
             with tc.manual_schedule():
-                for step in range(N_PAIRS + 4):
-                    if 0 <= step - 2 < N_PAIRS:
-                        turn_weights(step - 2)
+                rcp_turned = psum_f.tile([P, 4, P], F32, name="turned")
+                for pb in range(PB):
+                    nc.tensor.transpose(rcp_turned[:, pb, :], e_rcp[pb][:], ident_f32[:])
+                nc.vector.tensor_copy(out=rcp_g[:], in_=rcp_turned[:, :PB, :])
+                for step in range(N_PAIRS + 7):
                     if step < N_PAIRS:
-                        lay_weights(step)
-                    if 0 <= step - 3 < N_PAIRS:
-                        multiply(step - 3)
+                        normalise(step)
                     if 0 <= step - 4 < N_PAIRS:
-                        store(step - 4)
+                        split(step - 4)
+                    for k in range(8):
+                        if 0 <= step - 5 < N_PAIRS:
+                            turn_bank(step - 5, k)
+                        if k % 2 == 1 and 0 <= step - 6 < N_PAIRS:
+                            multiply_bank(step - 6, k // 2)
+                        if k % 2 == 0 and 0 <= step - 7 < N_PAIRS:
+                            store_bank(step - 7, k // 2)

@@ -36,9 +36,9 @@ N_PAIRS = PIX // PAIR
 PAIRS_PB = P // PAIR
 GH = 2
 QS = G // GH
-BAND_PITCH = 132
-BAND_START = 28
-BAND_LEN = BAND_START + PAIR * BAND_PITCH + 4
+BAND_PITCH = 136
+BAND_START = 32
+BAND_LEN = BAND_START + PAIR * BAND_PITCH + 8
 
 FLOPS = 2 * C * R * PIX + 2 * R * O * PIX + 2 * TAPS * C * PIX
 
@@ -241,8 +241,8 @@ def tile_involution_w_kernel(
             hold = taps.enter_context(tc.tile_pool(name="hold", bufs=1))
             turn = taps.enter_context(tc.tile_pool(name="turn", bufs=2))
             psum_w = taps.enter_context(tc.psum_pool(name="psum_w", bufs=3))
-            psum_mm = taps.enter_context(tc.psum_pool(name="psum_mm", bufs=2))
-            psum_f = taps.enter_context(tc.psum_pool(name="psum_f", bufs=3))
+            psum_mm = taps.enter_context(tc.psum_pool(name="psum_mm", bufs=3))
+            psum_f = taps.enter_context(tc.psum_pool(name="psum_f", bufs=2))
 
             rcp_g = hold.tile([P, PB, P], F32)
             p_g = [hold.tile([P, TAPS, P], F32, name="p_g%d" % pb) for pb in range(PB)]
@@ -279,7 +279,8 @@ def tile_involution_w_kernel(
                 nc.gpsimd.tensor_tensor(out=places[1], in0=p_view, in1=places[0], op=ALU.subtract)
 
             def turn_bank(a, k):
-                part, u = divmod(k, 4)
+                part = k // 4
+                u = 2 * (k % 2) + (k // 2) % 2
                 if k == 0:
                     banded_of[a] = turn.tile([P, QS, 2, GH, PAIR], BF16, name="banded")
                 w_turned = psum_w.tile([P, 8, P], BF16, name="w_turned")
@@ -349,7 +350,8 @@ def tile_involution_w_kernel(
                     for k in range(8):
                         if 0 <= step - 5 < N_PAIRS:
                             turn_bank(step - 5, k)
-                        if k % 2 == 1 and 0 <= step - 6 < N_PAIRS:
-                            multiply_bank(step - 6, k // 2)
                         if k % 2 == 0 and 0 <= step - 7 < N_PAIRS:
                             store_bank(step - 7, k // 2)
+                    if 0 <= step - 6 < N_PAIRS:
+                        for qb in range(QS // 16):
+                            multiply_bank(step - 6, qb)

@@ -39,6 +39,8 @@ QS = G // GH
 BAND_PITCH = 136
 BAND_START = 32
 BAND_LEN = BAND_START + PAIR * BAND_PITCH + 8
+LATE_GROUPS = 16
+TAP_PITCH = 52
 
 FLOPS = 2 * C * R * PIX + 2 * R * O * PIX + 2 * TAPS * C * PIX
 
@@ -85,6 +87,10 @@ def tile_involution_w_kernel(
         make_identity(nc, ident_bf[:])
         ident_f32 = keep.tile([P, P], F32)
         make_identity(nc, ident_f32[:])
+        perm_bf = keep.tile([P, P], BF16)
+        nc.vector.tensor_copy(
+            out=perm_bf[:].rearrange("k (q f) -> k q f", f=GH), in_=ident_bf[:].rearrange("k (f q) -> k q f", f=GH)
+        )
         edge = keep.tile([P, KER, W], F32)
         nc.vector.memset(edge[:], 1.0)
         for w in range(PAD):
@@ -97,18 +103,31 @@ def tile_involution_w_kernel(
             in1=edge[:].unsqueeze(2).to_broadcast([P, KER, P // W, W]),
             op=ALU.mult,
         )
-        e_pix = [keep.tile([P, TAPS, G], F32, name="e_pix%d" % pb) for pb in range(PB)]
+        e_pix = [keep.tile([P, O], F32, name="e_pix%d" % pb) for pb in range(PB)]
         e_sum = [keep.tile([P, G], F32, name="e_sum%d" % pb) for pb in range(PB)]
         e_rcp = [keep.tile([P, G], F32, name="e_rcp%d" % pb) for pb in range(PB)]
+        z_max = [keep.tile([P, G], F32, name="z_max%d" % pb) for pb in range(PB)]
         x8 = keep.tile([P, N_PAIRS, QS, GH, CG], BF16)
         bands = [[keep.tile([P, BAND_LEN], BF16, name="band%d_%d" % (part, b)) for b in range(2)] for part in range(2)]
         for part in range(2):
             for b in range(2):
                 nc.gpsimd.memset(bands[part][b][:], 0.0)
 
+        def softmax_numerators(pb, g_lo, g_hi, shifted):
+            ready = e_pix[pb][:, g_lo * TAPS : g_hi * TAPS].rearrange("x (g t) -> x g t", t=TAPS)
+            nc.vector.tensor_reduce(out=z_max[pb][:, g_lo:g_hi], in_=ready, axis=AXIS.X, op=ALU.max)
+            nc.gpsimd.tensor_tensor(
+                out=shifted[:, : g_hi - g_lo, :],
+                in0=ready,
+                in1=z_max[pb][:, g_lo:g_hi].unsqueeze(2).to_broadcast([P, g_hi - g_lo, TAPS]),
+                op=ALU.subtract,
+            )
+            nc.scalar.activation(out=ready, in_=shifted[:, : g_hi - g_lo, :], func=ACT.Exp)
+            nc.vector.tensor_reduce(out=e_sum[pb][:, g_lo:g_hi], in_=ready, axis=AXIS.X, op=ALU.add)
+
         with ExitStack() as branch:
             front = branch.enter_context(tc.tile_pool(name="front", bufs=1))
-            ring = branch.enter_context(tc.tile_pool(name="ring", bufs=3))
+            ring = branch.enter_context(tc.tile_pool(name="ring", bufs=4))
             work = branch.enter_context(tc.tile_pool(name="work", bufs=2))
             psum_mx = branch.enter_context(tc.psum_pool(name="psum_mx", bufs=4))
 
@@ -125,6 +144,7 @@ def tile_involution_w_kernel(
                 w1_planes = early.tile([P, R], U8, align_bytes=64)
                 x_ch = early.tile([P, C // P, (PAD + H + PAD + 1) * W], BF16)
                 b1_bc = early.tile([P, R], BF16)
+                b1_sorted = early.tile([P, KG, PACK, P], BF16)
 
                 with tc.tile_pool(name="xq", bufs=1) as xq:
                     x_raw = xq.tile([P, KG, PACK * PIX], BF16)
@@ -146,7 +166,7 @@ def tile_involution_w_kernel(
                     out=x_ch[:, :, PAD * W : (PAD + H) * W], in_=x[0].rearrange("(b c) h w -> c b (h w)", c=P)
                 )
                 nc.scalar.dma_start(out=b1_bc[:], in_=b_reduce.partition_broadcast(P))
-                nc.scalar.dma_start(out=b2_bc[:], in_=b_span.partition_broadcast(P))
+                nc.vector.tensor_copy(out=b1_sorted[:], in_=b1_bc[:].rearrange("x (g p t) -> x g t p", p=P, t=PACK))
                 for a in range(N_PAIRS):
                     for f in range(GH):
                         x_turned = psum_tr.tile([P, 8, P], BF16, name="x_turned")
@@ -167,15 +187,15 @@ def tile_involution_w_kernel(
                         for pb in range(PB):
                             acc = psum_mx.tile([P, N_TILE], F32, name="acc")
                             mx_product(nc, acc[:], x_codes, x_planes, pb, wt, w1_planes, rt * N_TILE, N_TILE)
-                            pre = work.tile([P, N_TILE], F32, name="pre")
+                            pre = work.tile([P, PACK, P], F32, name="pre")
                             nc.vector.tensor_tensor(
-                                out=pre[:], in0=acc[:], in1=b1_bc[:, rt * N_TILE : (rt + 1) * N_TILE], op=ALU.add
+                                out=pre[:],
+                                in0=acc[:].rearrange("x (p t) -> x t p", t=PACK),
+                                in1=b1_sorted[:, rt, :, :],
+                                op=ALU.add,
                             )
-                            nc.scalar.activation(
-                                out=red_pix[pb][:, rt, :, :],
-                                in_=pre[:].rearrange("x (p t) -> x t p", t=PACK),
-                                func=ACT.Relu,
-                            )
+                            nc.scalar.activation(out=red_pix[pb][:, rt, :, :], in_=pre[:], func=ACT.Relu)
+                    nc.sync.dma_start(out=b2_bc[:], in_=b_span.partition_broadcast(P))
                     load_scale_planes(nc, w2_planes, w_span_scales)
                     for g in range(KG):
                         for pb in range(PB):
@@ -192,9 +212,8 @@ def tile_involution_w_kernel(
                             in_=red_grouped[:, g, :, :].rearrange("p x t -> p (x t)"),
                         )
 
-            late = branch.enter_context(tc.tile_pool(name="late", bufs=1))
-            z = [late.tile([P, O], F32, name="z%d" % pb) for pb in range(PB)]
-            z_max = [late.tile([P, G], F32, name="z_max%d" % pb) for pb in range(PB)]
+            shifts = branch.enter_context(tc.tile_pool(name="shifts", bufs=3))
+            most = N_TILE // TAPS + 1
             g_lo = 0
             for col0 in range(0, O, N_TILE):
                 ncols = min(N_TILE, O - col0)
@@ -204,51 +223,33 @@ def tile_involution_w_kernel(
                     acc = psum_mx.tile([P, N_TILE], F32, name="acc")
                     mx_product(nc, acc[:, :ncols], red_codes, red_planes, pb, wt, w2_planes, col0, ncols)
                     nc.vector.tensor_tensor(
-                        out=z[pb][:, col0 : col0 + ncols],
+                        out=e_pix[pb][:, col0 : col0 + ncols],
                         in0=acc[:, :ncols],
                         in1=b2_bc[:, col0 : col0 + ncols],
                         op=ALU.add,
                     )
-                    ready = z[pb][:, g_lo * TAPS : g_hi * TAPS]
-                    nc.vector.tensor_reduce(
-                        out=z_max[pb][:, g_lo:g_hi],
-                        in_=ready.rearrange("x (g t) -> x g t", t=TAPS),
-                        axis=AXIS.X,
-                        op=ALU.max,
-                    )
-                    nc.gpsimd.tensor_tensor(
-                        out=ready.rearrange("x (g t) -> x g t", t=TAPS),
-                        in0=ready.rearrange("x (g t) -> x g t", t=TAPS),
-                        in1=z_max[pb][:, g_lo:g_hi].unsqueeze(2).to_broadcast([P, g_hi - g_lo, TAPS]),
-                        op=ALU.subtract,
-                    )
-                    nc.scalar.activation(
-                        out=e_pix[pb][:, :, g_lo:g_hi],
-                        in_=ready.rearrange("x (g t) -> x t g", t=TAPS),
-                        func=ACT.Exp,
-                    )
-                    nc.vector.tensor_reduce(
-                        out=e_sum[pb][:, g_lo:g_hi],
-                        in_=e_pix[pb][:, :, g_lo:g_hi].rearrange("x t g -> x g t"),
-                        axis=AXIS.X,
-                        op=ALU.add,
-                    )
+                softmax_numerators(0, g_lo, g_hi, shifts.tile([P, most, TAPS], F32, name="shifted"))
                 g_lo = g_hi
-            for pb in range(PB):
-                nc.vector.reciprocal(out=e_rcp[pb][:], in_=e_sum[pb][:])
 
         with ExitStack() as taps:
             hold = taps.enter_context(tc.tile_pool(name="hold", bufs=1))
             turn = taps.enter_context(tc.tile_pool(name="turn", bufs=2))
             psum_w = taps.enter_context(tc.psum_pool(name="psum_w", bufs=3))
-            psum_mm = taps.enter_context(tc.psum_pool(name="psum_mm", bufs=3))
-            psum_f = taps.enter_context(tc.psum_pool(name="psum_f", bufs=2))
+            psum_mm = taps.enter_context(tc.psum_pool(name="psum_mm", bufs=2))
+            psum_f = taps.enter_context(tc.psum_pool(name="psum_f", bufs=3))
+            late_shifts = taps.enter_context(tc.tile_pool(name="late_shifts", bufs=2))
 
             rcp_g = hold.tile([P, PB, P], F32)
-            p_g = [hold.tile([P, TAPS, P], F32, name="p_g%d" % pb) for pb in range(PB)]
+            p_g = [hold.tile([P, P, TAP_PITCH], F32, name="p_g%d" % pb) for pb in range(PB)]
             banded_of = {}
             sums_of = {}
             result_of = {}
+
+            def reciprocal_of(pb):
+                nc.vector.reciprocal(out=e_rcp[pb][:], in_=e_sum[pb][:])
+                rcp_turned = psum_f.tile([P, 4, P], F32, name="turned")
+                nc.tensor.transpose(rcp_turned[:, 0, :], e_rcp[pb][:], ident_f32[:])
+                nc.vector.tensor_copy(out=rcp_g[:, pb, :], in_=rcp_turned[:, 0, :])
 
             def normalise(step):
                 pb, quarter = divmod(step, 4)
@@ -258,17 +259,21 @@ def tile_involution_w_kernel(
                     nt = min(4, last - tap0)
                     e_turned = psum_f.tile([P, 4, P], F32, name="turned")
                     for tap in range(tap0, tap0 + nt):
-                        nc.tensor.transpose(e_turned[:, tap - tap0, :], e_pix[pb][:, tap, :], ident_edge[:, tap % KER, :])
+                        nc.tensor.transpose(
+                            e_turned[:, tap - tap0, :],
+                            e_pix[pb][:].rearrange("x (g t) -> x g t", t=TAPS)[:, :, tap],
+                            ident_edge[:, tap % KER, :],
+                        )
                     nc.vector.tensor_tensor(
-                        out=p_g[pb][:, tap0 : tap0 + nt, :],
-                        in0=e_turned[:, :nt, :],
-                        in1=rcp_g[:, pb, :].unsqueeze(1).to_broadcast([P, nt, P]),
+                        out=p_g[pb][:, :, tap0 : tap0 + nt],
+                        in0=e_turned[:, :nt, :].rearrange("g t n -> g n t"),
+                        in1=rcp_g[:, pb, :].unsqueeze(2).to_broadcast([P, P, nt]),
                         op=ALU.mult,
                     )
 
             def split(a):
                 pb, a4 = divmod(a, PAIRS_PB)
-                p_view = p_g[pb][:, :, PAIR * a4 : PAIR * (a4 + 1)].rearrange("g (i j) n -> g n i j", j=KER)
+                p_view = p_g[pb][:, PAIR * a4 : PAIR * (a4 + 1), :TAPS].rearrange("g n (i j) -> g n i j", j=KER)
                 places = [
                     bands[part][a % 2][:, BAND_START : BAND_START + PAIR * BAND_PITCH]
                     .rearrange("g (n l) -> g n l", l=BAND_PITCH)[:, :, : KER * W]
@@ -279,20 +284,21 @@ def tile_involution_w_kernel(
                 nc.gpsimd.tensor_tensor(out=places[1], in0=p_view, in1=places[0], op=ALU.subtract)
 
             def turn_bank(a, k):
-                part = k // 4
-                u = 2 * (k % 2) + (k // 2) % 2
+                part, u = divmod(k, 4)
                 if k == 0:
-                    banded_of[a] = turn.tile([P, QS, 2, GH, PAIR], BF16, name="banded")
+                    banded_of[a] = turn.tile([P, QS, 2, PAIR, GH], BF16, name="banded")
                 w_turned = psum_w.tile([P, 8, P], BF16, name="w_turned")
                 for v in range(8):
                     n = 8 * u + v
                     first = BAND_START + BAND_PITCH * n - (n - PAD)
-                    nc.tensor.transpose(w_turned[:, v, :], bands[part][a % 2][:, first : first + P], ident_bf[:])
-                sorted_view = w_turned[:].rearrange("k v (f q) -> k q f v", f=GH)
-                if u < 2:
-                    nc.vector.tensor_copy(out=banded_of[a][:, :, part, :, 8 * u : 8 * u + 8], in_=sorted_view)
-                else:
-                    nc.scalar.copy(out=banded_of[a][:, :, part, :, 8 * u : 8 * u + 8], in_=sorted_view)
+                    nc.tensor.transpose(w_turned[:, v, :], bands[part][a % 2][:, first : first + P], perm_bf[:])
+                for half in range(2):
+                    sorted_view = w_turned[:, 4 * half : 4 * half + 4, :].rearrange("k v (q f) -> k q v f", f=GH)
+                    n0 = 8 * u + 4 * half
+                    if k % 2 == 0:
+                        nc.vector.tensor_copy(out=banded_of[a][:, :, part, n0 : n0 + 4, :], in_=sorted_view)
+                    else:
+                        nc.scalar.copy(out=banded_of[a][:, :, part, n0 : n0 + 4, :], in_=sorted_view)
 
             def multiply_bank(a, qb):
                 if qb == 0:
@@ -302,7 +308,7 @@ def tile_involution_w_kernel(
                     q = 16 * qb + q16
                     nc.tensor.matmul(
                         out=crossed[:, q16, :],
-                        lhsT=banded_of[a][:, q].rearrange("k s f n -> k (s f n)"),
+                        lhsT=banded_of[a][:, q].rearrange("k s n f -> k (s n f)"),
                         rhs=x8[:, a, q].rearrange("k f c -> k (f c)"),
                         start=True,
                         stop=True,
@@ -325,11 +331,11 @@ def tile_involution_w_kernel(
                         sums_of[a][:, f, 8 * t : 8 * t + 8, :].rearrange("k q c -> k (q c)"),
                         ident_f32[:],
                     )
-                parts = out_turned[:].rearrange("m t (s f n) -> m t s f n", s=2, f=GH)
+                parts = out_turned[:].rearrange("m t (s n f) -> m t s n f", s=2, f=GH)
                 lo_part = turn.tile([P, 4, PAIR], F32, name="lo_part")
-                nc.scalar.copy(out=lo_part[:], in_=parts[:, :, 1, f, :])
+                nc.scalar.copy(out=lo_part[:], in_=parts[:, :, 1, :, f])
                 nc.vector.tensor_tensor(
-                    out=result_of[a][:, f, 4 * th : 4 * th + 4, :], in0=parts[:, :, 0, f, :], in1=lo_part[:], op=ALU.add
+                    out=result_of[a][:, f, 4 * th : 4 * th + 4, :], in0=parts[:, :, 0, :, f], in1=lo_part[:], op=ALU.add
                 )
                 if k == 3:
                     nc.sync.dma_start(
@@ -337,21 +343,33 @@ def tile_involution_w_kernel(
                         in_=result_of[a][:].rearrange("m f t n -> m (f t) n"),
                     )
 
-            with tc.manual_schedule():
-                rcp_turned = psum_f.tile([P, 4, P], F32, name="turned")
-                for pb in range(PB):
-                    nc.tensor.transpose(rcp_turned[:, pb, :], e_rcp[pb][:], ident_f32[:])
-                nc.vector.tensor_copy(out=rcp_g[:], in_=rcp_turned[:, :PB, :])
-                for step in range(N_PAIRS + 7):
-                    if step < N_PAIRS:
-                        normalise(step)
-                    if 0 <= step - 4 < N_PAIRS:
-                        split(step - 4)
-                    for k in range(8):
-                        if 0 <= step - 5 < N_PAIRS:
-                            turn_bank(step - 5, k)
-                        if k % 2 == 0 and 0 <= step - 7 < N_PAIRS:
-                            store_bank(step - 7, k // 2)
-                    if 0 <= step - 6 < N_PAIRS:
-                        for qb in range(QS // 16):
-                            multiply_bank(step - 6, qb)
+            second_block = []
+            for part in range(G // LATE_GROUPS):
+                second_block.append(
+                    lambda part=part: softmax_numerators(
+                        1,
+                        LATE_GROUPS * part,
+                        LATE_GROUPS * (part + 1),
+                        late_shifts.tile([P, LATE_GROUPS, TAPS], F32, name="late_shifted"),
+                    )
+                )
+            second_block.append(lambda: reciprocal_of(1))
+            for quarter in range(4):
+                second_block.append(lambda quarter=quarter: normalise(4 + quarter))
+
+            reciprocal_of(0)
+            for quarter in range(4):
+                normalise(quarter)
+            pieces = (len(second_block) + PAIRS_PB - 1) // PAIRS_PB
+            for r in range(N_PAIRS + 3):
+                if r < N_PAIRS:
+                    split(r)
+                for k in range(8):
+                    if 0 <= r - 1 < N_PAIRS:
+                        turn_bank(r - 1, k)
+                    if k % 2 == 1 and 0 <= r - 2 < N_PAIRS:
+                        multiply_bank(r - 2, k // 2)
+                    if k % 2 == 0 and 0 <= r - 3 < N_PAIRS:
+                        store_bank(r - 3, k // 2)
+                for piece in second_block[pieces * r : pieces * (r + 1)]:
+                    piece()

@@ -87,9 +87,9 @@ def tile_involution_w_kernel(
         make_identity(nc, ident_bf[:])
         ident_f32 = keep.tile([P, P], F32)
         make_identity(nc, ident_f32[:])
-        perm_bf = keep.tile([P, P], BF16)
+        perm = keep.tile([P, P], F32)
         nc.vector.tensor_copy(
-            out=perm_bf[:].rearrange("k (q f) -> k q f", f=GH), in_=ident_bf[:].rearrange("k (f q) -> k q f", f=GH)
+            out=perm[:].rearrange("k (q f) -> k q f", f=GH), in_=ident_f32[:].rearrange("k (f q) -> k q f", f=GH)
         )
         edge = keep.tile([P, KER, W], F32)
         nc.vector.memset(edge[:], 1.0)
@@ -108,10 +108,9 @@ def tile_involution_w_kernel(
         e_rcp = [keep.tile([P, G], F32, name="e_rcp%d" % pb) for pb in range(PB)]
         z_max = [keep.tile([P, G], F32, name="z_max%d" % pb) for pb in range(PB)]
         x8 = keep.tile([P, N_PAIRS, QS, GH, CG], BF16)
-        bands = [[keep.tile([P, BAND_LEN], BF16, name="band%d_%d" % (part, b)) for b in range(2)] for part in range(2)]
-        for part in range(2):
-            for b in range(2):
-                nc.gpsimd.memset(bands[part][b][:], 0.0)
+        bands = [keep.tile([P, BAND_LEN], F32, name="band%d" % b) for b in range(2)]
+        for b in range(2):
+            nc.gpsimd.memset(bands[b][:], 0.0)
 
         def softmax_numerators(pb, g_lo, g_hi, shifted):
             ready = e_pix[pb][:, g_lo * TAPS : g_hi * TAPS].rearrange("x (g t) -> x g t", t=TAPS)
@@ -271,34 +270,29 @@ def tile_involution_w_kernel(
                         op=ALU.mult,
                     )
 
-            def split(a):
+            def spread(a):
                 pb, a4 = divmod(a, PAIRS_PB)
                 p_view = p_g[pb][:, PAIR * a4 : PAIR * (a4 + 1), :TAPS].rearrange("g n (i j) -> g n i j", j=KER)
-                places = [
-                    bands[part][a % 2][:, BAND_START : BAND_START + PAIR * BAND_PITCH]
+                places = (
+                    bands[a % 2][:, BAND_START : BAND_START + PAIR * BAND_PITCH]
                     .rearrange("g (n l) -> g n l", l=BAND_PITCH)[:, :, : KER * W]
                     .rearrange("g n (i w) -> g n i w", w=W)[:, :, :, :KER]
-                    for part in range(2)
-                ]
-                nc.scalar.copy(out=places[0], in_=p_view)
-                nc.gpsimd.tensor_tensor(out=places[1], in0=p_view, in1=places[0], op=ALU.subtract)
+                )
+                nc.gpsimd.tensor_scalar(out=places, in0=p_view, scalar1=1.0, scalar2=0.0, op0=ALU.mult, op1=ALU.add)
 
-            def turn_bank(a, k):
-                part, u = divmod(k, 4)
-                if k == 0:
+            def turn_bank(a, u):
+                if u == 0:
                     banded_of[a] = turn.tile([P, QS, 2, PAIR, GH], BF16, name="banded")
-                w_turned = psum_w.tile([P, 8, P], BF16, name="w_turned")
-                for v in range(8):
-                    n = 8 * u + v
+                w_turned = psum_w.tile([P, 4, P], F32, name="w_turned")
+                for v in range(4):
+                    n = 4 * u + v
                     first = BAND_START + BAND_PITCH * n - (n - PAD)
-                    nc.tensor.transpose(w_turned[:, v, :], bands[part][a % 2][:, first : first + P], perm_bf[:])
-                for half in range(2):
-                    sorted_view = w_turned[:, 4 * half : 4 * half + 4, :].rearrange("k v (q f) -> k q v f", f=GH)
-                    n0 = 8 * u + 4 * half
-                    if k % 2 == 0:
-                        nc.vector.tensor_copy(out=banded_of[a][:, :, part, n0 : n0 + 4, :], in_=sorted_view)
-                    else:
-                        nc.scalar.copy(out=banded_of[a][:, :, part, n0 : n0 + 4, :], in_=sorted_view)
+                    nc.tensor.transpose(w_turned[:, v, :], bands[a % 2][:, first : first + P], perm[:])
+                sorted_view = w_turned[:].rearrange("k v (q f) -> k q v f", f=GH)
+                hi = banded_of[a][:, :, 0, 4 * u : 4 * u + 4, :]
+                lo = banded_of[a][:, :, 1, 4 * u : 4 * u + 4, :]
+                nc.scalar.copy(out=hi, in_=sorted_view)
+                nc.vector.tensor_tensor(out=lo, in0=sorted_view, in1=hi, op=ALU.subtract)
 
             def multiply_bank(a, qb):
                 if qb == 0:
@@ -363,7 +357,7 @@ def tile_involution_w_kernel(
             pieces = (len(second_block) + PAIRS_PB - 1) // PAIRS_PB
             for r in range(N_PAIRS + 3):
                 if r < N_PAIRS:
-                    split(r)
+                    spread(r)
                 for k in range(8):
                     if 0 <= r - 1 < N_PAIRS:
                         turn_bank(r - 1, k)

@@ -40,7 +40,7 @@ BAND_PITCH = 136
 BAND_START = 32
 BAND_LEN = BAND_START + PAIR * BAND_PITCH + 8
 LATE_GROUPS = 16
-TAP_PITCH = 52
+TAP_PITCH = 56
 
 FLOPS = 2 * C * R * PIX + 2 * R * O * PIX + 2 * TAPS * C * PIX
 
@@ -90,6 +90,10 @@ def tile_involution_w_kernel(
         perm = keep.tile([P, P], F32)
         nc.vector.tensor_copy(
             out=perm[:].rearrange("k (q f) -> k q f", f=GH), in_=ident_f32[:].rearrange("k (f q) -> k q f", f=GH)
+        )
+        parity = keep.tile([P, GH], F32)
+        nc.vector.tensor_reduce(
+            out=parity[:], in_=ident_f32[:].rearrange("k (a b) -> k b a", b=GH), axis=AXIS.X, op=ALU.add
         )
         edge = keep.tile([P, KER, W], F32)
         nc.vector.memset(edge[:], 1.0)
@@ -239,7 +243,7 @@ def tile_involution_w_kernel(
             late_shifts = taps.enter_context(tc.tile_pool(name="late_shifts", bufs=2))
 
             rcp_g = hold.tile([P, PB, P], F32)
-            p_g = [hold.tile([P, P, TAP_PITCH], F32, name="p_g%d" % pb) for pb in range(PB)]
+            e_g = [hold.tile([P, P, TAP_PITCH], F32, name="e_g%d" % pb) for pb in range(PB)]
             banded_of = {}
             sums_of = {}
             result_of = {}
@@ -250,7 +254,7 @@ def tile_involution_w_kernel(
                 nc.tensor.transpose(rcp_turned[:, 0, :], e_rcp[pb][:], ident_f32[:])
                 nc.vector.tensor_copy(out=rcp_g[:, pb, :], in_=rcp_turned[:, 0, :])
 
-            def normalise(step):
+            def turn_e(step):
                 pb, quarter = divmod(step, 4)
                 first = 12 * quarter
                 last = TAPS if quarter == 3 else first + 12
@@ -263,22 +267,29 @@ def tile_involution_w_kernel(
                             e_pix[pb][:].rearrange("x (g t) -> x g t", t=TAPS)[:, :, tap],
                             ident_edge[:, tap % KER, :],
                         )
-                    nc.vector.tensor_tensor(
-                        out=p_g[pb][:, :, tap0 : tap0 + nt],
-                        in0=e_turned[:, :nt, :].rearrange("g t n -> g n t"),
-                        in1=rcp_g[:, pb, :].unsqueeze(2).to_broadcast([P, P, nt]),
-                        op=ALU.mult,
-                    )
+                    if (tap0 // 8) % 2 == 0:
+                        nc.vector.tensor_copy(
+                            out=e_g[pb][:, :, tap0 : tap0 + nt], in_=e_turned[:, :nt, :].rearrange("g t n -> g n t")
+                        )
+                    else:
+                        nc.scalar.copy(
+                            out=e_g[pb][:, :, tap0 : tap0 + nt], in_=e_turned[:, :nt, :].rearrange("g t n -> g n t")
+                        )
 
             def spread(a):
                 pb, a4 = divmod(a, PAIRS_PB)
-                p_view = p_g[pb][:, PAIR * a4 : PAIR * (a4 + 1), :TAPS].rearrange("g n (i j) -> g n i j", j=KER)
+                e_view = e_g[pb][:, PAIR * a4 : PAIR * (a4 + 1), :TAPS].rearrange("g n (i j) -> g n i j", j=KER)
                 places = (
                     bands[a % 2][:, BAND_START : BAND_START + PAIR * BAND_PITCH]
                     .rearrange("g (n l) -> g n l", l=BAND_PITCH)[:, :, : KER * W]
                     .rearrange("g n (i w) -> g n i w", w=W)[:, :, :, :KER]
                 )
-                nc.gpsimd.tensor_scalar(out=places, in0=p_view, scalar1=1.0, scalar2=0.0, op0=ALU.mult, op1=ALU.add)
+                nc.gpsimd.tensor_tensor(
+                    out=places,
+                    in0=e_view,
+                    in1=rcp_g[:, pb, PAIR * a4 : PAIR * (a4 + 1)].unsqueeze(2).unsqueeze(3).to_broadcast([P, PAIR, KER, KER]),
+                    op=ALU.mult,
+                )
 
             def turn_bank(a, u):
                 if u == 0:
@@ -296,7 +307,7 @@ def tile_involution_w_kernel(
 
             def multiply_bank(a, qb):
                 if qb == 0:
-                    sums_of[a] = turn.tile([P, GH, QS, CG], F32, name="sums")
+                    sums_of[a] = turn.tile([P, QS, CG], F32, name="sums")
                 crossed = psum_mm.tile([P, 16, GH * CG], F32, name="crossed")
                 for q16 in range(16):
                     q = 16 * qb + q16
@@ -308,30 +319,35 @@ def tile_involution_w_kernel(
                         stop=True,
                     )
                 crossed_view = crossed[:].rearrange("k q (f c) -> k f q c", f=GH)
-                if qb % 2 == 0:
-                    nc.vector.tensor_copy(out=sums_of[a][:, :, 16 * qb : 16 * qb + 16, :], in_=crossed_view)
-                else:
-                    nc.scalar.copy(out=sums_of[a][:, :, 16 * qb : 16 * qb + 16, :], in_=crossed_view)
+                odd_rows = turn.tile([P, 16, CG], F32, name="odd_rows")
+                nc.scalar.activation(out=odd_rows[:], in_=crossed_view[:, 1], func=ACT.Copy, scale=parity[:, 1:2])
+                nc.vector.scalar_tensor_tensor(
+                    out=sums_of[a][:, 16 * qb : 16 * qb + 16, :],
+                    in0=crossed_view[:, 0],
+                    scalar=parity[:, 0:1],
+                    in1=odd_rows[:],
+                    op0=ALU.mult,
+                    op1=ALU.add,
+                )
 
-            def store_bank(a, k):
-                f, th = divmod(k, 2)
-                if k == 0:
+            def store_bank(a, th):
+                if th == 0:
                     result_of[a] = turn.tile([P, GH, 8, PAIR], F32, name="result")
                 out_turned = psum_f.tile([P, 4, P], F32, name="turned")
                 for t4 in range(4):
                     t = 4 * th + t4
                     nc.tensor.transpose(
                         out_turned[:, t4, :],
-                        sums_of[a][:, f, 8 * t : 8 * t + 8, :].rearrange("k q c -> k (q c)"),
+                        sums_of[a][:, 8 * t : 8 * t + 8, :].rearrange("k q c -> k (q c)"),
                         ident_f32[:],
                     )
-                parts = out_turned[:].rearrange("m t (s n f) -> m t s n f", s=2, f=GH)
-                lo_part = turn.tile([P, 4, PAIR], F32, name="lo_part")
-                nc.scalar.copy(out=lo_part[:], in_=parts[:, :, 1, :, f])
+                parts = out_turned[:].rearrange("m t (s n f) -> m s f t n", s=2, f=GH)
+                lo_part = turn.tile([P, GH, 4, PAIR], F32, name="lo_part")
+                nc.scalar.copy(out=lo_part[:], in_=parts[:, 1])
                 nc.vector.tensor_tensor(
-                    out=result_of[a][:, f, 4 * th : 4 * th + 4, :], in0=parts[:, :, 0, :, f], in1=lo_part[:], op=ALU.add
+                    out=result_of[a][:, :, 4 * th : 4 * th + 4, :], in0=parts[:, 0], in1=lo_part[:], op=ALU.add
                 )
-                if k == 3:
+                if th == 1:
                     nc.sync.dma_start(
                         out=out[0].rearrange("(b m) h w -> m b (h w)", m=P)[:, :, PAIR * a : PAIR * (a + 1)],
                         in_=result_of[a][:].rearrange("m f t n -> m (f t) n"),
@@ -349,11 +365,11 @@ def tile_involution_w_kernel(
                 )
             second_block.append(lambda: reciprocal_of(1))
             for quarter in range(4):
-                second_block.append(lambda quarter=quarter: normalise(4 + quarter))
+                second_block.append(lambda quarter=quarter: turn_e(4 + quarter))
 
             reciprocal_of(0)
             for quarter in range(4):
-                normalise(quarter)
+                turn_e(quarter)
             pieces = (len(second_block) + PAIRS_PB - 1) // PAIRS_PB
             for r in range(N_PAIRS + 3):
                 if r < N_PAIRS:
@@ -363,7 +379,7 @@ def tile_involution_w_kernel(
                         turn_bank(r - 1, k)
                     if k % 2 == 1 and 0 <= r - 2 < N_PAIRS:
                         multiply_bank(r - 2, k // 2)
-                    if k % 2 == 0 and 0 <= r - 3 < N_PAIRS:
-                        store_bank(r - 3, k // 2)
+                    if k % 4 == 0 and 0 <= r - 3 < N_PAIRS:
+                        store_bank(r - 3, k // 4)
                 for piece in second_block[pieces * r : pieces * (r + 1)]:
                     piece()

@@ -39,7 +39,8 @@ QS = G // GH
 BAND_PITCH = 136
 BAND_START = 32
 BAND_LEN = BAND_START + PAIR * BAND_PITCH + 8
-LATE_GROUPS = 16
+WINDOWS = 4
+LATE_GROUPS = 8
 TAP_PITCH = 56
 
 FLOPS = 2 * C * R * PIX + 2 * R * O * PIX + 2 * TAPS * C * PIX
@@ -91,10 +92,6 @@ def tile_involution_w_kernel(
         nc.vector.tensor_copy(
             out=perm[:].rearrange("k (q f) -> k q f", f=GH), in_=ident_f32[:].rearrange("k (f q) -> k q f", f=GH)
         )
-        parity = keep.tile([P, GH], F32)
-        nc.vector.tensor_reduce(
-            out=parity[:], in_=ident_f32[:].rearrange("k (a b) -> k b a", b=GH), axis=AXIS.X, op=ALU.add
-        )
         edge = keep.tile([P, KER, W], F32)
         nc.vector.memset(edge[:], 1.0)
         for w in range(PAD):
@@ -111,7 +108,6 @@ def tile_involution_w_kernel(
         e_sum = [keep.tile([P, G], F32, name="e_sum%d" % pb) for pb in range(PB)]
         e_rcp = [keep.tile([P, G], F32, name="e_rcp%d" % pb) for pb in range(PB)]
         z_max = [keep.tile([P, G], F32, name="z_max%d" % pb) for pb in range(PB)]
-        x8 = keep.tile([P, N_PAIRS, QS, GH, CG], BF16)
         bands = [keep.tile([P, BAND_LEN], F32, name="band%d" % b) for b in range(2)]
         for b in range(2):
             nc.gpsimd.memset(bands[b][:], 0.0)
@@ -130,7 +126,7 @@ def tile_involution_w_kernel(
 
         with ExitStack() as branch:
             front = branch.enter_context(tc.tile_pool(name="front", bufs=1))
-            ring = branch.enter_context(tc.tile_pool(name="ring", bufs=4))
+            ring = branch.enter_context(tc.tile_pool(name="ring", bufs=6))
             work = branch.enter_context(tc.tile_pool(name="work", bufs=2))
             psum_mx = branch.enter_context(tc.psum_pool(name="psum_mx", bufs=4))
 
@@ -145,7 +141,6 @@ def tile_involution_w_kernel(
                 early = reduce_scope.enter_context(tc.tile_pool(name="early", bufs=1))
                 psum_tr = reduce_scope.enter_context(tc.psum_pool(name="psum_tr", bufs=2))
                 w1_planes = early.tile([P, R], U8, align_bytes=64)
-                x_ch = early.tile([P, C // P, (PAD + H + PAD + 1) * W], BF16)
                 b1_bc = early.tile([P, R], BF16)
                 b1_sorted = early.tile([P, KG, PACK, P], BF16)
 
@@ -163,24 +158,8 @@ def tile_involution_w_kernel(
                     )
                 load_scale_planes(nc, w1_planes, w_reduce_scales)
 
-                nc.vector.memset(x_ch[:, :, : PAD * W], 0.0)
-                nc.vector.memset(x_ch[:, :, (PAD + H) * W :], 0.0)
-                nc.scalar.dma_start(
-                    out=x_ch[:, :, PAD * W : (PAD + H) * W], in_=x[0].rearrange("(b c) h w -> c b (h w)", c=P)
-                )
                 nc.scalar.dma_start(out=b1_bc[:], in_=b_reduce.partition_broadcast(P))
                 nc.vector.tensor_copy(out=b1_sorted[:], in_=b1_bc[:].rearrange("x (g p t) -> x g t p", p=P, t=PACK))
-                for a in range(N_PAIRS):
-                    for f in range(GH):
-                        x_turned = psum_tr.tile([P, 8, P], BF16, name="x_turned")
-                        for u in range(8):
-                            nc.tensor.transpose(
-                                x_turned[:, u, :], x_ch[:, 8 * f + u, PAIR * a : PAIR * a + P], ident_bf[:]
-                            )
-                        nc.scalar.copy(
-                            out=x8[:, a, :, f, :],
-                            in_=x_turned[:].rearrange("k u m -> k (u m)").rearrange("k (q c) -> k q c", c=CG),
-                        )
 
                 with tc.tile_pool(name="redq", bufs=1) as redq:
                     red_pix = [redq.tile([P, KG, PACK, P], BF16, name="red_pix%d" % pb) for pb in range(PB)]
@@ -243,12 +222,32 @@ def tile_involution_w_kernel(
             late_shifts = taps.enter_context(tc.tile_pool(name="late_shifts", bufs=2))
 
             rcp_g = hold.tile([P, PB, P], F32)
-            e_g = [hold.tile([P, P, TAP_PITCH], F32, name="e_g%d" % pb) for pb in range(PB)]
+            e_g = {0: hold.tile([P, P, TAP_PITCH], F32, name="e_g0")}
+
+            x_ch = hold.tile([P, C // P, (PAD + H + PAD + 1) * W], BF16, tag="x_ch_then_e_g1")
+            nc.vector.memset(x_ch[:, :, : PAD * W], 0.0)
+            nc.vector.memset(x_ch[:, :, (PAD + H) * W :], 0.0)
+            nc.sync.dma_start(out=x_ch[:, :, PAD * W : (PAD + H) * W], in_=x[0].rearrange("(b c) h w -> c b (h w)", c=P))
+            x8 = hold.tile([P, N_PAIRS, QS, GH, CG], BF16)
+
+            def turn_x(a):
+                for f in range(GH):
+                    x_turned = psum_w.tile([P, 8, P], BF16, name="x_turned", tag="w_turned")
+                    for u in range(8):
+                        nc.tensor.transpose(x_turned[:, u, :], x_ch[:, 8 * f + u, PAIR * a : PAIR * a + P], ident_bf[:])
+                    x_view = x_turned[:].rearrange("k u m -> k (u m)").rearrange("k (q c) -> k q c", c=CG)
+                    if f == 0:
+                        nc.scalar.copy(out=x8[:, a, :, f, :], in_=x_view)
+                    else:
+                        nc.vector.tensor_copy(out=x8[:, a, :, f, :], in_=x_view)
+
             banded_of = {}
             sums_of = {}
             result_of = {}
 
             def reciprocal_of(pb):
+                if pb not in e_g:
+                    e_g[pb] = hold.tile([P, P, TAP_PITCH], F32, name="e_g1", tag="x_ch_then_e_g1")
                 nc.vector.reciprocal(out=e_rcp[pb][:], in_=e_sum[pb][:])
                 rcp_turned = psum_f.tile([P, 4, P], F32, name="turned")
                 nc.tensor.transpose(rcp_turned[:, 0, :], e_rcp[pb][:], ident_f32[:])
@@ -307,7 +306,7 @@ def tile_involution_w_kernel(
 
             def multiply_bank(a, qb):
                 if qb == 0:
-                    sums_of[a] = turn.tile([P, QS, CG], F32, name="sums")
+                    sums_of[a] = turn.tile([P, GH, QS, CG], F32, name="sums")
                 crossed = psum_mm.tile([P, 16, GH * CG], F32, name="crossed")
                 for q16 in range(16):
                     q = 16 * qb + q16
@@ -319,35 +318,30 @@ def tile_involution_w_kernel(
                         stop=True,
                     )
                 crossed_view = crossed[:].rearrange("k q (f c) -> k f q c", f=GH)
-                odd_rows = turn.tile([P, 16, CG], F32, name="odd_rows")
-                nc.scalar.activation(out=odd_rows[:], in_=crossed_view[:, 1], func=ACT.Copy, scale=parity[:, 1:2])
-                nc.vector.scalar_tensor_tensor(
-                    out=sums_of[a][:, 16 * qb : 16 * qb + 16, :],
-                    in0=crossed_view[:, 0],
-                    scalar=parity[:, 0:1],
-                    in1=odd_rows[:],
-                    op0=ALU.mult,
-                    op1=ALU.add,
-                )
+                if qb % 2 == 0:
+                    nc.vector.tensor_copy(out=sums_of[a][:, :, 16 * qb : 16 * qb + 16, :], in_=crossed_view)
+                else:
+                    nc.scalar.copy(out=sums_of[a][:, :, 16 * qb : 16 * qb + 16, :], in_=crossed_view)
 
-            def store_bank(a, th):
-                if th == 0:
+            def store_bank(a, k):
+                f, th = divmod(k, 2)
+                if k == 0:
                     result_of[a] = turn.tile([P, GH, 8, PAIR], F32, name="result")
                 out_turned = psum_f.tile([P, 4, P], F32, name="turned")
                 for t4 in range(4):
                     t = 4 * th + t4
                     nc.tensor.transpose(
                         out_turned[:, t4, :],
-                        sums_of[a][:, 8 * t : 8 * t + 8, :].rearrange("k q c -> k (q c)"),
+                        sums_of[a][:, f, 8 * t : 8 * t + 8, :].rearrange("k q c -> k (q c)"),
                         ident_f32[:],
                     )
-                parts = out_turned[:].rearrange("m t (s n f) -> m s f t n", s=2, f=GH)
-                lo_part = turn.tile([P, GH, 4, PAIR], F32, name="lo_part")
-                nc.scalar.copy(out=lo_part[:], in_=parts[:, 1])
+                parts = out_turned[:].rearrange("m t (s n f) -> m t s n f", s=2, f=GH)
+                lo_part = turn.tile([P, 4, PAIR], F32, name="lo_part")
+                nc.scalar.copy(out=lo_part[:], in_=parts[:, :, 1, :, f])
                 nc.vector.tensor_tensor(
-                    out=result_of[a][:, :, 4 * th : 4 * th + 4, :], in0=parts[:, 0], in1=lo_part[:], op=ALU.add
+                    out=result_of[a][:, f, 4 * th : 4 * th + 4, :], in0=parts[:, :, 0, :, f], in1=lo_part[:], op=ALU.add
                 )
-                if th == 1:
+                if k == 3:
                     nc.sync.dma_start(
                         out=out[0].rearrange("(b m) h w -> m b (h w)", m=P)[:, :, PAIR * a : PAIR * (a + 1)],
                         in_=result_of[a][:].rearrange("m f t n -> m (f t) n"),
@@ -374,12 +368,14 @@ def tile_involution_w_kernel(
             for r in range(N_PAIRS + 3):
                 if r < N_PAIRS:
                     spread(r)
+                for a in range(WINDOWS * r, min(WINDOWS * (r + 1), N_PAIRS)):
+                    turn_x(a)
                 for k in range(8):
                     if 0 <= r - 1 < N_PAIRS:
                         turn_bank(r - 1, k)
                     if k % 2 == 1 and 0 <= r - 2 < N_PAIRS:
                         multiply_bank(r - 2, k // 2)
-                    if k % 4 == 0 and 0 <= r - 3 < N_PAIRS:
-                        store_bank(r - 3, k // 4)
+                    if k % 2 == 0 and 0 <= r - 3 < N_PAIRS:
+                        store_bank(r - 3, k // 2)
                 for piece in second_block[pieces * r : pieces * (r + 1)]:
                     piece()

@@ -31,23 +31,28 @@ TAPS = KER * KER
 O = G * TAPS
 N_TILE = 512
 
+HALVES = 2
+GH = G // HALVES
+OH = GH * TAPS
+FQ = 2
+QS = GH // FQ
 PAIR = 2 * W
-N_PAIRS = PIX // PAIR
 PAIRS_PB = P // PAIR
-GH = 2
-QS = G // GH
-BAND_PITCH = 136
-BAND_START = 32
-BAND_LEN = BAND_START + PAIR * BAND_PITCH + 8
-WINDOWS = 4
-LATE_GROUPS = 8
-TAP_PITCH = 56
+N_PAIRS = PIX // PAIR
+ROUNDS = HALVES * PAIRS_PB
+CHB = C // HALVES // P
+
+BANDS = 3
+BAND_PITCH = 132
+BAND_START = 28
+BAND_LEN = BAND_START + W * BAND_PITCH + 4
+TAP_PITCH = 52
+SLAB = max(PB * OH, P * TAP_PITCH)
 
 FLOPS = 2 * C * R * PIX + 2 * R * O * PIX + 2 * TAPS * C * PIX
 
 
 def load_scale_planes(nc, planes, scales):
-    nc.vector.memset(planes[:].bitcast(I32), 0)
     for q in range(4):
         nc.sync.dma_start(
             out=planes[32 * q : 32 * q + 16, :].bitcast(I32),
@@ -55,13 +60,11 @@ def load_scale_planes(nc, planes, scales):
         )
 
 
-def load_weight_tile(nc, ring, words, col0, ncols):
-    wt = ring.tile([P, KG, PACK * N_TILE], U8, name="wt", align_bytes=64)
+def load_weight_tile(nc, wt, words, col0, ncols):
     nc.sync.dma_start(
         out=wt[:, :, : PACK * ncols].bitcast(I32),
         in_=words.rearrange("g p n t -> p g (n t)")[:, :, PACK * col0 : PACK * (col0 + ncols)].bitcast(I32),
     )
-    return wt
 
 
 def mx_product(nc, acc, codes, planes, pb, wt, w_planes, col0, ncols):
@@ -78,19 +81,40 @@ def mx_product(nc, acc, codes, planes, pb, wt, w_planes, col0, ncols):
         )
 
 
+def weave(first, second):
+    places = [((i + 0.5) / len(pieces), which, i) for which, pieces in enumerate((first, second)) for i in range(len(pieces))]
+    return [(first, second)[which][i] for at, which, i in sorted(places)]
+
+
 def tile_involution_w_kernel(
     tc, x, w_reduce_words, w_reduce_scales, b_reduce, w_span_words, w_span_scales, b_span, out
 ):
     nc = tc.nc
     with ExitStack() as whole:
         keep = whole.enter_context(tc.tile_pool(name="keep", bufs=1))
+        slabs = whole.enter_context(tc.tile_pool(name="slabs", bufs=3))
+        bands_pool = whole.enter_context(tc.tile_pool(name="bands_pool", bufs=1))
+        ring = whole.enter_context(tc.tile_pool(name="ring", bufs=3))
+        psum = whole.enter_context(tc.psum_pool(name="psum", bufs=2))
+        stream = whole.enter_context(tc.psum_pool(name="stream", bufs=4))
+        whole.enter_context(
+            tc.manual_schedule(
+                engines={mybir.EngineType.PE, mybir.EngineType.DVE, mybir.EngineType.Activation, mybir.EngineType.Pool}
+            )
+        )
+
+        w1_planes = keep.tile([P, R], U8, align_bytes=64)
+        nc.vector.memset(w1_planes[:].bitcast(I32), 0)
+        w2_planes = keep.tile([P, O], U8, align_bytes=64)
+        nc.vector.memset(w2_planes[:].bitcast(I32), 0)
         ident_bf = keep.tile([P, P], BF16)
         make_identity(nc, ident_bf[:])
         ident_f32 = keep.tile([P, P], F32)
         make_identity(nc, ident_f32[:])
         perm = keep.tile([P, P], F32)
         nc.vector.tensor_copy(
-            out=perm[:].rearrange("k (q f) -> k q f", f=GH), in_=ident_f32[:].rearrange("k (f q) -> k q f", f=GH)
+            out=perm[:].rearrange("k (b q f) -> k b q f", b=PB, f=FQ),
+            in_=ident_f32[:].rearrange("k (b f q) -> k b q f", b=PB, f=FQ),
         )
         edge = keep.tile([P, KER, W], F32)
         nc.vector.memset(edge[:], 1.0)
@@ -104,278 +128,346 @@ def tile_involution_w_kernel(
             in1=edge[:].unsqueeze(2).to_broadcast([P, KER, P // W, W]),
             op=ALU.mult,
         )
-        e_pix = [keep.tile([P, O], F32, name="e_pix%d" % pb) for pb in range(PB)]
-        e_sum = [keep.tile([P, G], F32, name="e_sum%d" % pb) for pb in range(PB)]
-        e_rcp = [keep.tile([P, G], F32, name="e_rcp%d" % pb) for pb in range(PB)]
-        z_max = [keep.tile([P, G], F32, name="z_max%d" % pb) for pb in range(PB)]
-        bands = [keep.tile([P, BAND_LEN], F32, name="band%d" % b) for b in range(2)]
-        for b in range(2):
+        z_max = [keep.tile([P, PB * GH], F32, name="z_max%d" % h) for h in range(HALVES)]
+        rcp_g = [keep.tile([P, P], F32, name="rcp_g%d" % h) for h in range(HALVES)]
+        x8 = keep.tile([P, N_PAIRS, HALVES, QS, FQ, CG], BF16)
+        red_codes = keep.tile([P, KG * PIX], U32, align_bytes=64)
+        red_planes = keep.tile([P, KG * PIX], U8, align_bytes=64)
+        b2_bc = keep.tile([P, O], BF16)
+
+
+        bands = [bands_pool.tile([P, BAND_LEN], F32, name="band%d" % b) for b in range(BANDS)]
+        for b in range(BANDS):
             nc.gpsimd.memset(bands[b][:], 0.0)
 
-        def softmax_numerators(pb, g_lo, g_hi, shifted):
-            ready = e_pix[pb][:, g_lo * TAPS : g_hi * TAPS].rearrange("x (g t) -> x g t", t=TAPS)
-            nc.vector.tensor_reduce(out=z_max[pb][:, g_lo:g_hi], in_=ready, axis=AXIS.X, op=ALU.max)
-            nc.gpsimd.tensor_tensor(
-                out=shifted[:, : g_hi - g_lo, :],
-                in0=ready,
-                in1=z_max[pb][:, g_lo:g_hi].unsqueeze(2).to_broadcast([P, g_hi - g_lo, TAPS]),
-                op=ALU.subtract,
-            )
-            nc.scalar.activation(out=ready, in_=shifted[:, : g_hi - g_lo, :], func=ACT.Exp)
-            nc.vector.tensor_reduce(out=e_sum[pb][:, g_lo:g_hi], in_=ready, axis=AXIS.X, op=ALU.add)
 
-        with ExitStack() as branch:
-            front = branch.enter_context(tc.tile_pool(name="front", bufs=1))
-            ring = branch.enter_context(tc.tile_pool(name="ring", bufs=6))
-            work = branch.enter_context(tc.tile_pool(name="work", bufs=2))
-            psum_mx = branch.enter_context(tc.psum_pool(name="psum_mx", bufs=4))
-
-            x_codes = front.tile([P, KG * PIX], U32, align_bytes=64)
-            x_planes = front.tile([P, KG * PIX], U8, align_bytes=64)
-            red_codes = front.tile([P, KG * PIX], U32, align_bytes=64)
-            red_planes = front.tile([P, KG * PIX], U8, align_bytes=64)
-            w2_planes = front.tile([P, O], U8, align_bytes=64)
-            b2_bc = front.tile([P, O], BF16)
+        with tc.tile_pool(name="x_pool", bufs=1) as x_pool:
+            x_ch = x_pool.tile([P, C // P, (PAD + H + PAD + 1) * W], BF16)
+            nc.gpsimd.memset(x_ch[:, :, : PAD * W], 0.0)
+            nc.gpsimd.memset(x_ch[:, :, (PAD + H) * W :], 0.0)
 
             with ExitStack() as reduce_scope:
                 early = reduce_scope.enter_context(tc.tile_pool(name="early", bufs=1))
-                psum_tr = reduce_scope.enter_context(tc.psum_pool(name="psum_tr", bufs=2))
-                w1_planes = early.tile([P, R], U8, align_bytes=64)
+                work = reduce_scope.enter_context(tc.tile_pool(name="work", bufs=2))
+                x_codes = early.tile([P, KG * PIX], U32, align_bytes=64)
+                x_planes = early.tile([P, KG * PIX], U8, align_bytes=64)
                 b1_bc = early.tile([P, R], BF16)
                 b1_sorted = early.tile([P, KG, PACK, P], BF16)
 
                 with tc.tile_pool(name="xq", bufs=1) as xq:
                     x_raw = xq.tile([P, KG, PACK * PIX], BF16)
-                    nc.sync.dma_start(
-                        out=x_raw[:], in_=x[0].rearrange("(g p t) h w -> p g (t h w)", g=KG, p=P, t=PACK)
-                    )
                     x_grouped = xq.tile([P, KG, PIX, PACK], BF16, align_bytes=64)
-                    nc.vector.tensor_copy(out=x_grouped[:], in_=x_raw[:].rearrange("p g (t x) -> p g x t", t=PACK))
-                    nc.vector.quantize_mx(
-                        out=x_codes[:].bitcast(FP8X4),
-                        scales=x_planes[:],
-                        in_=x_grouped[:].rearrange("p g x t -> p (g x t)"),
-                    )
-                load_scale_planes(nc, w1_planes, w_reduce_scales)
-
-                nc.scalar.dma_start(out=b1_bc[:], in_=b_reduce.partition_broadcast(P))
-                nc.vector.tensor_copy(out=b1_sorted[:], in_=b1_bc[:].rearrange("x (g p t) -> x g t p", p=P, t=PACK))
-
-                with tc.tile_pool(name="redq", bufs=1) as redq:
-                    red_pix = [redq.tile([P, KG, PACK, P], BF16, name="red_pix%d" % pb) for pb in range(PB)]
-                    red_grouped = redq.tile([P, KG, PIX, PACK], BF16, align_bytes=64)
+                    for g in range(KG):
+                        nc.sync.dma_start(
+                            out=x_raw[:, g, :],
+                            in_=x[0].rearrange("(g p t) h w -> g p (t h w)", g=KG, p=P, t=PACK)[g],
+                        )
+                    load_scale_planes(nc, w1_planes, w_reduce_scales)
+                    nc.scalar.dma_start(out=b1_bc[:], in_=b_reduce.partition_broadcast(P))
+                    w1_slabs = [
+                        slabs.tile([P, 3, KG, PACK * N_TILE], U8, name="w1_slab%d" % s, tag="slab", align_bytes=64)
+                        for s in range(2)
+                    ]
+                    w1_tiles = [w1_slabs[rt // 3][:, rt % 3, :, :] for rt in range(R // N_TILE)]
                     for rt in range(R // N_TILE):
-                        wt = load_weight_tile(nc, ring, w_reduce_words, rt * N_TILE, N_TILE)
-                        for pb in range(PB):
-                            acc = psum_mx.tile([P, N_TILE], F32, name="acc")
-                            mx_product(nc, acc[:], x_codes, x_planes, pb, wt, w1_planes, rt * N_TILE, N_TILE)
-                            pre = work.tile([P, PACK, P], F32, name="pre")
-                            nc.vector.tensor_tensor(
-                                out=pre[:],
-                                in0=acc[:].rearrange("x (p t) -> x t p", t=PACK),
-                                in1=b1_sorted[:, rt, :, :],
-                                op=ALU.add,
-                            )
-                            nc.scalar.activation(out=red_pix[pb][:, rt, :, :], in_=pre[:], func=ACT.Relu)
+                        load_weight_tile(nc, w1_tiles[rt], w_reduce_words, rt * N_TILE, N_TILE)
                     nc.sync.dma_start(out=b2_bc[:], in_=b_span.partition_broadcast(P))
                     load_scale_planes(nc, w2_planes, w_span_scales)
-                    for g in range(KG):
-                        for pb in range(PB):
-                            flipped = psum_tr.tile([P, PACK, P], BF16, name="flipped")
-                            for t in range(PACK):
-                                nc.tensor.transpose(flipped[:, t, :], red_pix[pb][:, g, t, :], ident_bf[:])
-                            nc.vector.tensor_copy(
-                                out=red_grouped[:, g, pb * P : (pb + 1) * P, :],
-                                in_=flipped[:].rearrange("p t x -> p x t"),
-                            )
-                        nc.vector.quantize_mx(
-                            out=red_codes[:, g * PIX : (g + 1) * PIX].bitcast(FP8X4),
-                            scales=red_planes[:, g * PIX : (g + 1) * PIX],
-                            in_=red_grouped[:, g, :, :].rearrange("p x t -> p (x t)"),
+                    nc.sync.dma_start(
+                        out=x_ch[:, :, PAD * W : (PAD + H) * W], in_=x[0].rearrange("(b c) h w -> c b (h w)", c=P)
+                    )
+
+                    def group_x(g):
+                        nc.vector.tensor_copy(
+                            out=x_grouped[:, g, :, :], in_=x_raw[:, g, :].rearrange("p (t x) -> p x t", t=PACK)
                         )
 
-            shifts = branch.enter_context(tc.tile_pool(name="shifts", bufs=3))
-            most = N_TILE // TAPS + 1
-            g_lo = 0
-            for col0 in range(0, O, N_TILE):
-                ncols = min(N_TILE, O - col0)
-                wt = load_weight_tile(nc, ring, w_span_words, col0, ncols)
-                g_hi = (col0 + ncols) // TAPS
-                for pb in range(PB):
-                    acc = psum_mx.tile([P, N_TILE], F32, name="acc")
-                    mx_product(nc, acc[:, :ncols], red_codes, red_planes, pb, wt, w2_planes, col0, ncols)
-                    nc.vector.tensor_tensor(
-                        out=e_pix[pb][:, col0 : col0 + ncols],
-                        in0=acc[:, :ncols],
-                        in1=b2_bc[:, col0 : col0 + ncols],
-                        op=ALU.add,
+                    def quantise_x(g):
+                        nc.vector.quantize_mx(
+                            out=x_codes[:, g * PIX : (g + 1) * PIX].bitcast(FP8X4),
+                            scales=x_planes[:, g * PIX : (g + 1) * PIX],
+                            in_=x_grouped[:, g, :, :].rearrange("p x t -> p (x t)"),
+                        )
+
+                    group_x(0)
+                    for g in range(1, KG):
+                        group_x(g)
+                        quantise_x(g - 1)
+                    quantise_x(KG - 1)
+                nc.scalar.copy(out=b1_sorted[:], in_=b1_bc[:].rearrange("x (g p t) -> x g t p", p=P, t=PACK))
+
+                redq = reduce_scope.enter_context(tc.tile_pool(name="redq", bufs=1))
+                red_pix = [redq.tile([P, KG, PACK, P], BF16, name="red_pix%d" % pb) for pb in range(PB)]
+                red_grouped = redq.tile([P, KG, PIX, PACK], BF16, align_bytes=64)
+
+                def red_tile(rt):
+                    for pb in range(PB):
+                        acc = stream.tile([P, N_TILE], F32, name="acc", tag="bank")
+                        mx_product(nc, acc[:], x_codes, x_planes, pb, w1_tiles[rt], w1_planes, rt * N_TILE, N_TILE)
+                        pre = work.tile([P, PACK, P], F32, name="pre")
+                        nc.vector.tensor_tensor(
+                            out=pre[:],
+                            in0=acc[:].rearrange("x (p t) -> x t p", t=PACK),
+                            in1=b1_sorted[:, rt, :, :],
+                            op=ALU.add,
+                        )
+                        nc.scalar.activation(out=red_pix[pb][:, rt, :, :], in_=pre[:], func=ACT.Relu)
+
+                def turn_red(g):
+                    for pb in range(PB):
+                        flipped = psum.tile([P, PACK, P], BF16, name="flipped", tag="turned")
+                        for t in range(PACK):
+                            nc.tensor.transpose(flipped[:, t, :], red_pix[pb][:, g, t, :], ident_bf[:])
+                        nc.scalar.copy(
+                            out=red_grouped[:, g, pb * P : (pb + 1) * P, :],
+                            in_=flipped[:].rearrange("p t x -> p x t"),
+                        )
+
+                def quantise_red(g):
+                    nc.vector.quantize_mx(
+                        out=red_codes[:, g * PIX : (g + 1) * PIX].bitcast(FP8X4),
+                        scales=red_planes[:, g * PIX : (g + 1) * PIX],
+                        in_=red_grouped[:, g, :, :].rearrange("p x t -> p (x t)"),
                     )
-                softmax_numerators(0, g_lo, g_hi, shifts.tile([P, most, TAPS], F32, name="shifted"))
-                g_lo = g_hi
 
-        with ExitStack() as taps:
-            hold = taps.enter_context(tc.tile_pool(name="hold", bufs=1))
-            turn = taps.enter_context(tc.tile_pool(name="turn", bufs=2))
-            psum_w = taps.enter_context(tc.psum_pool(name="psum_w", bufs=3))
-            psum_mm = taps.enter_context(tc.psum_pool(name="psum_mm", bufs=2))
-            psum_f = taps.enter_context(tc.psum_pool(name="psum_f", bufs=3))
-            late_shifts = taps.enter_context(tc.tile_pool(name="late_shifts", bufs=2))
+                for rt in range(KG + 2):
+                    if rt < KG:
+                        red_tile(rt)
+                    if 0 <= rt - 1 < KG:
+                        turn_red(rt - 1)
+                    if 0 <= rt - 2 < KG:
+                        quantise_red(rt - 2)
 
-            rcp_g = hold.tile([P, PB, P], F32)
-            e_g = {0: hold.tile([P, P, TAP_PITCH], F32, name="e_g0")}
+            numerators = [slabs.tile([P, SLAB], F32, name="numerators%d" % h, tag="slab", align_bytes=64) for h in range(HALVES)]
+            by_group = [
+                numerators[h][:, : PB * OH].rearrange("x (b g t) -> x b g t", b=PB, t=TAPS) for h in range(HALVES)
+            ]
+            tile_starts = list(range(0, O, N_TILE))
 
-            x_ch = hold.tile([P, C // P, (PAD + H + PAD + 1) * W], BF16, tag="x_ch_then_e_g1")
-            nc.vector.memset(x_ch[:, :, : PAD * W], 0.0)
-            nc.vector.memset(x_ch[:, :, (PAD + H) * W :], 0.0)
-            nc.sync.dma_start(out=x_ch[:, :, PAD * W : (PAD + H) * W], in_=x[0].rearrange("(b c) h w -> c b (h w)", c=P))
-            x8 = hold.tile([P, N_PAIRS, QS, GH, CG], BF16)
+            def whole_groups(i):
+                lo = tile_starts[i] // TAPS
+                hi = min(tile_starts[i] + N_TILE, O) // TAPS
+                parts = [(h, max(lo, GH * h) - GH * h, min(hi, GH * (h + 1)) - GH * h) for h in range(HALVES)]
+                return [(h, first, last) for h, first, last in parts if first < last]
+
+            w2_tiles = {}
+
+            def kern_block(i, pb):
+                col0 = tile_starts[i]
+                ncols = min(N_TILE, O - col0)
+                if pb == 0:
+                    w2_tiles[i] = ring.tile([P, KG, PACK * N_TILE], U8, name="wt", align_bytes=64)
+                    load_weight_tile(nc, w2_tiles[i], w_span_words, col0, ncols)
+                acc = stream.tile([P, N_TILE], F32, name="acc", tag="bank")
+                mx_product(nc, acc[:, :ncols], red_codes, red_planes, pb, w2_tiles[i], w2_planes, col0, ncols)
+                for h in range(HALVES):
+                    first = max(col0, OH * h)
+                    last = min(col0 + ncols, OH * (h + 1))
+                    if first < last:
+                        base = OH * (pb - h)
+                        nc.vector.tensor_tensor(
+                            out=numerators[h][:, base + first : base + last],
+                            in0=acc[:, first - col0 : last - col0],
+                            in1=b2_bc[:, first:last],
+                            op=ALU.add,
+                        )
+
+            def shift_tile(i, pb):
+                for h, first, last in whole_groups(i):
+                    ready = by_group[h][:, pb, first:last, :]
+                    top = z_max[h][:, GH * pb + first : GH * pb + last]
+                    nc.vector.tensor_reduce(out=top, in_=ready, axis=AXIS.X, op=ALU.max)
+                    nc.gpsimd.tensor_tensor(
+                        out=ready, in0=ready, in1=top.unsqueeze(2).to_broadcast([P, last - first, TAPS]), op=ALU.subtract
+                    )
+
+            def exp_tile(i, pb):
+                for h, first, last in whole_groups(i):
+                    ready = by_group[h][:, pb, first:last, :]
+                    nc.scalar.activation(out=ready, in_=ready, func=ACT.Exp)
 
             def turn_x(a):
-                for f in range(GH):
-                    x_turned = psum_w.tile([P, 8, P], BF16, name="x_turned", tag="w_turned")
-                    for u in range(8):
-                        nc.tensor.transpose(x_turned[:, u, :], x_ch[:, 8 * f + u, PAIR * a : PAIR * a + P], ident_bf[:])
-                    x_view = x_turned[:].rearrange("k u m -> k (u m)").rearrange("k (q c) -> k q c", c=CG)
-                    if f == 0:
-                        nc.scalar.copy(out=x8[:, a, :, f, :], in_=x_view)
-                    else:
-                        nc.vector.tensor_copy(out=x8[:, a, :, f, :], in_=x_view)
-
-            banded_of = {}
-            sums_of = {}
-            result_of = {}
-
-            def reciprocal_of(pb):
-                if pb not in e_g:
-                    e_g[pb] = hold.tile([P, P, TAP_PITCH], F32, name="e_g1", tag="x_ch_then_e_g1")
-                nc.vector.reciprocal(out=e_rcp[pb][:], in_=e_sum[pb][:])
-                rcp_turned = psum_f.tile([P, 4, P], F32, name="turned")
-                nc.tensor.transpose(rcp_turned[:, 0, :], e_rcp[pb][:], ident_f32[:])
-                nc.vector.tensor_copy(out=rcp_g[:, pb, :], in_=rcp_turned[:, 0, :])
-
-            def turn_e(step):
-                pb, quarter = divmod(step, 4)
-                first = 12 * quarter
-                last = TAPS if quarter == 3 else first + 12
-                for tap0 in range(first, last, 4):
-                    nt = min(4, last - tap0)
-                    e_turned = psum_f.tile([P, 4, P], F32, name="turned")
-                    for tap in range(tap0, tap0 + nt):
-                        nc.tensor.transpose(
-                            e_turned[:, tap - tap0, :],
-                            e_pix[pb][:].rearrange("x (g t) -> x g t", t=TAPS)[:, :, tap],
-                            ident_edge[:, tap % KER, :],
-                        )
-                    if (tap0 // 8) % 2 == 0:
-                        nc.vector.tensor_copy(
-                            out=e_g[pb][:, :, tap0 : tap0 + nt], in_=e_turned[:, :nt, :].rearrange("g t n -> g n t")
-                        )
-                    else:
-                        nc.scalar.copy(
-                            out=e_g[pb][:, :, tap0 : tap0 + nt], in_=e_turned[:, :nt, :].rearrange("g t n -> g n t")
-                        )
-
-            def spread(a):
-                pb, a4 = divmod(a, PAIRS_PB)
-                e_view = e_g[pb][:, PAIR * a4 : PAIR * (a4 + 1), :TAPS].rearrange("g n (i j) -> g n i j", j=KER)
-                places = (
-                    bands[a % 2][:, BAND_START : BAND_START + PAIR * BAND_PITCH]
-                    .rearrange("g (n l) -> g n l", l=BAND_PITCH)[:, :, : KER * W]
-                    .rearrange("g n (i w) -> g n i w", w=W)[:, :, :, :KER]
-                )
-                nc.gpsimd.tensor_tensor(
-                    out=places,
-                    in0=e_view,
-                    in1=rcp_g[:, pb, PAIR * a4 : PAIR * (a4 + 1)].unsqueeze(2).unsqueeze(3).to_broadcast([P, PAIR, KER, KER]),
-                    op=ALU.mult,
-                )
-
-            def turn_bank(a, u):
-                if u == 0:
-                    banded_of[a] = turn.tile([P, QS, 2, PAIR, GH], BF16, name="banded")
-                w_turned = psum_w.tile([P, 4, P], F32, name="w_turned")
-                for v in range(4):
-                    n = 4 * u + v
-                    first = BAND_START + BAND_PITCH * n - (n - PAD)
-                    nc.tensor.transpose(w_turned[:, v, :], bands[a % 2][:, first : first + P], perm[:])
-                sorted_view = w_turned[:].rearrange("k v (q f) -> k q v f", f=GH)
-                hi = banded_of[a][:, :, 0, 4 * u : 4 * u + 4, :]
-                lo = banded_of[a][:, :, 1, 4 * u : 4 * u + 4, :]
-                nc.scalar.copy(out=hi, in_=sorted_view)
-                nc.vector.tensor_tensor(out=lo, in0=sorted_view, in1=hi, op=ALU.subtract)
-
-            def multiply_bank(a, qb):
-                if qb == 0:
-                    sums_of[a] = turn.tile([P, GH, QS, CG], F32, name="sums")
-                crossed = psum_mm.tile([P, 16, GH * CG], F32, name="crossed")
-                for q16 in range(16):
-                    q = 16 * qb + q16
-                    nc.tensor.matmul(
-                        out=crossed[:, q16, :],
-                        lhsT=banded_of[a][:, q].rearrange("k s n f -> k (s n f)"),
-                        rhs=x8[:, a, q].rearrange("k f c -> k (f c)"),
-                        start=True,
-                        stop=True,
-                    )
-                crossed_view = crossed[:].rearrange("k q (f c) -> k f q c", f=GH)
-                if qb % 2 == 0:
-                    nc.vector.tensor_copy(out=sums_of[a][:, :, 16 * qb : 16 * qb + 16, :], in_=crossed_view)
-                else:
-                    nc.scalar.copy(out=sums_of[a][:, :, 16 * qb : 16 * qb + 16, :], in_=crossed_view)
-
-            def store_bank(a, k):
-                f, th = divmod(k, 2)
-                if k == 0:
-                    result_of[a] = turn.tile([P, GH, 8, PAIR], F32, name="result")
-                out_turned = psum_f.tile([P, 4, P], F32, name="turned")
-                for t4 in range(4):
-                    t = 4 * th + t4
-                    nc.tensor.transpose(
-                        out_turned[:, t4, :],
-                        sums_of[a][:, f, 8 * t : 8 * t + 8, :].rearrange("k q c -> k (q c)"),
-                        ident_f32[:],
-                    )
-                parts = out_turned[:].rearrange("m t (s n f) -> m t s n f", s=2, f=GH)
-                lo_part = turn.tile([P, 4, PAIR], F32, name="lo_part")
-                nc.scalar.copy(out=lo_part[:], in_=parts[:, :, 1, :, f])
-                nc.vector.tensor_tensor(
-                    out=result_of[a][:, f, 4 * th : 4 * th + 4, :], in0=parts[:, :, 0, :, f], in1=lo_part[:], op=ALU.add
-                )
-                if k == 3:
-                    nc.sync.dma_start(
-                        out=out[0].rearrange("(b m) h w -> m b (h w)", m=P)[:, :, PAIR * a : PAIR * (a + 1)],
-                        in_=result_of[a][:].rearrange("m f t n -> m (f t) n"),
+                for h in range(HALVES):
+                    x_turned = stream.tile([P, CHB, P], BF16, name="x_turned", tag="bank")
+                    for u in range(CHB):
+                        nc.tensor.transpose(x_turned[:, u, :], x_ch[:, CHB * h + u, PAIR * a : PAIR * a + P], ident_bf[:])
+                    nc.scalar.copy(
+                        out=x8[:, a, h].rearrange("k q f c -> k f q c"),
+                        in_=x_turned[:].rearrange("k u m -> k (u m)").rearrange("k (f q c) -> k f q c", f=FQ, c=CG),
                     )
 
-            second_block = []
-            for part in range(G // LATE_GROUPS):
-                second_block.append(
-                    lambda part=part: softmax_numerators(
-                        1,
-                        LATE_GROUPS * part,
-                        LATE_GROUPS * (part + 1),
-                        late_shifts.tile([P, LATE_GROUPS, TAPS], F32, name="late_shifted"),
-                    )
-                )
-            second_block.append(lambda: reciprocal_of(1))
-            for quarter in range(4):
-                second_block.append(lambda quarter=quarter: turn_e(4 + quarter))
+            first_tiles = -(-OH // N_TILE)
+            n_tiles = len(tile_starts)
+            windows = [a4 + PAIRS_PB * pb for a4 in range(PAIRS_PB) for pb in range(PB)]
+            for i in range(first_tiles + 1):
+                for pb in range(PB):
+                    kern_block(i, pb)
+                    shift_tile(i, pb)
+                    if i > 0:
+                        exp_tile(i - 1, pb)
+                if i > 1:
+                    turn_x(windows.pop(0))
+            while windows:
+                turn_x(windows.pop(0))
 
-            reciprocal_of(0)
-            for quarter in range(4):
-                turn_e(quarter)
-            pieces = (len(second_block) + PAIRS_PB - 1) // PAIRS_PB
-            for r in range(N_PAIRS + 3):
-                if r < N_PAIRS:
-                    spread(r)
-                for a in range(WINDOWS * r, min(WINDOWS * (r + 1), N_PAIRS)):
-                    turn_x(a)
-                for k in range(8):
-                    if 0 <= r - 1 < N_PAIRS:
-                        turn_bank(r - 1, k)
-                    if k % 2 == 1 and 0 <= r - 2 < N_PAIRS:
-                        multiply_bank(r - 2, k // 2)
-                    if k % 2 == 0 and 0 <= r - 3 < N_PAIRS:
-                        store_bank(r - 3, k // 2)
-                for piece in second_block[pieces * r : pieces * (r + 1)]:
-                    piece()
+        turn = whole.enter_context(tc.tile_pool(name="turn", bufs=2))
+        weights_of = {}
+        banded_of = {}
+        sum_of = {}
+        sums_of = {}
+        parts_of = {}
+
+        def add_taps(h, taps, tag):
+            if taps[0] == 0:
+                sum_of[h] = psum.tile([P, P], F32, name="tap_sum", tag=tag)
+            for tap in taps:
+                nc.tensor.matmul(
+                    out=sum_of[h][:],
+                    lhsT=numerators[h][:, : PB * OH].rearrange("x (m t) -> x m t", t=TAPS)[:, :, tap],
+                    rhs=ident_f32[:],
+                    start=(tap == 0),
+                    stop=(tap == TAPS - 1),
+                    is_transpose=True,
+                )
+
+        def reciprocal_of(h):
+            nc.vector.reciprocal(out=rcp_g[h][:], in_=sum_of[h][:])
+            weights_of[h] = slabs.tile([P, SLAB], F32, name="weights%d" % h, tag="slab", align_bytes=64)
+
+        def turn_weights(h, tap0):
+            nt = min(4, TAPS - tap0)
+            e_turned = stream.tile([P, 4, P], F32, name="e_turned", tag="bank")
+            for tap in range(tap0, tap0 + nt):
+                nc.tensor.transpose(
+                    e_turned[:, tap - tap0, :],
+                    numerators[h][:, : PB * OH].rearrange("x (m t) -> x m t", t=TAPS)[:, :, tap],
+                    ident_edge[:, tap % KER, :],
+                )
+            nc.vector.tensor_tensor(
+                out=weights_of[h][:, : P * TAP_PITCH].rearrange("g (n t) -> g n t", t=TAP_PITCH)[:, :, tap0 : tap0 + nt],
+                in0=e_turned[:, :nt, :].rearrange("g t n -> g n t"),
+                in1=rcp_g[h][:].unsqueeze(2).to_broadcast([P, P, nt]),
+                op=ALU.mult,
+            )
+
+        def spread(r, h2):
+            h, a4 = divmod(r, PAIRS_PB)
+            n0 = PAIR * a4 + W * h2
+            p_view = (
+                weights_of[h][:, : P * TAP_PITCH]
+                .rearrange("g (n t) -> g n t", t=TAP_PITCH)[:, n0 : n0 + W, :TAPS]
+                .rearrange("g n (i j) -> g n i j", j=KER)
+            )
+            places = (
+                bands[(2 * r + h2) % BANDS][:]
+                .bitcast(BF16)[:, 2 * BAND_START : 2 * (BAND_START + W * BAND_PITCH)]
+                .rearrange("g (n l) -> g n l", n=W)[:, :, : 2 * KER * W]
+                .rearrange("g n (i w s) -> g n i w s", w=W, s=2)
+            )
+            hi = places[:, :, :, :KER, 1]
+            if h2 == 0:
+                nc.scalar.copy(out=hi, in_=p_view)
+            else:
+                nc.gpsimd.tensor_scalar(out=hi, in0=p_view, scalar1=1.0, scalar2=0.0, op0=ALU.mult, op1=ALU.add)
+            nc.gpsimd.tensor_tensor(out=places[:, :, :, :KER, 0], in0=p_view, in1=hi, op=ALU.subtract)
+
+        def turn_bank(r, u):
+            if u == 0:
+                banded_of[r] = [turn.tile([P, GH, PAIR], F32, name="banded%d" % pb) for pb in range(PB)]
+            w_turned = stream.tile([P, 4, P], F32, name="w_turned", tag="bank")
+            for v in range(4):
+                n = 4 * u + v
+                h2, w = divmod(n, W)
+                first = BAND_START + BAND_PITCH * w - (n - PAD)
+                nc.tensor.transpose(w_turned[:, v, :], bands[(2 * r + h2) % BANDS][:, first : first + P], perm[:])
+            view = w_turned[:].rearrange("k v (b m) -> k b m v", b=PB)
+            for pb in range(PB):
+                copy = nc.scalar.copy if pb == 0 else nc.vector.tensor_copy
+                copy(out=banded_of[r][pb][:, :, 4 * u : 4 * u + 4], in_=view[:, pb])
+
+        def multiply_bank(r, k):
+            h, a4 = divmod(r, PAIRS_PB)
+            pb, qb = divmod(k, 2)
+            a = PAIRS_PB * pb + a4
+            if k == 0:
+                sums_of[r] = turn.tile([P, PB, QS, CG], F32, name="sums")
+            crossed = psum.tile([P, 16, FQ * CG], F32, name="crossed")
+            pairs = banded_of[r][pb][:].rearrange("k m n -> k (m n)").bitcast(BF16)
+            for q16 in range(16):
+                q = 16 * qb + q16
+                first = q * FQ * PAIR * 2
+                nc.tensor.matmul(
+                    out=crossed[:, q16, :],
+                    lhsT=pairs[:, first : first + P],
+                    rhs=x8[:, a, h, q].rearrange("k f c -> k (f c)"),
+                    start=True,
+                    stop=True,
+                )
+            copy = nc.vector.tensor_copy if qb == 0 else nc.scalar.copy
+            for f in range(FQ):
+                rows = slice(64 * f, 64 * (f + 1))
+                copy(out=sums_of[r][rows, pb, 16 * qb : 16 * qb + 16, :], in_=crossed[rows, :, CG * f : CG * (f + 1)])
+
+        def turn_sums(r, pb):
+            out_turned = psum.tile([P, 4, P], F32, name="out_turned", tag="turned")
+            for t in range(4):
+                nc.tensor.transpose(
+                    out_turned[:, t, :],
+                    sums_of[r][:, pb, 8 * t : 8 * t + 8, :].rearrange("k q c -> k (q c)"),
+                    ident_f32[:],
+                )
+            lo_part = turn.tile([P, FQ, 4, PAIR], F32, name="lo_part")
+            parts_of[r, pb] = out_turned[:].rearrange("m t (f n s) -> m f t n s", f=FQ, s=2), lo_part
+            nc.scalar.copy(out=lo_part[:], in_=parts_of[r, pb][0][:, :, :, :, 0])
+
+        def store_sums(r, pb):
+            h, a4 = divmod(r, PAIRS_PB)
+            parts, lo_part = parts_of[r, pb]
+            result = turn.tile([P, FQ, 4, PAIR], F32, name="result")
+            nc.vector.tensor_tensor(out=result[:], in0=parts[:, :, :, :, 1], in1=lo_part[:], op=ALU.add)
+            pix0 = P * pb + PAIR * a4
+            nc.sync.dma_start(
+                out=out[0].rearrange("(h k m) y x -> h m k (y x)", h=HALVES, m=P)[h][:, :, pix0 : pix0 + PAIR],
+                in_=result[:].rearrange("m f t n -> m (f t) n"),
+            )
+
+        def spread_step(r):
+            pieces = []
+            for k in range(8):
+                if r < ROUNDS and k in (0, 4):
+                    pieces.append(lambda k=k: spread(r, k // 4))
+                if 0 <= r - 1 < ROUNDS:
+                    pieces.append(lambda k=k: turn_bank(r - 1, k))
+                if k % 2 == 1 and 0 <= r - 2 < ROUNDS:
+                    pieces.append(lambda k=k: multiply_bank(r - 2, k // 2))
+                if k % 4 == 0 and 0 <= r - 3 < ROUNDS:
+                    pieces.append(lambda k=k: turn_sums(r - 3, k // 4))
+                if k % 4 == 2 and 0 <= r - 3 < ROUNDS:
+                    pieces.append(lambda k=k: store_sums(r - 3, k // 4))
+            return pieces
+
+        def weights_pieces(h, tag):
+            pieces = [lambda t=t: add_taps(h, range(t, t + 7), tag) for t in range(0, TAPS, 7)]
+            pieces.append(lambda: reciprocal_of(h))
+            return pieces + [lambda tap0=tap0: turn_weights(h, tap0) for tap0 in range(0, TAPS, 4)]
+
+        def tile_piece(i, pb):
+            kern_block(i, pb)
+            shift_tile(i, pb)
+            exp_tile(i - 1, pb)
+
+        tiles = [lambda i=i, pb=pb: tile_piece(i, pb) for i in range(first_tiles + 1, n_tiles) for pb in range(PB)]
+        for piece in weights_pieces(0, "crossed"):
+            piece()
+        early_rounds = [piece for r in range(PAIRS_PB - 2) for piece in spread_step(r)]
+        for piece in weave(tiles, early_rounds):
+            piece()
+        for pb in range(PB):
+            exp_tile(n_tiles - 1, pb)
+        for piece in spread_step(PAIRS_PB - 2):
+            piece()
+        for piece in weave(spread_step(PAIRS_PB - 1), weights_pieces(1, "crossed")):
+            piece()
+        for r in range(PAIRS_PB, ROUNDS + 3):
+            for piece in spread_step(r):
+                piece()

@@ -129,8 +129,14 @@ def tile_involution_w_kernel(
             op=ALU.mult,
         )
         z_max = [keep.tile([P, PB * GH], F32, name="z_max%d" % h) for h in range(HALVES)]
+        e_sum = [keep.tile([P, PB * GH], F32, name="e_sum%d" % h) for h in range(HALVES)]
+        e_rcp = [keep.tile([P, PB * GH], F32, name="e_rcp%d" % h) for h in range(HALVES)]
+        z_neg = [keep.tile([P, PB * GH], F32, name="z_neg%d" % h) for h in range(HALVES)]
         rcp_g = [keep.tile([P, P], F32, name="rcp_g%d" % h) for h in range(HALVES)]
         x8 = keep.tile([P, N_PAIRS, HALVES, QS, FQ, CG], BF16)
+        for a in range(N_PAIRS):
+            if PAIR * a < PAD * W or PAIR * a - PAD * W + P > PIX:
+                nc.gpsimd.memset(x8[:, a], 0.0)
         red_codes = keep.tile([P, KG * PIX], U32, align_bytes=64)
         red_planes = keep.tile([P, KG * PIX], U8, align_bytes=64)
         b2_bc = keep.tile([P, O], BF16)
@@ -141,197 +147,160 @@ def tile_involution_w_kernel(
             nc.gpsimd.memset(bands[b][:], 0.0)
 
 
-        with tc.tile_pool(name="x_pool", bufs=1) as x_pool:
-            x_ch = x_pool.tile([P, C // P, (PAD + H + PAD + 1) * W], BF16)
-            nc.gpsimd.memset(x_ch[:, :, : PAD * W], 0.0)
-            nc.gpsimd.memset(x_ch[:, :, (PAD + H) * W :], 0.0)
+        with ExitStack() as reduce_scope:
+            early = reduce_scope.enter_context(tc.tile_pool(name="early", bufs=1))
+            work = reduce_scope.enter_context(tc.tile_pool(name="work", bufs=2))
+            x_codes = early.tile([P, KG * PIX], U32, align_bytes=64)
+            x_planes = early.tile([P, KG * PIX], U8, align_bytes=64)
+            b1_bc = early.tile([P, R], BF16)
 
-            with ExitStack() as reduce_scope:
-                early = reduce_scope.enter_context(tc.tile_pool(name="early", bufs=1))
-                work = reduce_scope.enter_context(tc.tile_pool(name="work", bufs=2))
-                x_codes = early.tile([P, KG * PIX], U32, align_bytes=64)
-                x_planes = early.tile([P, KG * PIX], U8, align_bytes=64)
-                b1_bc = early.tile([P, R], BF16)
-                b1_sorted = early.tile([P, KG, PACK, P], BF16)
-
-                with tc.tile_pool(name="xq", bufs=1) as xq:
-                    x_raw = xq.tile([P, KG, PACK * PIX], BF16)
-                    x_grouped = xq.tile([P, KG, PIX, PACK], BF16, align_bytes=64)
-                    for g in range(KG):
-                        nc.sync.dma_start(
-                            out=x_raw[:, g, :],
-                            in_=x[0].rearrange("(g p t) h w -> g p (t h w)", g=KG, p=P, t=PACK)[g],
-                        )
-                    load_scale_planes(nc, w1_planes, w_reduce_scales)
-                    nc.scalar.dma_start(out=b1_bc[:], in_=b_reduce.partition_broadcast(P))
-                    w1_slabs = [
-                        slabs.tile([P, 3, KG, PACK * N_TILE], U8, name="w1_slab%d" % s, tag="slab", align_bytes=64)
-                        for s in range(2)
-                    ]
-                    w1_tiles = [w1_slabs[rt // 3][:, rt % 3, :, :] for rt in range(R // N_TILE)]
-                    for rt in range(R // N_TILE):
-                        load_weight_tile(nc, w1_tiles[rt], w_reduce_words, rt * N_TILE, N_TILE)
-                    nc.sync.dma_start(out=b2_bc[:], in_=b_span.partition_broadcast(P))
-                    load_scale_planes(nc, w2_planes, w_span_scales)
+            with tc.tile_pool(name="xq", bufs=1) as xq:
+                x_raw = xq.tile([P, KG, PACK * PIX], BF16)
+                x_grouped = xq.tile([P, KG, PIX, PACK], BF16, align_bytes=64)
+                for g in range(KG):
                     nc.sync.dma_start(
-                        out=x_ch[:, :, PAD * W : (PAD + H) * W], in_=x[0].rearrange("(b c) h w -> c b (h w)", c=P)
+                        out=x_raw[:, g, :],
+                        in_=x[0].rearrange("(g p t) h w -> g p (t h w)", g=KG, p=P, t=PACK)[g],
+                    )
+                load_scale_planes(nc, w1_planes, w_reduce_scales)
+                w1_slabs = [
+                    slabs.tile([P, 3, KG, PACK * N_TILE], U8, name="w1_slab%d" % s, tag="slab", align_bytes=64)
+                    for s in range(2)
+                ]
+                w1_tiles = [w1_slabs[rt // 3][:, rt % 3, :, :] for rt in range(R // N_TILE)]
+                for rt in range(R // N_TILE):
+                    load_weight_tile(nc, w1_tiles[rt], w_reduce_words, rt * N_TILE, N_TILE)
+                    if rt == 0:
+                        nc.scalar.dma_start(out=b1_bc[:], in_=b_reduce.partition_broadcast(P))
+                load_scale_planes(nc, w2_planes, w_span_scales)
+                nc.sync.dma_start(out=b2_bc[:, :OH], in_=b_span[:OH].partition_broadcast(P))
+
+                def group_x(g):
+                    nc.vector.tensor_copy(
+                        out=x_grouped[:, g, :, :], in_=x_raw[:, g, :].rearrange("p (t x) -> p x t", t=PACK)
                     )
 
-                    def group_x(g):
-                        nc.vector.tensor_copy(
-                            out=x_grouped[:, g, :, :], in_=x_raw[:, g, :].rearrange("p (t x) -> p x t", t=PACK)
-                        )
-
-                    def quantise_x(g):
-                        nc.vector.quantize_mx(
-                            out=x_codes[:, g * PIX : (g + 1) * PIX].bitcast(FP8X4),
-                            scales=x_planes[:, g * PIX : (g + 1) * PIX],
-                            in_=x_grouped[:, g, :, :].rearrange("p x t -> p (x t)"),
-                        )
-
-                    group_x(0)
-                    for g in range(1, KG):
-                        group_x(g)
-                        quantise_x(g - 1)
-                    quantise_x(KG - 1)
-                nc.scalar.copy(out=b1_sorted[:], in_=b1_bc[:].rearrange("x (g p t) -> x g t p", p=P, t=PACK))
-
-                redq = reduce_scope.enter_context(tc.tile_pool(name="redq", bufs=1))
-                red_pix = [redq.tile([P, KG, PACK, P], BF16, name="red_pix%d" % pb) for pb in range(PB)]
-                red_grouped = redq.tile([P, KG, PIX, PACK], BF16, align_bytes=64)
-
-                def red_tile(rt):
-                    for pb in range(PB):
-                        acc = stream.tile([P, N_TILE], F32, name="acc", tag="bank")
-                        mx_product(nc, acc[:], x_codes, x_planes, pb, w1_tiles[rt], w1_planes, rt * N_TILE, N_TILE)
-                        pre = work.tile([P, PACK, P], F32, name="pre")
-                        nc.vector.tensor_tensor(
-                            out=pre[:],
-                            in0=acc[:].rearrange("x (p t) -> x t p", t=PACK),
-                            in1=b1_sorted[:, rt, :, :],
-                            op=ALU.add,
-                        )
-                        nc.scalar.activation(out=red_pix[pb][:, rt, :, :], in_=pre[:], func=ACT.Relu)
-
-                def turn_red(g):
-                    for pb in range(PB):
-                        flipped = psum.tile([P, PACK, P], BF16, name="flipped", tag="turned")
-                        for t in range(PACK):
-                            nc.tensor.transpose(flipped[:, t, :], red_pix[pb][:, g, t, :], ident_bf[:])
-                        nc.scalar.copy(
-                            out=red_grouped[:, g, pb * P : (pb + 1) * P, :],
-                            in_=flipped[:].rearrange("p t x -> p x t"),
-                        )
-
-                def quantise_red(g):
+                def quantise_x(g):
                     nc.vector.quantize_mx(
-                        out=red_codes[:, g * PIX : (g + 1) * PIX].bitcast(FP8X4),
-                        scales=red_planes[:, g * PIX : (g + 1) * PIX],
-                        in_=red_grouped[:, g, :, :].rearrange("p x t -> p (x t)"),
+                        out=x_codes[:, g * PIX : (g + 1) * PIX].bitcast(FP8X4),
+                        scales=x_planes[:, g * PIX : (g + 1) * PIX],
+                        in_=x_grouped[:, g, :, :].rearrange("p x t -> p (x t)"),
                     )
 
-                for rt in range(KG + 2):
-                    if rt < KG:
-                        red_tile(rt)
-                    if 0 <= rt - 1 < KG:
-                        turn_red(rt - 1)
-                    if 0 <= rt - 2 < KG:
-                        quantise_red(rt - 2)
+                group_x(0)
+                for g in range(1, KG):
+                    group_x(g)
+                    quantise_x(g - 1)
+                quantise_x(KG - 1)
 
-            numerators = [slabs.tile([P, SLAB], F32, name="numerators%d" % h, tag="slab", align_bytes=64) for h in range(HALVES)]
-            by_group = [
-                numerators[h][:, : PB * OH].rearrange("x (b g t) -> x b g t", b=PB, t=TAPS) for h in range(HALVES)
-            ]
-            tile_starts = list(range(0, O, N_TILE))
+            redq = reduce_scope.enter_context(tc.tile_pool(name="redq", bufs=1))
+            red_pix = [redq.tile([P, KG, PACK, P], BF16, name="red_pix%d" % pb) for pb in range(PB)]
+            red_grouped = redq.tile([P, KG, PIX, PACK], BF16, align_bytes=64)
 
-            def whole_groups(i):
-                lo = tile_starts[i] // TAPS
-                hi = min(tile_starts[i] + N_TILE, O) // TAPS
-                parts = [(h, max(lo, GH * h) - GH * h, min(hi, GH * (h + 1)) - GH * h) for h in range(HALVES)]
-                return [(h, first, last) for h, first, last in parts if first < last]
-
-            w2_tiles = {}
-
-            def kern_block(i, pb):
-                col0 = tile_starts[i]
-                ncols = min(N_TILE, O - col0)
-                if pb == 0:
-                    w2_tiles[i] = ring.tile([P, KG, PACK * N_TILE], U8, name="wt", align_bytes=64)
-                    load_weight_tile(nc, w2_tiles[i], w_span_words, col0, ncols)
+            def red_block(rt, pb):
                 acc = stream.tile([P, N_TILE], F32, name="acc", tag="bank")
-                mx_product(nc, acc[:, :ncols], red_codes, red_planes, pb, w2_tiles[i], w2_planes, col0, ncols)
-                for h in range(HALVES):
-                    first = max(col0, OH * h)
-                    last = min(col0 + ncols, OH * (h + 1))
-                    if first < last:
-                        base = OH * (pb - h)
-                        nc.vector.tensor_tensor(
-                            out=numerators[h][:, base + first : base + last],
-                            in0=acc[:, first - col0 : last - col0],
-                            in1=b2_bc[:, first:last],
-                            op=ALU.add,
-                        )
+                mx_product(nc, acc[:], x_codes, x_planes, pb, w1_tiles[rt], w1_planes, rt * N_TILE, N_TILE)
+                pre = work.tile([P, PACK, P], F32, name="pre")
+                nc.vector.tensor_tensor(
+                    out=pre[:],
+                    in0=acc[:].rearrange("x (p t) -> x t p", t=PACK),
+                    in1=b1_bc[:, rt * N_TILE : (rt + 1) * N_TILE].rearrange("x (p t) -> x t p", t=PACK),
+                    op=ALU.add,
+                )
+                nc.scalar.activation(out=red_pix[pb][:, rt, :, :], in_=pre[:], func=ACT.Relu)
 
-            def shift_tile(i, pb):
-                for h, first, last in whole_groups(i):
-                    ready = by_group[h][:, pb, first:last, :]
-                    top = z_max[h][:, GH * pb + first : GH * pb + last]
-                    nc.vector.tensor_reduce(out=top, in_=ready, axis=AXIS.X, op=ALU.max)
-                    nc.gpsimd.tensor_tensor(
-                        out=ready, in0=ready, in1=top.unsqueeze(2).to_broadcast([P, last - first, TAPS]), op=ALU.subtract
-                    )
-
-            def exp_tile(i, pb):
-                for h, first, last in whole_groups(i):
-                    ready = by_group[h][:, pb, first:last, :]
-                    nc.scalar.activation(out=ready, in_=ready, func=ACT.Exp)
-
-            def turn_x(a):
-                for h in range(HALVES):
-                    x_turned = stream.tile([P, CHB, P], BF16, name="x_turned", tag="bank")
-                    for u in range(CHB):
-                        nc.tensor.transpose(x_turned[:, u, :], x_ch[:, CHB * h + u, PAIR * a : PAIR * a + P], ident_bf[:])
-                    nc.scalar.copy(
-                        out=x8[:, a, h].rearrange("k q f c -> k f q c"),
-                        in_=x_turned[:].rearrange("k u m -> k (u m)").rearrange("k (f q c) -> k f q c", f=FQ, c=CG),
-                    )
-
-            first_tiles = -(-OH // N_TILE)
-            n_tiles = len(tile_starts)
-            windows = [a4 + PAIRS_PB * pb for a4 in range(PAIRS_PB) for pb in range(PB)]
-            for i in range(first_tiles + 1):
-                for pb in range(PB):
-                    kern_block(i, pb)
-                    shift_tile(i, pb)
-                    if i > 0:
-                        exp_tile(i - 1, pb)
-                if i > 1:
-                    turn_x(windows.pop(0))
-            while windows:
-                turn_x(windows.pop(0))
-
-        turn = whole.enter_context(tc.tile_pool(name="turn", bufs=2))
-        weights_of = {}
-        banded_of = {}
-        sum_of = {}
-        sums_of = {}
-        parts_of = {}
-
-        def add_taps(h, taps, tag):
-            if taps[0] == 0:
-                sum_of[h] = psum.tile([P, P], F32, name="tap_sum", tag=tag)
-            for tap in taps:
-                nc.tensor.matmul(
-                    out=sum_of[h][:],
-                    lhsT=numerators[h][:, : PB * OH].rearrange("x (m t) -> x m t", t=TAPS)[:, :, tap],
-                    rhs=ident_f32[:],
-                    start=(tap == 0),
-                    stop=(tap == TAPS - 1),
-                    is_transpose=True,
+            def turn_red(g, pb):
+                flipped = psum.tile([P, PACK, P], BF16, name="flipped", tag="turned")
+                for t in range(PACK):
+                    nc.tensor.transpose(flipped[:, t, :], red_pix[pb][:, g, t, :], ident_bf[:])
+                nc.scalar.copy(
+                    out=red_grouped[:, g, pb * P : (pb + 1) * P, :],
+                    in_=flipped[:].rearrange("p t x -> p x t"),
                 )
 
+            def quantise_red(g, pb):
+                cols = slice(g * PIX + pb * P, g * PIX + (pb + 1) * P)
+                nc.vector.quantize_mx(
+                    out=red_codes[:, cols].bitcast(FP8X4),
+                    scales=red_planes[:, cols],
+                    in_=red_grouped[:, g, pb * P : (pb + 1) * P, :].rearrange("p x t -> p (x t)"),
+                )
+
+            steps = [(rt, pb) for rt in range(KG) for pb in range(PB)]
+            for s in range(len(steps) + 3):
+                if s < len(steps):
+                    red_block(*steps[s])
+                if 0 <= s - 2 < len(steps):
+                    turn_red(*steps[s - 2])
+                if 0 <= s - 3 < len(steps):
+                    quantise_red(*steps[s - 3])
+
+        numerators = [slabs.tile([P, SLAB], F32, name="numerators%d" % h, tag="slab", align_bytes=64) for h in range(HALVES)]
+        by_group = [
+            numerators[h][:, : PB * OH].rearrange("x (b g t) -> x b g t", b=PB, t=TAPS) for h in range(HALVES)
+        ]
+        tile_starts = list(range(0, O, N_TILE))
+
+        def whole_groups(i):
+            lo = tile_starts[i] // TAPS
+            hi = min(tile_starts[i] + N_TILE, O) // TAPS
+            parts = [(h, max(lo, GH * h) - GH * h, min(hi, GH * (h + 1)) - GH * h) for h in range(HALVES)]
+            return [(h, first, last) for h, first, last in parts if first < last]
+
+        w2_tiles = {}
+
+        def load_tile(i):
+            w2_tiles[i] = ring.tile([P, KG, PACK * N_TILE], U8, name="wt", align_bytes=64)
+            load_weight_tile(nc, w2_tiles[i], w_span_words, tile_starts[i], min(N_TILE, O - tile_starts[i]))
+
+        def kern_block(i, pb):
+            col0 = tile_starts[i]
+            ncols = min(N_TILE, O - col0)
+            if pb == 0 and i + 2 < n_tiles:
+                load_tile(i + 2)
+            acc = stream.tile([P, N_TILE], F32, name="acc", tag="bank")
+            mx_product(nc, acc[:, :ncols], red_codes, red_planes, pb, w2_tiles[i], w2_planes, col0, ncols)
+            for h in range(HALVES):
+                first = max(col0, OH * h)
+                last = min(col0 + ncols, OH * (h + 1))
+                if first < last:
+                    base = OH * (pb - h)
+                    nc.vector.tensor_tensor(
+                        out=numerators[h][:, base + first : base + last],
+                        in0=acc[:, first - col0 : last - col0],
+                        in1=b2_bc[:, first:last],
+                        op=ALU.add,
+                    )
+
+        def max_tile(i, pb):
+            for h, first, last in whole_groups(i):
+                cols = slice(GH * pb + first, GH * pb + last)
+                nc.vector.tensor_reduce(
+                    out=z_max[h][:, cols], in_=by_group[h][:, pb, first:last, :], axis=AXIS.X, op=ALU.max
+                )
+                nc.gpsimd.tensor_scalar(
+                    out=z_neg[h][:, cols], in0=z_max[h][:, cols], scalar1=-1.0, scalar2=0.0, op0=ALU.mult, op1=ALU.add
+                )
+
+        def exp_tile(i, pb):
+            for h, first, last in whole_groups(i):
+                for g in range(first, last):
+                    ready = by_group[h][:, pb, g, :]
+                    col = GH * pb + g
+                    nc.scalar.activation(
+                        out=ready, in_=ready, func=ACT.Exp, bias=z_neg[h][:, col : col + 1], accum_out=e_sum[h][:, col : col + 1]
+                    )
+
+        weights_of = {}
+        banded_of = {}
+        sums_of = {}
+        turned_of = {}
+
         def reciprocal_of(h):
-            nc.vector.reciprocal(out=rcp_g[h][:], in_=sum_of[h][:])
+            nc.vector.reciprocal(out=e_rcp[h][:], in_=e_sum[h][:])
+            rcp_turned = psum.tile([P, 4, P], F32, name="rcp_turned", tag="turned")
+            nc.tensor.transpose(rcp_turned[:, 0, :], e_rcp[h][:], ident_f32[:])
+            nc.vector.tensor_copy(out=rcp_g[h][:], in_=rcp_turned[:, 0, :])
             weights_of[h] = slabs.tile([P, SLAB], F32, name="weights%d" % h, tag="slab", align_bytes=64)
 
         def turn_weights(h, tap0):
@@ -366,24 +335,21 @@ def tile_involution_w_kernel(
             )
             hi = places[:, :, :, :KER, 1]
             if h2 == 0:
-                nc.scalar.copy(out=hi, in_=p_view)
+                nc.vector.tensor_copy(out=hi, in_=p_view)
             else:
                 nc.gpsimd.tensor_scalar(out=hi, in0=p_view, scalar1=1.0, scalar2=0.0, op0=ALU.mult, op1=ALU.add)
             nc.gpsimd.tensor_tensor(out=places[:, :, :, :KER, 0], in0=p_view, in1=hi, op=ALU.subtract)
 
         def turn_bank(r, u):
             if u == 0:
-                banded_of[r] = [turn.tile([P, GH, PAIR], F32, name="banded%d" % pb) for pb in range(PB)]
+                banded_of[r] = turn.tile([P, P, PAIR], F32, name="banded")
             w_turned = stream.tile([P, 4, P], F32, name="w_turned", tag="bank")
             for v in range(4):
                 n = 4 * u + v
                 h2, w = divmod(n, W)
                 first = BAND_START + BAND_PITCH * w - (n - PAD)
                 nc.tensor.transpose(w_turned[:, v, :], bands[(2 * r + h2) % BANDS][:, first : first + P], perm[:])
-            view = w_turned[:].rearrange("k v (b m) -> k b m v", b=PB)
-            for pb in range(PB):
-                copy = nc.scalar.copy if pb == 0 else nc.vector.tensor_copy
-                copy(out=banded_of[r][pb][:, :, 4 * u : 4 * u + 4], in_=view[:, pb])
+            nc.scalar.copy(out=banded_of[r][:, :, 4 * u : 4 * u + 4], in_=w_turned[:].rearrange("k v m -> k m v"))
 
         def multiply_bank(r, k):
             h, a4 = divmod(r, PAIRS_PB)
@@ -392,10 +358,10 @@ def tile_involution_w_kernel(
             if k == 0:
                 sums_of[r] = turn.tile([P, PB, QS, CG], F32, name="sums")
             crossed = psum.tile([P, 16, FQ * CG], F32, name="crossed")
-            pairs = banded_of[r][pb][:].rearrange("k m n -> k (m n)").bitcast(BF16)
+            pairs = banded_of[r][:].rearrange("k m n -> k (m n)").bitcast(BF16)
             for q16 in range(16):
                 q = 16 * qb + q16
-                first = q * FQ * PAIR * 2
+                first = (QS * pb + q) * FQ * PAIR * 2
                 nc.tensor.matmul(
                     out=crossed[:, q16, :],
                     lhsT=pairs[:, first : first + P],
@@ -403,28 +369,25 @@ def tile_involution_w_kernel(
                     start=True,
                     stop=True,
                 )
-            copy = nc.vector.tensor_copy if qb == 0 else nc.scalar.copy
             for f in range(FQ):
                 rows = slice(64 * f, 64 * (f + 1))
-                copy(out=sums_of[r][rows, pb, 16 * qb : 16 * qb + 16, :], in_=crossed[rows, :, CG * f : CG * (f + 1)])
+                nc.vector.tensor_copy(out=sums_of[r][rows, pb, 16 * qb : 16 * qb + 16, :], in_=crossed[rows, :, CG * f : CG * (f + 1)])
 
         def turn_sums(r, pb):
-            out_turned = psum.tile([P, 4, P], F32, name="out_turned", tag="turned")
+            turned_of[r, pb] = psum.tile([P, 4, P], F32, name="out_turned", tag="turned")
             for t in range(4):
                 nc.tensor.transpose(
-                    out_turned[:, t, :],
+                    turned_of[r, pb][:, t, :],
                     sums_of[r][:, pb, 8 * t : 8 * t + 8, :].rearrange("k q c -> k (q c)"),
                     ident_f32[:],
                 )
-            lo_part = turn.tile([P, FQ, 4, PAIR], F32, name="lo_part")
-            parts_of[r, pb] = out_turned[:].rearrange("m t (f n s) -> m f t n s", f=FQ, s=2), lo_part
-            nc.scalar.copy(out=lo_part[:], in_=parts_of[r, pb][0][:, :, :, :, 0])
 
         def store_sums(r, pb):
             h, a4 = divmod(r, PAIRS_PB)
-            parts, lo_part = parts_of[r, pb]
+            parts = turned_of[r, pb][:].rearrange("m t (f n s) -> m f t n s", f=FQ, s=2)
             result = turn.tile([P, FQ, 4, PAIR], F32, name="result")
-            nc.vector.tensor_tensor(out=result[:], in0=parts[:, :, :, :, 1], in1=lo_part[:], op=ALU.add)
+            for f in range(FQ):
+                nc.vector.tensor_reduce(out=result[:, f], in_=parts[:, f], axis=AXIS.X, op=ALU.add)
             pix0 = P * pb + PAIR * a4
             nc.sync.dma_start(
                 out=out[0].rearrange("(h k m) y x -> h m k (y x)", h=HALVES, m=P)[h][:, :, pix0 : pix0 + PAIR],
@@ -446,28 +409,71 @@ def tile_involution_w_kernel(
                     pieces.append(lambda k=k: store_sums(r - 3, k // 4))
             return pieces
 
-        def weights_pieces(h, tag):
-            pieces = [lambda t=t: add_taps(h, range(t, t + 7), tag) for t in range(0, TAPS, 7)]
-            pieces.append(lambda: reciprocal_of(h))
-            return pieces + [lambda tap0=tap0: turn_weights(h, tap0) for tap0 in range(0, TAPS, 4)]
+        def weights_pieces(h):
+            return [lambda: reciprocal_of(h)] + [lambda tap0=tap0: turn_weights(h, tap0) for tap0 in range(0, TAPS, 4)]
 
         def tile_piece(i, pb):
             kern_block(i, pb)
-            shift_tile(i, pb)
+            max_tile(i, pb)
             exp_tile(i - 1, pb)
 
+        def run(pieces):
+            for piece in pieces:
+                piece()
+
+        first_tiles = -(-OH // N_TILE)
+        n_tiles = len(tile_starts)
         tiles = [lambda i=i, pb=pb: tile_piece(i, pb) for i in range(first_tiles + 1, n_tiles) for pb in range(PB)]
-        for piece in weights_pieces(0, "crossed"):
-            piece()
-        early_rounds = [piece for r in range(PAIRS_PB - 2) for piece in spread_step(r)]
-        for piece in weave(tiles, early_rounds):
-            piece()
+        half_0 = [piece for r in range(PAIRS_PB - 1) for piece in spread_step(r)]
+        between = spread_step(PAIRS_PB - 1)
+        half_1 = [piece for r in range(PAIRS_PB, ROUNDS + 3) for piece in spread_step(r)]
+
+        with tc.tile_pool(name="x_pool", bufs=1) as x_pool:
+            x_ch = x_pool.tile([P, C // P, PIX], BF16)
+            nc.sync.dma_start(out=x_ch[:], in_=x[0].rearrange("(b c) h w -> c b (h w)", c=P))
+            x_pix = [x_pool.tile([P, HALVES, QS, FQ, CG], BF16, name="x_pix%d" % pb) for pb in range(PB)]
+
+            def turn_x(pb, h):
+                x_turned = stream.tile([P, CHB, P], BF16, name="x_turned", tag="bank")
+                for u in range(CHB):
+                    nc.tensor.transpose(x_turned[:, u, :], x_ch[:, CHB * h + u, P * pb : P * (pb + 1)], ident_bf[:])
+                nc.scalar.copy(
+                    out=x_pix[pb][:, h].rearrange("k q f c -> k f q c"),
+                    in_=x_turned[:].rearrange("k u m -> k (u m)").rearrange("k (f q c) -> k f q c", f=FQ, c=CG),
+                )
+
+            def place_window(a):
+                low = PAIR * a - PAD * W
+                for pb in range(PB):
+                    first = max(low, P * pb)
+                    last = min(low + P, P * (pb + 1))
+                    if first < last:
+                        nc.sync.dma_start(
+                            out=x8[first - low : last - low, a].rearrange("k h q f c -> k (h q f c)"),
+                            in_=x_pix[pb][first - P * pb : last - P * pb].rearrange("k h q f c -> k (h q f c)"),
+                        )
+
+            turns = [(pb, h) for pb in range(PB) for h in range(HALVES)]
+            for i in range(2):
+                load_tile(i)
+            nc.sync.dma_start(out=b2_bc[:, OH:], in_=b_span[OH:].partition_broadcast(P))
+            for i in range(first_tiles + 1):
+                for pb in range(PB):
+                    kern_block(i, pb)
+                    max_tile(i, pb)
+                    if i > 0:
+                        exp_tile(i - 1, pb)
+                    if i > 1 and turns:
+                        turn_x(*turns.pop(0))
+            run(weave(weights_pieces(0), tiles[:PB]))
+            for a4 in range(PAIRS_PB):
+                for pb in range(PB):
+                    place_window(a4 + PAIRS_PB * pb)
+
+        turn = whole.enter_context(tc.tile_pool(name="turn", bufs=2))
+        run(weave(tiles[PB:], half_0))
         for pb in range(PB):
             exp_tile(n_tiles - 1, pb)
-        for piece in spread_step(PAIRS_PB - 2):
-            piece()
-        for piece in weave(spread_step(PAIRS_PB - 1), weights_pieces(1, "crossed")):
-            piece()
-        for r in range(PAIRS_PB, ROUNDS + 3):
-            for piece in spread_step(r):
-                piece()
+        run(between[:10])
+        run(weave(between[10:], weights_pieces(1)))
+        run(half_1)

@@ -95,7 +95,8 @@ def tile_involution_w_kernel(
         slabs = whole.enter_context(tc.tile_pool(name="slabs", bufs=3))
         bands_pool = whole.enter_context(tc.tile_pool(name="bands_pool", bufs=1))
         ring = whole.enter_context(tc.tile_pool(name="ring", bufs=3))
-        psum = whole.enter_context(tc.psum_pool(name="psum", bufs=2))
+        turned_pool = whole.enter_context(tc.psum_pool(name="turned_pool", bufs=1))
+        crossed_pool = whole.enter_context(tc.psum_pool(name="crossed_pool", bufs=3))
         stream = whole.enter_context(tc.psum_pool(name="stream", bufs=4))
         whole.enter_context(
             tc.manual_schedule(
@@ -210,7 +211,7 @@ def tile_involution_w_kernel(
                 nc.scalar.activation(out=red_pix[pb][:, rt, :, :], in_=pre[:], func=ACT.Relu)
 
             def turn_red(g, pb):
-                flipped = psum.tile([P, PACK, P], BF16, name="flipped", tag="turned")
+                flipped = stream.tile([P, PACK, P], BF16, name="flipped", tag="bank")
                 for t in range(PACK):
                     nc.tensor.transpose(flipped[:, t, :], red_pix[pb][:, g, t, :], ident_bf[:])
                 nc.scalar.copy(
@@ -294,11 +295,12 @@ def tile_involution_w_kernel(
         weights_of = {}
         banded_of = {}
         sums_of = {}
+        crossed_of = {}
         turned_of = {}
 
         def reciprocal_of(h):
             nc.vector.reciprocal(out=e_rcp[h][:], in_=e_sum[h][:])
-            rcp_turned = psum.tile([P, 4, P], F32, name="rcp_turned", tag="turned")
+            rcp_turned = turned_pool.tile([P, 4, P], F32, name="rcp_turned", tag="turned")
             nc.tensor.transpose(rcp_turned[:, 0, :], e_rcp[h][:], ident_f32[:])
             nc.vector.tensor_copy(out=rcp_g[h][:], in_=rcp_turned[:, 0, :])
             weights_of[h] = slabs.tile([P, SLAB], F32, name="weights%d" % h, tag="slab", align_bytes=64)
@@ -357,7 +359,8 @@ def tile_involution_w_kernel(
             a = PAIRS_PB * pb + a4
             if k == 0:
                 sums_of[r] = turn.tile([P, PB, QS, CG], F32, name="sums")
-            crossed = psum.tile([P, 16, FQ * CG], F32, name="crossed")
+            crossed = crossed_pool.tile([P, 16, FQ * CG], F32, name="crossed")
+            crossed_of[r, k] = crossed
             pairs = banded_of[r][:].rearrange("k m n -> k (m n)").bitcast(BF16)
             for q16 in range(16):
                 q = 16 * qb + q16
@@ -369,12 +372,16 @@ def tile_involution_w_kernel(
                     start=True,
                     stop=True,
                 )
-            for f in range(FQ):
-                rows = slice(64 * f, 64 * (f + 1))
-                nc.vector.tensor_copy(out=sums_of[r][rows, pb, 16 * qb : 16 * qb + 16, :], in_=crossed[rows, :, CG * f : CG * (f + 1)])
+            nc.vector.tensor_copy(out=sums_of[r][:, pb, 16 * qb : 16 * qb + 16, :], in_=crossed[:, :, CG:])
+
+        def settle_bank(r, k):
+            pb, qb = divmod(k, 2)
+            nc.vector.tensor_copy(
+                out=sums_of[r][: P // FQ, pb, 16 * qb : 16 * qb + 16, :], in_=crossed_of[r, k][: P // FQ, :, :CG]
+            )
 
         def turn_sums(r, pb):
-            turned_of[r, pb] = psum.tile([P, 4, P], F32, name="out_turned", tag="turned")
+            turned_of[r, pb] = turned_pool.tile([P, 4, P], F32, name="out_turned", tag="turned")
             for t in range(4):
                 nc.tensor.transpose(
                     turned_of[r, pb][:, t, :],
@@ -385,7 +392,7 @@ def tile_involution_w_kernel(
         def store_sums(r, pb):
             h, a4 = divmod(r, PAIRS_PB)
             parts = turned_of[r, pb][:].rearrange("m t (f n s) -> m f t n s", f=FQ, s=2)
-            result = turn.tile([P, FQ, 4, PAIR], F32, name="result")
+            result = results.tile([P, FQ, 4, PAIR], F32, name="result")
             for f in range(FQ):
                 nc.vector.tensor_reduce(out=result[:, f], in_=parts[:, f], axis=AXIS.X, op=ALU.add)
             pix0 = P * pb + PAIR * a4
@@ -403,6 +410,10 @@ def tile_involution_w_kernel(
                     pieces.append(lambda k=k: turn_bank(r - 1, k))
                 if k % 2 == 1 and 0 <= r - 2 < ROUNDS:
                     pieces.append(lambda k=k: multiply_bank(r - 2, k // 2))
+                if k % 2 == 1 and k > 1 and 0 <= r - 2 < ROUNDS:
+                    pieces.append(lambda k=k: settle_bank(r - 2, k // 2 - 1))
+                if k == 1 and 0 <= r - 3 < ROUNDS:
+                    pieces.append(lambda: settle_bank(r - 3, 3))
                 if k % 4 == 0 and 0 <= r - 3 < ROUNDS:
                     pieces.append(lambda k=k: turn_sums(r - 3, k // 4))
                 if k % 4 == 2 and 0 <= r - 3 < ROUNDS:
@@ -412,10 +423,13 @@ def tile_involution_w_kernel(
         def weights_pieces(h):
             return [lambda: reciprocal_of(h)] + [lambda tap0=tap0: turn_weights(h, tap0) for tap0 in range(0, TAPS, 4)]
 
-        def tile_piece(i, pb):
-            kern_block(i, pb)
-            max_tile(i, pb)
-            exp_tile(i - 1, pb)
+        def tile_piece(p):
+            if p < PB * n_tiles:
+                kern_block(*divmod(p, PB))
+            if 0 <= p - 1 < PB * n_tiles:
+                max_tile(*divmod(p - 1, PB))
+            if 0 <= p - 2 < PB * n_tiles:
+                exp_tile(*divmod(p - 2, PB))
 
         def run(pieces):
             for piece in pieces:
@@ -423,7 +437,7 @@ def tile_involution_w_kernel(
 
         first_tiles = -(-OH // N_TILE)
         n_tiles = len(tile_starts)
-        tiles = [lambda i=i, pb=pb: tile_piece(i, pb) for i in range(first_tiles + 1, n_tiles) for pb in range(PB)]
+        tiles = [lambda p=p: tile_piece(p) for p in range(PB * (first_tiles + 1), PB * n_tiles + 2)]
         half_0 = [piece for r in range(PAIRS_PB - 1) for piece in spread_step(r)]
         between = spread_step(PAIRS_PB - 1)
         half_1 = [piece for r in range(PAIRS_PB, ROUNDS + 3) for piece in spread_step(r)]
@@ -457,23 +471,18 @@ def tile_involution_w_kernel(
             for i in range(2):
                 load_tile(i)
             nc.sync.dma_start(out=b2_bc[:, OH:], in_=b_span[OH:].partition_broadcast(P))
-            for i in range(first_tiles + 1):
-                for pb in range(PB):
-                    kern_block(i, pb)
-                    max_tile(i, pb)
-                    if i > 0:
-                        exp_tile(i - 1, pb)
-                    if i > 1 and turns:
-                        turn_x(*turns.pop(0))
+            for p in range(PB * (first_tiles + 1)):
+                tile_piece(p)
+                if p >= 2 * PB and turns:
+                    turn_x(*turns.pop(0))
             run(weave(weights_pieces(0), tiles[:PB]))
             for a4 in range(PAIRS_PB):
                 for pb in range(PB):
                     place_window(a4 + PAIRS_PB * pb)
 
         turn = whole.enter_context(tc.tile_pool(name="turn", bufs=2))
+        results = whole.enter_context(tc.tile_pool(name="results", bufs=4))
         run(weave(tiles[PB:], half_0))
-        for pb in range(PB):
-            exp_tile(n_tiles - 1, pb)
         run(between[:10])
         run(weave(between[10:], weights_pieces(1)))
         run(half_1)

@@ -43,8 +43,8 @@ ROUNDS = HALVES * PAIRS_PB
 CHB = C // HALVES // P
 
 BANDS = 3
-BAND_PITCH = 132
-BAND_START = 28
+BAND_PITCH = 133
+BAND_START = 29
 BAND_LEN = BAND_START + W * BAND_PITCH + 4
 TAP_PITCH = 52
 SLAB = max(PB * OH, P * TAP_PITCH)
@@ -129,7 +129,6 @@ def tile_involution_w_kernel(
             in1=edge[:].unsqueeze(2).to_broadcast([P, KER, P // W, W]),
             op=ALU.mult,
         )
-        z_max = [keep.tile([P, PB * GH], F32, name="z_max%d" % h) for h in range(HALVES)]
         e_sum = [keep.tile([P, PB * GH], F32, name="e_sum%d" % h) for h in range(HALVES)]
         e_rcp = [keep.tile([P, PB * GH], F32, name="e_rcp%d" % h) for h in range(HALVES)]
         z_neg = [keep.tile([P, PB * GH], F32, name="z_neg%d" % h) for h in range(HALVES)]
@@ -257,8 +256,8 @@ def tile_involution_w_kernel(
         def kern_block(i, pb):
             col0 = tile_starts[i]
             ncols = min(N_TILE, O - col0)
-            if pb == 0 and i + 2 < n_tiles:
-                load_tile(i + 2)
+            if pb == 0 and i + 3 < n_tiles:
+                load_tile(i + 3)
             acc = stream.tile([P, N_TILE], F32, name="acc", tag="bank")
             mx_product(nc, acc[:, :ncols], red_codes, red_planes, pb, w2_tiles[i], w2_planes, col0, ncols)
             for h in range(HALVES):
@@ -277,10 +276,7 @@ def tile_involution_w_kernel(
             for h, first, last in whole_groups(i):
                 cols = slice(GH * pb + first, GH * pb + last)
                 nc.vector.tensor_reduce(
-                    out=z_max[h][:, cols], in_=by_group[h][:, pb, first:last, :], axis=AXIS.X, op=ALU.max
-                )
-                nc.gpsimd.tensor_scalar(
-                    out=z_neg[h][:, cols], in0=z_max[h][:, cols], scalar1=-1.0, scalar2=0.0, op0=ALU.mult, op1=ALU.add
+                    out=z_neg[h][:, cols], in_=by_group[h][:, pb, first:last, :], axis=AXIS.X, op=ALU.max, negate=True
                 )
 
         def exp_tile(i, pb):
@@ -298,8 +294,10 @@ def tile_involution_w_kernel(
         crossed_of = {}
         turned_of = {}
 
-        def reciprocal_of(h):
+        def invert_sums(h):
             nc.vector.reciprocal(out=e_rcp[h][:], in_=e_sum[h][:])
+
+        def turn_reciprocals(h):
             rcp_turned = turned_pool.tile([P, 4, P], F32, name="rcp_turned", tag="turned")
             nc.tensor.transpose(rcp_turned[:, 0, :], e_rcp[h][:], ident_f32[:])
             nc.vector.tensor_copy(out=rcp_g[h][:], in_=rcp_turned[:, 0, :])
@@ -376,7 +374,8 @@ def tile_involution_w_kernel(
 
         def settle_bank(r, k):
             pb, qb = divmod(k, 2)
-            nc.vector.tensor_copy(
+            copy = nc.scalar.copy if r >= ROUNDS - 1 else nc.vector.tensor_copy
+            copy(
                 out=sums_of[r][: P // FQ, pb, 16 * qb : 16 * qb + 16, :], in_=crossed_of[r, k][: P // FQ, :, :CG]
             )
 
@@ -421,7 +420,7 @@ def tile_involution_w_kernel(
             return pieces
 
         def weights_pieces(h):
-            return [lambda: reciprocal_of(h)] + [lambda tap0=tap0: turn_weights(h, tap0) for tap0 in range(0, TAPS, 4)]
+            return [lambda: turn_reciprocals(h)] + [lambda tap0=tap0: turn_weights(h, tap0) for tap0 in range(0, TAPS, 4)]
 
         def tile_piece(p):
             if p < PB * n_tiles:
@@ -437,14 +436,13 @@ def tile_involution_w_kernel(
 
         first_tiles = -(-OH // N_TILE)
         n_tiles = len(tile_starts)
-        tiles = [lambda p=p: tile_piece(p) for p in range(PB * (first_tiles + 1), PB * n_tiles + 2)]
-        half_0 = [piece for r in range(PAIRS_PB - 1) for piece in spread_step(r)]
+        tiles = [lambda p=p: tile_piece(p) for p in range(PB * (first_tiles + 2), PB * n_tiles + 2)]
+        half_0 = [piece for r in range(1, PAIRS_PB - 1) for piece in spread_step(r)]
         between = spread_step(PAIRS_PB - 1)
         half_1 = [piece for r in range(PAIRS_PB, ROUNDS + 3) for piece in spread_step(r)]
 
         with tc.tile_pool(name="x_pool", bufs=1) as x_pool:
             x_ch = x_pool.tile([P, C // P, PIX], BF16)
-            nc.sync.dma_start(out=x_ch[:], in_=x[0].rearrange("(b c) h w -> c b (h w)", c=P))
             x_pix = [x_pool.tile([P, HALVES, QS, FQ, CG], BF16, name="x_pix%d" % pb) for pb in range(PB)]
 
             def turn_x(pb, h):
@@ -468,12 +466,17 @@ def tile_involution_w_kernel(
                         )
 
             turns = [(pb, h) for pb in range(PB) for h in range(HALVES)]
-            for i in range(2):
+            for i in range(3):
                 load_tile(i)
-            nc.sync.dma_start(out=b2_bc[:, OH:], in_=b_span[OH:].partition_broadcast(P))
-            for p in range(PB * (first_tiles + 1)):
+            for p in range(PB * (first_tiles + 2)):
                 tile_piece(p)
-                if p >= 2 * PB and turns:
+                if p == PB:
+                    nc.sync.dma_start(out=x_ch[:], in_=x[0].rearrange("(b c) h w -> c b (h w)", c=P))
+                if p == 2 * PB:
+                    nc.sync.dma_start(out=b2_bc[:, OH:], in_=b_span[OH:].partition_broadcast(P))
+                if p == PB * (first_tiles + 1):
+                    invert_sums(0)
+                if p >= 5 * PB and turns:
                     turn_x(*turns.pop(0))
             run(weave(weights_pieces(0), tiles[:PB]))
             for a4 in range(PAIRS_PB):
@@ -482,7 +485,11 @@ def tile_involution_w_kernel(
 
         turn = whole.enter_context(tc.tile_pool(name="turn", bufs=2))
         results = whole.enter_context(tc.tile_pool(name="results", bufs=4))
-        run(weave(tiles[PB:], half_0))
-        run(between[:10])
+        run(spread_step(0))
+        run(tiles[PB : 2 * PB])
+        run(weave(tiles[2 * PB :], half_0))
+        run(between[:8])
+        invert_sums(1)
+        run(between[8:10])
         run(weave(between[10:], weights_pieces(1)))
         run(half_1)

@@ -36,6 +36,7 @@ GH = G // HALVES
 OH = GH * TAPS
 FQ = 2
 QS = GH // FQ
+QB = P // CG
 PAIR = 2 * W
 PAIRS_PB = P // PAIR
 N_PAIRS = PIX // PAIR
@@ -114,8 +115,7 @@ def tile_involution_w_kernel(
         make_identity(nc, ident_f32[:])
         perm = keep.tile([P, P], F32)
         nc.vector.tensor_copy(
-            out=perm[:].rearrange("k (b q f) -> k b q f", b=PB, f=FQ),
-            in_=ident_f32[:].rearrange("k (b f q) -> k b q f", b=PB, f=FQ),
+            out=perm[:].rearrange("k (m r f) -> k m f r", f=FQ, r=QB), in_=ident_f32[:].rearrange("k (m f r) -> k m f r", f=FQ, r=QB)
         )
         edge = keep.tile([P, KER, W], F32)
         nc.vector.memset(edge[:], 1.0)
@@ -374,8 +374,7 @@ def tile_involution_w_kernel(
 
         def settle_bank(r, k):
             pb, qb = divmod(k, 2)
-            copy = nc.scalar.copy if r >= ROUNDS - 1 else nc.vector.tensor_copy
-            copy(
+            nc.scalar.copy(
                 out=sums_of[r][: P // FQ, pb, 16 * qb : 16 * qb + 16, :], in_=crossed_of[r, k][: P // FQ, :, :CG]
             )
 
@@ -390,14 +389,17 @@ def tile_involution_w_kernel(
 
         def store_sums(r, pb):
             h, a4 = divmod(r, PAIRS_PB)
-            parts = turned_of[r, pb][:].rearrange("m t (f n s) -> m f t n s", f=FQ, s=2)
-            result = results.tile([P, FQ, 4, PAIR], F32, name="result")
-            for f in range(FQ):
-                nc.vector.tensor_reduce(out=result[:, f], in_=parts[:, f], axis=AXIS.X, op=ALU.add)
+            result = results.tile([P, CHB, PAIR], F32, name="result")
+            nc.vector.tensor_reduce(
+                out=result[:].rearrange("m k n -> m (k n)"),
+                in_=turned_of[r, pb][:].rearrange("m t (u s) -> m (t u) s", s=2),
+                axis=AXIS.X,
+                op=ALU.add,
+            )
             pix0 = P * pb + PAIR * a4
             nc.sync.dma_start(
                 out=out[0].rearrange("(h k m) y x -> h m k (y x)", h=HALVES, m=P)[h][:, :, pix0 : pix0 + PAIR],
-                in_=result[:].rearrange("m f t n -> m (f t) n"),
+                in_=result[:],
             )
 
         def spread_step(r):
@@ -449,10 +451,11 @@ def tile_involution_w_kernel(
                 x_turned = stream.tile([P, CHB, P], BF16, name="x_turned", tag="bank")
                 for u in range(CHB):
                     nc.tensor.transpose(x_turned[:, u, :], x_ch[:, CHB * h + u, P * pb : P * (pb + 1)], ident_bf[:])
-                nc.scalar.copy(
-                    out=x_pix[pb][:, h].rearrange("k q f c -> k f q c"),
-                    in_=x_turned[:].rearrange("k u m -> k (u m)").rearrange("k (f q c) -> k f q c", f=FQ, c=CG),
-                )
+                for f in range(FQ):
+                    nc.scalar.copy(
+                        out=x_pix[pb][:, h, :, f, :].rearrange("k (t r) c -> k t r c", r=QB),
+                        in_=x_turned[:].rearrange("k (t f) (r c) -> k t f r c", f=FQ, c=CG)[:, :, f],
+                    )
 
             def place_window(a):
                 low = PAIR * a - PAD * W

from contextlib import ExitStack

import concourse.mybir as mybir
from concourse.masks import make_identity

F32 = mybir.dt.float32
BF16 = mybir.dt.bfloat16
U8 = mybir.dt.uint8
U32 = mybir.dt.uint32
I32 = mybir.dt.int32
FP8X4 = mybir.dt.float8_e4m3fn_x4
ALU = mybir.AluOpType
ACT = mybir.ActivationFunctionType
AXIS = mybir.AxisListType

P = 128
PACK = 4
K_PASS = P * PACK
C = 2048
R = 2048
KG = C // K_PASS
H = 16
W = 16
PIX = H * W
PB = PIX // P
G = 128
CG = C // G
KER = 7
PAD = KER // 2
TAPS = KER * KER
O = G * TAPS
N_TILE = 512

HALVES = 2
GH = G // HALVES
OH = GH * TAPS
FQ = 2
QS = GH // FQ
QB = P // CG
PAIR = 2 * W
PAIRS_PB = P // PAIR
N_PAIRS = PIX // PAIR
ROUNDS = HALVES * PAIRS_PB
CHB = C // HALVES // P

BANDS = 3
BAND_PITCH = 133
BAND_START = 29
BAND_LEN = BAND_START + W * BAND_PITCH + 4
TAP_PITCH = 52
SLAB = max(PB * OH, P * TAP_PITCH)

FLOPS = 2 * C * R * PIX + 2 * R * O * PIX + 2 * TAPS * C * PIX


def load_scale_planes(nc, planes, scales):
    for q in range(4):
        nc.sync.dma_start(
            out=planes[32 * q : 32 * q + 16, :].bitcast(I32),
            in_=scales[:, 4 * q : 4 * q + 4, :].bitcast(I32),
        )


def load_weight_tile(nc, wt, words, col0, ncols):
    nc.sync.dma_start(
        out=wt[:, :, : PACK * ncols].bitcast(I32),
        in_=words.rearrange("g p n t -> p g (n t)")[:, :, PACK * col0 : PACK * (col0 + ncols)].bitcast(I32),
    )


def mx_product(nc, acc, codes, planes, pb, wt, w_planes, col0, ncols):
    for g in range(KG):
        cols = slice(g * PIX + pb * P, g * PIX + (pb + 1) * P)
        nc.tensor.matmul_mx(
            out=acc,
            lhsT=codes[:, cols].bitcast(FP8X4),
            lhsT_scale=planes[:, cols],
            rhs=wt[:, g, : PACK * ncols].bitcast(FP8X4),
            rhs_scale=w_planes[4 * g : P, col0 : col0 + ncols],
            start=(g == 0),
            stop=(g == KG - 1),
        )


def weave(first, second):
    places = [((i + 0.5) / len(pieces), which, i) for which, pieces in enumerate((first, second)) for i in range(len(pieces))]
    return [(first, second)[which][i] for at, which, i in sorted(places)]


def tile_involution_w_kernel(
    tc, x, w_reduce_words, w_reduce_scales, b_reduce, w_span_words, w_span_scales, b_span, out
):
    nc = tc.nc
    with ExitStack() as whole:
        keep = whole.enter_context(tc.tile_pool(name="keep", bufs=1))
        slabs = whole.enter_context(tc.tile_pool(name="slabs", bufs=3))
        bands_pool = whole.enter_context(tc.tile_pool(name="bands_pool", bufs=1))
        ring = whole.enter_context(tc.tile_pool(name="ring", bufs=3))
        turned_pool = whole.enter_context(tc.psum_pool(name="turned_pool", bufs=1))
        crossed_pool = whole.enter_context(tc.psum_pool(name="crossed_pool", bufs=3))
        stream = whole.enter_context(tc.psum_pool(name="stream", bufs=4))
        whole.enter_context(
            tc.manual_schedule(
                engines={mybir.EngineType.PE, mybir.EngineType.DVE, mybir.EngineType.Activation, mybir.EngineType.Pool}
            )
        )

        w1_planes = keep.tile([P, R], U8, align_bytes=64)
        nc.vector.memset(w1_planes[:].bitcast(I32), 0)
        w2_planes = keep.tile([P, O], U8, align_bytes=64)
        nc.vector.memset(w2_planes[:].bitcast(I32), 0)
        ident_bf = keep.tile([P, P], BF16)
        make_identity(nc, ident_bf[:])
        ident_f32 = keep.tile([P, P], F32)
        make_identity(nc, ident_f32[:])
        perm = keep.tile([P, P], F32)
        nc.vector.tensor_copy(
            out=perm[:].rearrange("k (m r f) -> k m f r", f=FQ, r=QB), in_=ident_f32[:].rearrange("k (m f r) -> k m f r", f=FQ, r=QB)
        )
        edge = keep.tile([P, KER, W], F32)
        nc.vector.memset(edge[:], 1.0)
        for w in range(PAD):
            nc.vector.memset(edge[:, 0 : PAD - w, w : w + 1], 0.0)
            nc.vector.memset(edge[:, KER - PAD + w : KER, W - 1 - w : W - w], 0.0)
        ident_edge = keep.tile([P, KER, P], F32)
        nc.vector.tensor_tensor(
            out=ident_edge[:].rearrange("k j (h w) -> k j h w", w=W),
            in0=ident_f32[:].rearrange("k (h w) -> k h w", w=W).unsqueeze(1).to_broadcast([P, KER, P // W, W]),
            in1=edge[:].unsqueeze(2).to_broadcast([P, KER, P // W, W]),
            op=ALU.mult,
        )
        e_sum = [keep.tile([P, PB * GH], F32, name="e_sum%d" % h) for h in range(HALVES)]
        e_rcp = [keep.tile([P, PB * GH], F32, name="e_rcp%d" % h) for h in range(HALVES)]
        z_neg = [keep.tile([P, PB * GH], F32, name="z_neg%d" % h) for h in range(HALVES)]
        rcp_g = [keep.tile([P, P], F32, name="rcp_g%d" % h) for h in range(HALVES)]
        x8 = keep.tile([P, N_PAIRS, HALVES, QS, FQ, CG], BF16)
        for a in range(N_PAIRS):
            if PAIR * a < PAD * W or PAIR * a - PAD * W + P > PIX:
                nc.gpsimd.memset(x8[:, a], 0.0)
        red_codes = keep.tile([P, KG * PIX], U32, align_bytes=64)
        red_planes = keep.tile([P, KG * PIX], U8, align_bytes=64)
        b2_bc = keep.tile([P, O], BF16)


        bands = [bands_pool.tile([P, BAND_LEN], F32, name="band%d" % b) for b in range(BANDS)]
        for b in range(BANDS):
            nc.gpsimd.memset(bands[b][:], 0.0)


        with ExitStack() as reduce_scope:
            early = reduce_scope.enter_context(tc.tile_pool(name="early", bufs=1))
            work = reduce_scope.enter_context(tc.tile_pool(name="work", bufs=2))
            x_codes = early.tile([P, KG * PIX], U32, align_bytes=64)
            x_planes = early.tile([P, KG * PIX], U8, align_bytes=64)
            b1_bc = early.tile([P, R], BF16)

            with tc.tile_pool(name="xq", bufs=1) as xq:
                x_raw = xq.tile([P, KG, PACK * PIX], BF16)
                x_grouped = xq.tile([P, KG, PIX, PACK], BF16, align_bytes=64)
                for g in range(KG):
                    nc.sync.dma_start(
                        out=x_raw[:, g, :],
                        in_=x[0].rearrange("(g p t) h w -> g p (t h w)", g=KG, p=P, t=PACK)[g],
                    )
                load_scale_planes(nc, w1_planes, w_reduce_scales)
                w1_slabs = [
                    slabs.tile([P, 3, KG, PACK * N_TILE], U8, name="w1_slab%d" % s, tag="slab", align_bytes=64)
                    for s in range(2)
                ]
                w1_tiles = [w1_slabs[rt // 3][:, rt % 3, :, :] for rt in range(R // N_TILE)]
                for rt in range(R // N_TILE):
                    load_weight_tile(nc, w1_tiles[rt], w_reduce_words, rt * N_TILE, N_TILE)
                    if rt == 0:
                        nc.scalar.dma_start(out=b1_bc[:], in_=b_reduce.partition_broadcast(P))
                load_scale_planes(nc, w2_planes, w_span_scales)
                nc.sync.dma_start(out=b2_bc[:, :OH], in_=b_span[:OH].partition_broadcast(P))

                def group_x(g):
                    nc.vector.tensor_copy(
                        out=x_grouped[:, g, :, :], in_=x_raw[:, g, :].rearrange("p (t x) -> p x t", t=PACK)
                    )

                def quantise_x(g):
                    nc.vector.quantize_mx(
                        out=x_codes[:, g * PIX : (g + 1) * PIX].bitcast(FP8X4),
                        scales=x_planes[:, g * PIX : (g + 1) * PIX],
                        in_=x_grouped[:, g, :, :].rearrange("p x t -> p (x t)"),
                    )

                group_x(0)
                for g in range(1, KG):
                    group_x(g)
                    quantise_x(g - 1)
                quantise_x(KG - 1)

            redq = reduce_scope.enter_context(tc.tile_pool(name="redq", bufs=1))
            red_pix = [redq.tile([P, KG, PACK, P], BF16, name="red_pix%d" % pb) for pb in range(PB)]
            red_grouped = redq.tile([P, KG, PIX, PACK], BF16, align_bytes=64)

            def red_block(rt, pb):
                acc = stream.tile([P, N_TILE], F32, name="acc", tag="bank")
                mx_product(nc, acc[:], x_codes, x_planes, pb, w1_tiles[rt], w1_planes, rt * N_TILE, N_TILE)
                pre = work.tile([P, PACK, P], F32, name="pre")
                nc.vector.tensor_tensor(
                    out=pre[:],
                    in0=acc[:].rearrange("x (p t) -> x t p", t=PACK),
                    in1=b1_bc[:, rt * N_TILE : (rt + 1) * N_TILE].rearrange("x (p t) -> x t p", t=PACK),
                    op=ALU.add,
                )
                nc.scalar.activation(out=red_pix[pb][:, rt, :, :], in_=pre[:], func=ACT.Relu)

            def turn_red(g, pb):
                flipped = stream.tile([P, PACK, P], BF16, name="flipped", tag="bank")
                for t in range(PACK):
                    nc.tensor.transpose(flipped[:, t, :], red_pix[pb][:, g, t, :], ident_bf[:])
                nc.scalar.copy(
                    out=red_grouped[:, g, pb * P : (pb + 1) * P, :],
                    in_=flipped[:].rearrange("p t x -> p x t"),
                )

            def quantise_red(g, pb):
                cols = slice(g * PIX + pb * P, g * PIX + (pb + 1) * P)
                nc.vector.quantize_mx(
                    out=red_codes[:, cols].bitcast(FP8X4),
                    scales=red_planes[:, cols],
                    in_=red_grouped[:, g, pb * P : (pb + 1) * P, :].rearrange("p x t -> p (x t)"),
                )

            steps = [(rt, pb) for rt in range(KG) for pb in range(PB)]
            for s in range(len(steps) + 3):
                if s < len(steps):
                    red_block(*steps[s])
                if 0 <= s - 2 < len(steps):
                    turn_red(*steps[s - 2])
                if 0 <= s - 3 < len(steps):
                    quantise_red(*steps[s - 3])

        numerators = [slabs.tile([P, SLAB], F32, name="numerators%d" % h, tag="slab", align_bytes=64) for h in range(HALVES)]
        by_group = [
            numerators[h][:, : PB * OH].rearrange("x (b g t) -> x b g t", b=PB, t=TAPS) for h in range(HALVES)
        ]
        tile_starts = list(range(0, O, N_TILE))

        def whole_groups(i):
            lo = tile_starts[i] // TAPS
            hi = min(tile_starts[i] + N_TILE, O) // TAPS
            parts = [(h, max(lo, GH * h) - GH * h, min(hi, GH * (h + 1)) - GH * h) for h in range(HALVES)]
            return [(h, first, last) for h, first, last in parts if first < last]

        w2_tiles = {}

        def load_tile(i):
            w2_tiles[i] = ring.tile([P, KG, PACK * N_TILE], U8, name="wt", align_bytes=64)
            load_weight_tile(nc, w2_tiles[i], w_span_words, tile_starts[i], min(N_TILE, O - tile_starts[i]))

        def kern_block(i, pb):
            col0 = tile_starts[i]
            ncols = min(N_TILE, O - col0)
            if pb == 0 and i + 3 < n_tiles:
                load_tile(i + 3)
            acc = stream.tile([P, N_TILE], F32, name="acc", tag="bank")
            mx_product(nc, acc[:, :ncols], red_codes, red_planes, pb, w2_tiles[i], w2_planes, col0, ncols)
            for h in range(HALVES):
                first = max(col0, OH * h)
                last = min(col0 + ncols, OH * (h + 1))
                if first < last:
                    base = OH * (pb - h)
                    nc.vector.tensor_tensor(
                        out=numerators[h][:, base + first : base + last],
                        in0=acc[:, first - col0 : last - col0],
                        in1=b2_bc[:, first:last],
                        op=ALU.add,
                    )

        def max_tile(i, pb):
            for h, first, last in whole_groups(i):
                cols = slice(GH * pb + first, GH * pb + last)
                nc.vector.tensor_reduce(
                    out=z_neg[h][:, cols], in_=by_group[h][:, pb, first:last, :], axis=AXIS.X, op=ALU.max, negate=True
                )

        def exp_tile(i, pb):
            for h, first, last in whole_groups(i):
                for g in range(first, last):
                    ready = by_group[h][:, pb, g, :]
                    col = GH * pb + g
                    nc.scalar.activation(
                        out=ready, in_=ready, func=ACT.Exp, bias=z_neg[h][:, col : col + 1], accum_out=e_sum[h][:, col : col + 1]
                    )

        weights_of = {}
        banded_of = {}
        sums_of = {}
        crossed_of = {}
        turned_of = {}

        def invert_sums(h):
            nc.vector.reciprocal(out=e_rcp[h][:], in_=e_sum[h][:])

        def turn_reciprocals(h):
            rcp_turned = turned_pool.tile([P, 4, P], F32, name="rcp_turned", tag="turned")
            nc.tensor.transpose(rcp_turned[:, 0, :], e_rcp[h][:], ident_f32[:])
            nc.vector.tensor_copy(out=rcp_g[h][:], in_=rcp_turned[:, 0, :])
            weights_of[h] = slabs.tile([P, SLAB], F32, name="weights%d" % h, tag="slab", align_bytes=64)

        def turn_weights(h, tap0):
            nt = min(4, TAPS - tap0)
            e_turned = stream.tile([P, 4, P], F32, name="e_turned", tag="bank")
            for tap in range(tap0, tap0 + nt):
                nc.tensor.transpose(
                    e_turned[:, tap - tap0, :],
                    numerators[h][:, : PB * OH].rearrange("x (m t) -> x m t", t=TAPS)[:, :, tap],
                    ident_edge[:, tap % KER, :],
                )
            nc.vector.tensor_tensor(
                out=weights_of[h][:, : P * TAP_PITCH].rearrange("g (n t) -> g n t", t=TAP_PITCH)[:, :, tap0 : tap0 + nt],
                in0=e_turned[:, :nt, :].rearrange("g t n -> g n t"),
                in1=rcp_g[h][:].unsqueeze(2).to_broadcast([P, P, nt]),
                op=ALU.mult,
            )

        def spread(r, h2):
            h, a4 = divmod(r, PAIRS_PB)
            n0 = PAIR * a4 + W * h2
            p_view = (
                weights_of[h][:, : P * TAP_PITCH]
                .rearrange("g (n t) -> g n t", t=TAP_PITCH)[:, n0 : n0 + W, :TAPS]
                .rearrange("g n (i j) -> g n i j", j=KER)
            )
            places = (
                bands[(2 * r + h2) % BANDS][:]
                .bitcast(BF16)[:, 2 * BAND_START : 2 * (BAND_START + W * BAND_PITCH)]
                .rearrange("g (n l) -> g n l", n=W)[:, :, : 2 * KER * W]
                .rearrange("g n (i w s) -> g n i w s", w=W, s=2)
            )
            hi = places[:, :, :, :KER, 1]
            if h2 == 0:
                nc.vector.tensor_copy(out=hi, in_=p_view)
            else:
                nc.gpsimd.tensor_scalar(out=hi, in0=p_view, scalar1=1.0, scalar2=0.0, op0=ALU.mult, op1=ALU.add)
            nc.gpsimd.tensor_tensor(out=places[:, :, :, :KER, 0], in0=p_view, in1=hi, op=ALU.subtract)

        def turn_bank(r, u):
            if u == 0:
                banded_of[r] = turn.tile([P, P, PAIR], F32, name="banded")
            w_turned = stream.tile([P, 4, P], F32, name="w_turned", tag="bank")
            for v in range(4):
                n = 4 * u + v
                h2, w = divmod(n, W)
                first = BAND_START + BAND_PITCH * w - (n - PAD)
                nc.tensor.transpose(w_turned[:, v, :], bands[(2 * r + h2) % BANDS][:, first : first + P], perm[:])
            nc.scalar.copy(out=banded_of[r][:, :, 4 * u : 4 * u + 4], in_=w_turned[:].rearrange("k v m -> k m v"))

        def multiply_bank(r, k):
            h, a4 = divmod(r, PAIRS_PB)
            pb, qb = divmod(k, 2)
            a = PAIRS_PB * pb + a4
            if k == 0:
                sums_of[r] = turn.tile([P, PB, QS, CG], F32, name="sums")
            crossed = crossed_pool.tile([P, 16, FQ * CG], F32, name="crossed")
            crossed_of[r, k] = crossed
            pairs = banded_of[r][:].rearrange("k m n -> k (m n)").bitcast(BF16)
            for q16 in range(16):
                q = 16 * qb + q16
                first = (QS * pb + q) * FQ * PAIR * 2
                nc.tensor.matmul(
                    out=crossed[:, q16, :],
                    lhsT=pairs[:, first : first + P],
                    rhs=x8[:, a, h, q].rearrange("k f c -> k (f c)"),
                    start=True,
                    stop=True,
                )
            nc.vector.tensor_copy(out=sums_of[r][:, pb, 16 * qb : 16 * qb + 16, :], in_=crossed[:, :, CG:])

        def settle_bank(r, k):
            pb, qb = divmod(k, 2)
            nc.scalar.copy(
                out=sums_of[r][: P // FQ, pb, 16 * qb : 16 * qb + 16, :], in_=crossed_of[r, k][: P // FQ, :, :CG]
            )

        def turn_sums(r, pb):
            turned_of[r, pb] = turned_pool.tile([P, 4, P], F32, name="out_turned", tag="turned")
            for t in range(4):
                nc.tensor.transpose(
                    turned_of[r, pb][:, t, :],
                    sums_of[r][:, pb, 8 * t : 8 * t + 8, :].rearrange("k q c -> k (q c)"),
                    ident_f32[:],
                )

        def store_sums(r, pb):
            h, a4 = divmod(r, PAIRS_PB)
            result = results.tile([P, CHB, PAIR], F32, name="result")
            nc.vector.tensor_reduce(
                out=result[:].rearrange("m k n -> m (k n)"),
                in_=turned_of[r, pb][:].rearrange("m t (u s) -> m (t u) s", s=2),
                axis=AXIS.X,
                op=ALU.add,
            )
            pix0 = P * pb + PAIR * a4
            nc.sync.dma_start(
                out=out[0].rearrange("(h k m) y x -> h m k (y x)", h=HALVES, m=P)[h][:, :, pix0 : pix0 + PAIR],
                in_=result[:],
            )

        def spread_step(r):
            pieces = []
            for k in range(8):
                if r < ROUNDS and k in (0, 4):
                    pieces.append(lambda k=k: spread(r, k // 4))
                if 0 <= r - 1 < ROUNDS:
                    pieces.append(lambda k=k: turn_bank(r - 1, k))
                if k % 2 == 1 and 0 <= r - 2 < ROUNDS:
                    pieces.append(lambda k=k: multiply_bank(r - 2, k // 2))
                if k % 2 == 1 and k > 1 and 0 <= r - 2 < ROUNDS:
                    pieces.append(lambda k=k: settle_bank(r - 2, k // 2 - 1))
                if k == 1 and 0 <= r - 3 < ROUNDS:
                    pieces.append(lambda: settle_bank(r - 3, 3))
                if k % 4 == 0 and 0 <= r - 3 < ROUNDS:
                    pieces.append(lambda k=k: turn_sums(r - 3, k // 4))
                if k % 4 == 2 and 0 <= r - 3 < ROUNDS:
                    pieces.append(lambda k=k: store_sums(r - 3, k // 4))
            return pieces

        def weights_pieces(h):
            return [lambda: turn_reciprocals(h)] + [lambda tap0=tap0: turn_weights(h, tap0) for tap0 in range(0, TAPS, 4)]

        def tile_piece(p):
            if p < PB * n_tiles:
                kern_block(*divmod(p, PB))
            if 0 <= p - 1 < PB * n_tiles:
                max_tile(*divmod(p - 1, PB))
            if 0 <= p - 2 < PB * n_tiles:
                exp_tile(*divmod(p - 2, PB))

        def run(pieces):
            for piece in pieces:
                piece()

        first_tiles = -(-OH // N_TILE)
        n_tiles = len(tile_starts)
        tiles = [lambda p=p: tile_piece(p) for p in range(PB * (first_tiles + 2), PB * n_tiles + 2)]
        half_0 = [piece for r in range(1, PAIRS_PB - 1) for piece in spread_step(r)]
        between = spread_step(PAIRS_PB - 1)
        half_1 = [piece for r in range(PAIRS_PB, ROUNDS + 3) for piece in spread_step(r)]

        with tc.tile_pool(name="x_pool", bufs=1) as x_pool:
            x_ch = x_pool.tile([P, C // P, PIX], BF16)
            x_pix = [x_pool.tile([P, HALVES, QS, FQ, CG], BF16, name="x_pix%d" % pb) for pb in range(PB)]

            def turn_x(pb, h):
                x_turned = stream.tile([P, CHB, P], BF16, name="x_turned", tag="bank")
                for u in range(CHB):
                    nc.tensor.transpose(x_turned[:, u, :], x_ch[:, CHB * h + u, P * pb : P * (pb + 1)], ident_bf[:])
                for f in range(FQ):
                    nc.scalar.copy(
                        out=x_pix[pb][:, h, :, f, :].rearrange("k (t r) c -> k t r c", r=QB),
                        in_=x_turned[:].rearrange("k (t f) (r c) -> k t f r c", f=FQ, c=CG)[:, :, f],
                    )

            def place_window(a):
                low = PAIR * a - PAD * W
                for pb in range(PB):
                    first = max(low, P * pb)
                    last = min(low + P, P * (pb + 1))
                    if first < last:
                        nc.sync.dma_start(
                            out=x8[first - low : last - low, a].rearrange("k h q f c -> k (h q f c)"),
                            in_=x_pix[pb][first - P * pb : last - P * pb].rearrange("k h q f c -> k (h q f c)"),
                        )

            turns = [(pb, h) for pb in range(PB) for h in range(HALVES)]
            for i in range(3):
                load_tile(i)
            for p in range(PB * (first_tiles + 2)):
                tile_piece(p)
                if p == PB:
                    nc.sync.dma_start(out=x_ch[:], in_=x[0].rearrange("(b c) h w -> c b (h w)", c=P))
                if p == 2 * PB:
                    nc.sync.dma_start(out=b2_bc[:, OH:], in_=b_span[OH:].partition_broadcast(P))
                if p == PB * (first_tiles + 1):
                    invert_sums(0)
                if p >= 5 * PB and turns:
                    turn_x(*turns.pop(0))
            run(weave(weights_pieces(0), tiles[:PB]))
            for a4 in range(PAIRS_PB):
                for pb in range(PB):
                    place_window(a4 + PAIRS_PB * pb)

        turn = whole.enter_context(tc.tile_pool(name="turn", bufs=2))
        results = whole.enter_context(tc.tile_pool(name="results", bufs=4))
        run(spread_step(0))
        run(tiles[PB : 2 * PB])
        run(weave(tiles[2 * PB :], half_0))
        run(between[:8])
        invert_sums(1)
        run(between[8:10])
        run(weave(between[10:], weights_pieces(1)))
        run(half_1)
